import numpy as np
import ml_dtypes


def mxq(x, axis, fmt="e4m3"):
    dtype, down = {"e4m3": (ml_dtypes.float8_e4m3fn, 7), "e5m2": (ml_dtypes.float8_e5m2, 14)}[fmt]
    v = np.moveaxis(np.asarray(x, np.float32).astype(ml_dtypes.bfloat16).astype(np.float64), axis, -1)
    blocks = v.reshape(v.shape[:-1] + (-1, 32))
    amax = np.abs(blocks).max(-1, keepdims=True)
    byte = np.maximum(np.where(amax > 0, np.frexp(amax)[1] - 1 + 127, 0) - down, 1)
    scale = np.exp2(byte - 127.0)
    codes = (blocks / scale).astype(np.float32).astype(dtype).astype(np.float64)
    return np.moveaxis((codes * scale).reshape(v.shape), -1, axis)


WIDE = False


def mx_kscale(k):
    if not WIDE:
        return np.ones(k)
    levels = np.array([10, -10, 5, -5, 0])
    a = np.random.permutation(np.resize(levels, k // 512 * 4)).reshape(k // 512, 4)
    idx = np.arange(k)
    return np.exp2(a[idx // 512, idx % 128 // 32])


BF16 = ml_dtypes.bfloat16


def bf(x):
    return np.asarray(x, np.float32).astype(BF16)


def f64(x):
    return np.asarray(x).astype(np.float64)


B, C, W, H, K, S, NEW = 2, 62, 64, 64, 4, 2, 2
KK = K * K
IN = 2 * K * C + KK
OUT = C * NEW * NEW * KK
BN_EPS = 1e-5


def unfold(x, oh, ow):
    p = (K - 1) // 2
    xp = np.pad(x, ((0, 0), (0, 0), (p, p), (p, p)))
    rows = []
    for i in range(K):
        cols = []
        for j in range(K):
            cols.append(xp[:, :, i:i + S * (oh - 1) + 1:S, j:j + S * (ow - 1) + 1:S])
        rows.append(np.stack(cols, axis=2))
    return np.stack(rows, axis=2)


def setup_inputs():
    s = mx_kscale(IN)
    sc = s[KK:KK + C * K:K]
    col = np.concatenate([np.full(KK, sc.max()), np.repeat(sc, K), np.repeat(sc, K)])
    so = np.repeat(sc, KK * NEW * NEW)
    return {"x": bf(np.random.standard_normal((B, C, W, H)) * sc[None, :, None, None]),
            "conv_w": bf(np.random.standard_normal((OUT, IN)) * 0.16 / np.sqrt(IN) / col),
            "bn_gamma": bf((0.2 + 0.02 * np.random.standard_normal(OUT)) / so),
            "bn_beta": bf(0.4 * np.random.standard_normal(OUT) / so),
            "bn_mean": bf(0.1 * np.random.standard_normal(OUT)),
            "bn_var": bf(BN_EPS * (15.0 + 25.0 * np.random.random(OUT)))}


def reference(x, conv_w, bn_gamma, bn_beta, bn_mean, bn_var):
    x = f64(x)
    oh = -(-W // S)
    ow = -(-H // S)
    patches = unfold(x, oh, ow)
    x1 = patches.max(axis=1).reshape(B, KK, oh, ow)
    x2 = patches.max(axis=2).reshape(B, C * K, oh, ow)
    x3 = patches.max(axis=3).reshape(B, C * K, oh, ow)
    feat = np.concatenate([x1, x2, x3], axis=1).reshape(B, IN, oh * ow)
    y = (mxq(f64(conv_w), 1, "e4m3") @ mxq(feat, 1, "e4m3")).reshape(B, OUT, oh, ow)
    inv = (f64(bn_gamma) / np.sqrt(f64(bn_var) + BN_EPS))[None, :, None, None]
    y = (y - f64(bn_mean)[None, :, None, None]) * inv + f64(bn_beta)[None, :, None, None]
    y = np.maximum(y, 0.0)
    w = y.reshape(B, C, KK, NEW, NEW, oh, ow)
    px = patches.reshape(B, C, KK, 1, 1, oh, ow)
    out = np.mean(px * w, axis=2)
    out = out.transpose(0, 1, 4, 2, 5, 3)
    out = out.reshape(B, C, oh * NEW, ow * NEW)
    return out[:, :, :W, :H]

@@ -1,0 +1,318 @@
+from contextlib import ExitStack
+
+import concourse.bass as bass
+import concourse.mybir as mybir
+import concourse.tile as tile
+from concourse.masks import make_identity
+
+F32 = mybir.dt.float32
+BF16 = mybir.dt.bfloat16
+U32 = mybir.dt.uint32
+U8 = mybir.dt.uint8
+FP8X4 = mybir.dt.float8_e4m3fn_x4
+ACT = mybir.ActivationFunctionType
+ALU = mybir.AluOpType
+
+P = 128
+C = 62
+FLOPS = 2 * 3968 * 512 * 2048
+BN_EPS = 1e-5
+
+REGIONS = [(4, 0, 32, 0), (36, 32, 30, 0), (66, 0, 32, 1), (98, 32, 30, 1)]
+
+
+def tile_revolutionnaive_kernel(tc, x, conv_w, bn_gamma, bn_beta, bn_mean, bn_var, out):
+    nc = tc.nc
+    with ExitStack() as ctx:
+        keep = ctx.enter_context(tc.tile_pool(name="keep", bufs=1))
+        wgp = ctx.enter_context(tc.tile_pool(name="wgp", bufs=2))
+        zp = ctx.enter_context(tc.tile_pool(name="zp", bufs=4))
+        atp = ctx.enter_context(tc.tile_pool(name="atp", bufs=4))
+        op = ctx.enter_context(tc.tile_pool(name="op", bufs=2))
+        accp = ctx.enter_context(tc.psum_pool(name="accp", bufs=1))
+        yp = ctx.enter_context(tc.psum_pool(name="yp", bufs=4))
+        mp = ctx.enter_context(tc.psum_pool(name="mp", bufs=2))
+
+        X = keep.tile([P, 2, 68, 64], BF16, name="X")
+        XS = keep.tile([P, C * 64], BF16, name="XS")
+        Wsb = keep.tile([P, 16, 1024], BF16, name="Wsb")
+        E = keep.tile([P, 2, 33, 66], BF16, name="E")
+        FT = keep.tile([P, 2, 33, 66], BF16, name="FT")
+        M4 = keep.tile([P, 2, 32, 66], BF16, name="M4")
+        G = keep.tile([P, 4, 2048], BF16, name="G", align_bytes=64)
+        FC = keep.tile([P, 2048], U32, name="FC", align_bytes=64)
+        FS = keep.tile([P, 2048], U8, name="FS", align_bytes=64)
+        WC = keep.tile([P, 4096], U32, name="WC", align_bytes=64)
+        WS = keep.tile([P, 4096], U8, name="WS", align_bytes=64)
+        tbuf = [keep.tile([P, 2, 512], F32, name="t%d" % j) for j in range(4)]
+        identF = keep.tile([P, P], F32, name="identF")
+        identB = keep.tile([P, P], BF16, name="identB")
+        band = keep.tile([P, 192], BF16, name="band")
+        MR = keep.tile([P, 2, 66], BF16, name="MR")
+        raw = [keep.tile([P, 64], BF16, name="raw%d" % q) for q in range(4)]
+        Stab = keep.tile([P, 16, 2], F32, name="Stab")
+        Btab = keep.tile([P, 16, 2], F32, name="Btab")
+
+        for q in range(4):
+            nc.vector.memset(raw[q][:], 0.0)
+        nc.vector.memset(X[:, :, 0:66:65, :], 0.0)
+        for b in range(2):
+            nc.scalar.dma_start(out=XS[64 * b:64 * b + 64, :].rearrange("r (c s) -> r c s", s=64),
+                                in_=x[b].rearrange("c r s -> r c s"))
+
+        def load_x(b):
+            for (p0, c0, cn, n) in REGIONS + [(0, 0, 4, 0)]:
+                nc.sync.dma_start(out=X[p0:p0 + cn, b, 1:65, :], in_=x[b, c0:c0 + cn])
+
+        w5 = conv_w.rearrange("(c k n m) f -> c k n (m f)", c=C, k=16, n=2, m=2)
+
+        def load_w(k0, k1):
+            for (p0, c0, cn, n) in REGIONS:
+                nc.sync.dma_start(out=Wsb[p0:p0 + cn, k0:k1, :], in_=w5[c0:c0 + cn, k0:k1, n, :])
+
+        load_x(0)
+        nc.sync.dma_start(out=Wsb[0:4, :, :].rearrange("p k f -> p (k f)"),
+                          in_=conv_w[0:128, :].rearrange("(p a) f -> p (a f)", p=4))
+        load_w(0, 4)
+        for q, vec in enumerate((bn_gamma, bn_beta, bn_mean, bn_var)):
+            v2 = vec.rearrange("(c q) -> c q", q=64)
+            nc.scalar.dma_start(out=raw[q][4:66, :], in_=v2)
+            nc.scalar.dma_start(out=raw[q][66:128, :], in_=v2)
+        load_w(4, 8)
+        load_x(1)
+        load_w(8, 12)
+        load_w(12, 16)
+
+        make_identity(nc, identF[:])
+        make_identity(nc, identB[:])
+        nc.vector.memset(band[:], 0.0)
+        nc.vector.tensor_tensor(out=band[:, 1:65], in0=identB[:, 0:64], in1=identB[:, 64:128], op=ALU.add)
+        nc.vector.memset(MR[:], 0.0)
+        nc.vector.memset(E[:, :, :, 0:66:65], 0.0)
+
+        vv = keep.tile([P, 64], F32, name="vv")
+        sfull = keep.tile([P, 64], F32, name="sfull")
+        bfull = keep.tile([P, 64], F32, name="bfull")
+        nc.vector.tensor_scalar_add(out=vv[:], in0=raw[3][:], scalar1=BN_EPS)
+        nc.scalar.sqrt(out=vv[:], in_=vv[:])
+        nc.vector.reciprocal(out=vv[:], in_=vv[:])
+        nc.vector.tensor_mul(out=sfull[:], in0=raw[0][:], in1=vv[:])
+        nc.vector.tensor_mul(out=bfull[:], in0=raw[2][:], in1=sfull[:])
+        nc.vector.tensor_sub(out=bfull[:], in0=raw[1][:], in1=bfull[:])
+        for tab, full in ((Stab, sfull), (Btab, bfull)):
+            fv = full[:].rearrange("p (k n m) -> p k n m", k=16, n=2, m=2)
+            nc.vector.tensor_copy(out=tab[64:128], in_=fv[64:128, :, 1, :])
+            nc.vector.tensor_copy(out=tab[0:66], in_=fv[0:66, :, 0, :])
+
+        def feat_e(b):
+            xr = X[0:66, b, 0:66, :].rearrange("p (u r2) s -> p u r2 s", r2=2)
+            nc.vector.tensor_max(out=E[0:66, b, :, 1:65], in0=xr[:, :, 0, :], in1=xr[:, :, 1, :])
+
+        def feat_ft(b):
+            nc.vector.tensor_max(out=FT[64:128, b, 1:32, :],
+                                 in0=X[64:128, b, 0:66, 1:62:2].rearrange("p r v -> p v r"),
+                                 in1=X[64:128, b, 0:66, 2:63:2].rearrange("p r v -> p v r"))
+            nc.vector.tensor_scalar_max(out=FT[64:128, b, 0:33:32, :],
+                                        in0=X[64:128, b, 0:66, 0:64:63].rearrange("p r v -> p v r"),
+                                        scalar1=0.0)
+
+        def feat_g3(nt, up):
+            b, vp = divmod(nt, 2)
+            nc.vector.tensor_max(
+                out=G[64:128, nt, up * 1024:(up + 1) * 1024].rearrange("p (a w i) -> p a w i", a=16, w=16, i=4),
+                in0=FT[64:128, b, vp:vp + 31:2, 2 * up:2 * up + 64].rearrange("p w (a i) -> p a w i", i=4),
+                in1=FT[64:128, b, vp + 1:vp + 32:2, 2 * up:2 * up + 64].rearrange("p w (a i) -> p a w i", i=4))
+
+        def feat_g2(nt):
+            b, vp = divmod(nt, 2)
+            nc.vector.tensor_max(
+                out=G[0:66, nt, :].rearrange("p (up a x) -> p up a x", up=2, a=16, x=64),
+                in0=E[0:66, b, 0:32, 2 * vp:2 * vp + 64].rearrange("p (a up) x -> p up a x", up=2),
+                in1=E[0:66, b, 1:33, 2 * vp:2 * vp + 64].rearrange("p (a up) x -> p up a x", up=2))
+
+        def feat_x1(nt):
+            b, vp = divmod(nt, 2)
+            nc.vector.tensor_copy(
+                out=G[0:4, nt, :].rearrange("p (up a x) -> p up a x", up=2, a=16, x=64),
+                in_=M4[0:4, b, :, 2 * vp:2 * vp + 64].rearrange("p (a up) x -> p up a x", up=2))
+
+        def feat_q(nt):
+            nc.vector.quantize_mx(out=FC[:, nt * 512:(nt + 1) * 512].bitcast(FP8X4),
+                                  scales=FS[:, nt * 512:(nt + 1) * 512], in_=G[:, nt, :])
+
+        def chan_max():
+            ta = keep.tile([P, 1984], BF16, name="ta")
+            tb = keep.tile([P, 1024], BF16, name="tb")
+            nc.vector.tensor_max(out=ta[:], in0=XS[:, 0:1984], in1=XS[:, 1984:3968])
+            nc.vector.tensor_max(out=tb[:], in0=ta[:, 0:1024], in1=ta[:, 960:1984])
+            nc.vector.tensor_max(out=ta[:, 0:512], in0=tb[:, 0:512], in1=tb[:, 512:1024])
+            nc.vector.tensor_max(out=tb[:, 0:256], in0=ta[:, 0:256], in1=ta[:, 256:512])
+            nc.vector.tensor_max(out=ta[:, 0:128], in0=tb[:, 0:128], in1=tb[:, 128:256])
+            nc.vector.tensor_max(out=MR[0:64, 0, 1:65], in0=ta[0:64, 0:64], in1=ta[0:64, 64:128])
+            nc.vector.tensor_max(out=MR[64:128, 1, 1:65], in0=ta[64:128, 0:64], in1=ta[64:128, 64:128])
+
+        def select_rows(b):
+            for u0 in range(0, 32, 7):
+                un = min(7, 32 - u0)
+                ps = mp.tile([P, 512], F32, name="ps", tag="misc")
+                for ul in range(un):
+                    u = u0 + ul
+                    nc.tensor.matmul(out=ps[:, ul * 66:(ul + 1) * 66], lhsT=band[:, 2 * u:2 * u + 128],
+                                     rhs=MR[:, b, :], start=True, stop=True)
+                nc.scalar.copy(out=M4[0:4, b, u0:u0 + un, :],
+                               in_=ps[0:4, 0:un * 66].rearrange("p (u s) -> p u s", s=66))
+
+        def wprep(r):
+            wg = wgp.tile([P, 2048], BF16, name="wg", align_bytes=64)
+            for kl in range(2):
+                k = 2 * r + kl
+                wt = mp.tile([P, 512], F32, name="wt", tag="misc")
+                for m in range(2):
+                    words = Wsb[:, k, m * 512:(m + 1) * 512].bitcast(F32)
+                    for e in range(2):
+                        q = 2 * m + e
+                        nc.tensor.transpose(out=wt[:, q * 128:(q + 1) * 128], in_=words[:, e:256:2],
+                                            identity=identF[:])
+                nc.scalar.copy(
+                    out=wg[:, kl * 1024:(kl + 1) * 1024].bitcast(F32).rearrange("p (m o e) -> p m o e", m=2, o=128, e=2),
+                    in_=wt[:].rearrange("p (m e o) -> p m o e", m=2, e=2, o=128))
+            nc.vector.quantize_mx(out=WC[:, r * 512:(r + 1) * 512].bitcast(FP8X4),
+                                  scales=WS[:, r * 512:(r + 1) * 512], in_=wg[:])
+
+        ys = {}
+        zs = {}
+        accs = {}
+        ats = {}
+
+        def mx(g):
+            nt, kp = divmod(g, 8)
+            for kl in range(2):
+                for m in range(2):
+                    tl = (2 * kp + kl) * 2 + m
+                    y = yp.tile([P, 512], F32, name="y")
+                    nc.tensor.matmul_mx(out=y[:],
+                                        lhsT=WC[:, tl * 128:(tl + 1) * 128].bitcast(FP8X4),
+                                        lhsT_scale=WS[:, tl * 128:(tl + 1) * 128],
+                                        rhs=FC[:, nt * 512:(nt + 1) * 512].bitcast(FP8X4),
+                                        rhs_scale=FS[:, nt * 512:(nt + 1) * 512],
+                                        start=True, stop=True)
+                    ys[(g, kl, m)] = y
+
+        def act(g):
+            nt, kp = divmod(g, 8)
+            for kl in range(2):
+                k = 2 * kp + kl
+                z = zp.tile([P, 2, 512], F32, name="z")
+                zs[(g, kl)] = z
+                for m in range(2):
+                    nc.scalar.activation(out=z[:, m, :], in_=ys[(g, kl, m)][:], func=ACT.Relu,
+                                         bias=Btab[:, k, m:m + 1], scale=Stab[:, k, m:m + 1])
+
+        def mul(g):
+            nt, kp = divmod(g, 8)
+            b, vp = divmod(nt, 2)
+            for kl in range(2):
+                k = 2 * kp + kl
+                i, j = divmod(k, 4)
+                w0 = 1 if (j == 0 and vp == 0) else 0
+                w1 = 15 if (j == 3 and vp == 1) else 16
+                s0 = 2 * vp + j - 1 + 4 * w0
+                s1 = 2 * vp + j - 1 + 4 * (w1 - 1) + 1
+                xv = X[:, b, i:i + 64, :].rearrange("p (a up r2) s -> p up a r2 s", a=16, up=2, r2=2)[:, :, :, 0, s0:s1:4]
+                z = zs[(g, kl)]
+                for m in range(2):
+                    nc.vector.tensor_mul(
+                        out=tbuf[j][:, m, :].rearrange("p (up a w) -> p up a w", up=2, a=16, w=16)[:, :, :, w0:w1],
+                        in0=z[:, m, :].rearrange("p (up a w) -> p up a w", up=2, a=16, w=16)[:, :, :, w0:w1],
+                        in1=xv)
+
+        def tr(g):
+            nt, kp = divmod(g, 8)
+            if kp == 0:
+                for m in range(2):
+                    accs[(nt, m)] = accp.tile([P, 512], F32, name="acc%d" % m)
+            for kl in range(2):
+                k = 2 * kp + kl
+                j = k % 4
+                for m in range(2):
+                    for blk in range(4):
+                        nc.tensor.matmul(out=accs[(nt, m)][:, blk * 128:(blk + 1) * 128],
+                                         lhsT=tbuf[j][:, m, blk * 128:(blk + 1) * 128],
+                                         rhs=identF[:], is_transpose=True,
+                                         start=(k == 0 and blk == 0), stop=(k == 15 and blk == 3))
+
+        def border(nt):
+            vp = nt % 2
+            j, w = (0, 0) if vp == 0 else (3, 15)
+            nc.vector.memset(tbuf[j][:].rearrange("p m (q w) -> p m q w", w=16)[:, :, :, w:w + 1], 0.0)
+
+        def evac(nt):
+            for m in range(2):
+                at = atp.tile([P, 512], F32, name="at")
+                nc.scalar.mul(out=at[:], in_=accs[(nt, m)][:], mul=1.0 / 16.0)
+                ats[(nt, m)] = at
+
+        def fin(b):
+            o = op.tile([P, 2048], F32, name="o")
+            ov = o[:].rearrange("p (ah al up x) -> p ah up al x", ah=2, al=8, up=2, x=64)
+            for blk in range(4):
+                up, ah = divmod(blk, 2)
+                fb = mp.tile([P, 512], F32, name="fb", tag="misc")
+                for vp in range(2):
+                    for m in range(2):
+                        q = 2 * vp + m
+                        nc.tensor.transpose(out=fb[:, q * 128:(q + 1) * 128],
+                                            in_=ats[(2 * b + vp, m)][:, blk * 128:(blk + 1) * 128],
+                                            identity=identF[:])
+                dst = ov[:, ah, up].rearrange("p al (w q) -> p al w q", q=4)
+                src = fb[:].rearrange("p (q al w) -> p al w q", q=4, al=8, w=16)
+                if blk % 2 == 0:
+                    nc.vector.tensor_copy(out=dst, in_=src)
+                else:
+                    nc.scalar.copy(out=dst, in_=src)
+            for (p0, c0, cn, n) in REGIONS:
+                nc.sync.dma_start(
+                    out=out[b, c0:c0 + cn].rearrange("c (u n) x -> c u n x", n=2)[:, :, n, :],
+                    in_=o[p0:p0 + cn, :].rearrange("p (u x) -> p u x", x=64))
+
+        feat_e(0)
+        feat_ft(0)
+        feat_g3(0, 0)
+        feat_g3(0, 1)
+        feat_g2(0)
+        chan_max()
+        select_rows(0)
+        feat_x1(0)
+        feat_q(0)
+        wprep(0)
+        wprep(1)
+        select_rows(1)
+
+        extra = {
+            1: [lambda: feat_g3(1, 0)], 2: [lambda: feat_g3(1, 1)],
+            3: [lambda: feat_g2(1), lambda: feat_x1(1)], 4: [lambda: feat_q(1)],
+            5: [lambda: feat_e(1)], 6: [lambda: feat_ft(1)],
+            8: [lambda: feat_g3(2, 0)], 9: [lambda: feat_g3(2, 1)],
+            10: [lambda: feat_g2(2), lambda: feat_x1(2)], 11: [lambda: feat_q(2)],
+            16: [lambda: feat_g3(3, 0)], 17: [lambda: feat_g3(3, 1)],
+            18: [lambda: feat_g2(3), lambda: feat_x1(3)], 19: [lambda: feat_q(3)],
+        }
+        for g in range(32):
+            mx(g)
+            act(g)
+            if g >= 1:
+                tr(g - 1)
+                if g % 8 == 0:
+                    evac(g // 8 - 1)
+                    if g == 16:
+                        fin(0)
+            if g + 2 < 8:
+                wprep(g + 2)
+            if g % 8 == 0:
+                border(g // 8)
+            mul(g)
+            for fn in extra.get(g, []):
+                fn()
+        tr(31)
+        evac(3)
+        fin(1)

@@ -17,6 +17,8 @@ P = 128
 C = 62
 FLOPS = 2 * 3968 * 512 * 2048
 BN_EPS = 1e-5
+PG = 1
+NS = 64
 
 REGIONS = [(4, 0, 32, 0), (36, 32, 30, 0), (66, 0, 32, 1), (98, 32, 30, 1)]
 
@@ -25,13 +27,13 @@ def tile_revolutionnaive_kernel(tc, x, conv_w, bn_gamma, bn_beta, bn_mean, bn_va
     nc = tc.nc
     with ExitStack() as ctx:
         keep = ctx.enter_context(tc.tile_pool(name="keep", bufs=1))
-        wgp = ctx.enter_context(tc.tile_pool(name="wgp", bufs=2))
-        zp = ctx.enter_context(tc.tile_pool(name="zp", bufs=4))
+        wgp = ctx.enter_context(tc.tile_pool(name="wgp", bufs=3))
+        zp = ctx.enter_context(tc.tile_pool(name="zp", bufs=3))
         atp = ctx.enter_context(tc.tile_pool(name="atp", bufs=4))
         op = ctx.enter_context(tc.tile_pool(name="op", bufs=2))
-        accp = ctx.enter_context(tc.psum_pool(name="accp", bufs=1))
         yp = ctx.enter_context(tc.psum_pool(name="yp", bufs=4))
-        mp = ctx.enter_context(tc.psum_pool(name="mp", bufs=2))
+        mp = ctx.enter_context(tc.psum_pool(name="mp", bufs=4))
+        ctx.enter_context(tc.manual_schedule())
 
         X = keep.tile([P, 2, 68, 64], BF16, name="X")
         XS = keep.tile([P, C * 64], BF16, name="XS")
@@ -53,12 +55,24 @@ def tile_revolutionnaive_kernel(tc, x, conv_w, bn_gamma, bn_beta, bn_mean, bn_va
         Stab = keep.tile([P, 16, 2], F32, name="Stab")
         Btab = keep.tile([P, 16, 2], F32, name="Btab")
 
+        ta = keep.tile([P, 1984], BF16, name="ta")
+        tb = keep.tile([P, 1024], BF16, name="tb")
+        vv = keep.tile([P, 64], F32, name="vv")
+        sfull = keep.tile([P, 64], F32, name="sfull")
+        bfull = keep.tile([P, 64], F32, name="bfull")
+
+        for b in range(2):
+            nc.gpsimd.dma_start(out=XS[64 * b:64 * b + 64, :].rearrange("r (c s) -> r c s", s=64),
+                                in_=x[b].rearrange("c r s -> r c s"))
+        make_identity(nc, identF[:])
+        make_identity(nc, identB[:])
         for q in range(4):
             nc.vector.memset(raw[q][:], 0.0)
+        for q, vec in enumerate((bn_var, bn_gamma, bn_mean, bn_beta)):
+            v2 = vec.rearrange("(c q) -> c q", q=64)
+            nc.gpsimd.dma_start(out=raw[q][4:66, :], in_=v2)
+            nc.gpsimd.dma_start(out=raw[q][66:128, :], in_=v2)
         nc.vector.memset(X[:, :, 0:66:65, :], 0.0)
-        for b in range(2):
-            nc.scalar.dma_start(out=XS[64 * b:64 * b + 64, :].rearrange("r (c s) -> r c s", s=64),
-                                in_=x[b].rearrange("c r s -> r c s"))
 
         def load_x(b):
             for (p0, c0, cn, n) in REGIONS + [(0, 0, 4, 0)]:
@@ -74,44 +88,25 @@ def tile_revolutionnaive_kernel(tc, x, conv_w, bn_gamma, bn_beta, bn_mean, bn_va
         nc.sync.dma_start(out=Wsb[0:4, :, :].rearrange("p k f -> p (k f)"),
                           in_=conv_w[0:128, :].rearrange("(p a) f -> p (a f)", p=4))
         load_w(0, 4)
-        for q, vec in enumerate((bn_gamma, bn_beta, bn_mean, bn_var)):
-            v2 = vec.rearrange("(c q) -> c q", q=64)
-            nc.scalar.dma_start(out=raw[q][4:66, :], in_=v2)
-            nc.scalar.dma_start(out=raw[q][66:128, :], in_=v2)
         load_w(4, 8)
-        load_x(1)
         load_w(8, 12)
         load_w(12, 16)
+        load_x(1)
 
-        make_identity(nc, identF[:])
-        make_identity(nc, identB[:])
         nc.vector.memset(band[:], 0.0)
-        nc.vector.tensor_tensor(out=band[:, 1:65], in0=identB[:, 0:64], in1=identB[:, 64:128], op=ALU.add)
         nc.vector.memset(MR[:], 0.0)
         nc.vector.memset(E[:, :, :, 0:66:65], 0.0)
 
-        vv = keep.tile([P, 64], F32, name="vv")
-        sfull = keep.tile([P, 64], F32, name="sfull")
-        bfull = keep.tile([P, 64], F32, name="bfull")
-        nc.vector.tensor_scalar_add(out=vv[:], in0=raw[3][:], scalar1=BN_EPS)
-        nc.scalar.sqrt(out=vv[:], in_=vv[:])
-        nc.vector.reciprocal(out=vv[:], in_=vv[:])
-        nc.vector.tensor_mul(out=sfull[:], in0=raw[0][:], in1=vv[:])
-        nc.vector.tensor_mul(out=bfull[:], in0=raw[2][:], in1=sfull[:])
-        nc.vector.tensor_sub(out=bfull[:], in0=raw[1][:], in1=bfull[:])
-        for tab, full in ((Stab, sfull), (Btab, bfull)):
-            fv = full[:].rearrange("p (k n m) -> p k n m", k=16, n=2, m=2)
-            nc.vector.tensor_copy(out=tab[64:128], in_=fv[64:128, :, 1, :])
-            nc.vector.tensor_copy(out=tab[0:66], in_=fv[0:66, :, 0, :])
+        def feat_e(b, u0, u1):
+            xr = X[0:66, b, 2 * u0:2 * u1, :].rearrange("p (u r2) s -> p u r2 s", r2=2)
+            nc.vector.tensor_max(out=E[0:66, b, u0:u1, 1:65], in0=xr[:, :, 0, :], in1=xr[:, :, 1, :])
 
-        def feat_e(b):
-            xr = X[0:66, b, 0:66, :].rearrange("p (u r2) s -> p u r2 s", r2=2)
-            nc.vector.tensor_max(out=E[0:66, b, :, 1:65], in0=xr[:, :, 0, :], in1=xr[:, :, 1, :])
+        def feat_ft(b, v0, v1):
+            nc.vector.tensor_max(out=FT[64:128, b, v0:v1, :],
+                                 in0=X[64:128, b, 0:66, 2 * v0 - 1:2 * v1 - 2:2].rearrange("p r v -> p v r"),
+                                 in1=X[64:128, b, 0:66, 2 * v0:2 * v1 - 1:2].rearrange("p r v -> p v r"))
 
-        def feat_ft(b):
-            nc.vector.tensor_max(out=FT[64:128, b, 1:32, :],
-                                 in0=X[64:128, b, 0:66, 1:62:2].rearrange("p r v -> p v r"),
-                                 in1=X[64:128, b, 0:66, 2:63:2].rearrange("p r v -> p v r"))
+        def feat_ftb(b):
             nc.vector.tensor_scalar_max(out=FT[64:128, b, 0:33:32, :],
                                         in0=X[64:128, b, 0:66, 0:64:63].rearrange("p r v -> p v r"),
                                         scalar1=0.0)
@@ -123,12 +118,12 @@ def tile_revolutionnaive_kernel(tc, x, conv_w, bn_gamma, bn_beta, bn_mean, bn_va
                 in0=FT[64:128, b, vp:vp + 31:2, 2 * up:2 * up + 64].rearrange("p w (a i) -> p a w i", i=4),
                 in1=FT[64:128, b, vp + 1:vp + 32:2, 2 * up:2 * up + 64].rearrange("p w (a i) -> p a w i", i=4))
 
-        def feat_g2(nt):
+        def feat_g2(nt, up):
             b, vp = divmod(nt, 2)
             nc.vector.tensor_max(
-                out=G[0:66, nt, :].rearrange("p (up a x) -> p up a x", up=2, a=16, x=64),
-                in0=E[0:66, b, 0:32, 2 * vp:2 * vp + 64].rearrange("p (a up) x -> p up a x", up=2),
-                in1=E[0:66, b, 1:33, 2 * vp:2 * vp + 64].rearrange("p (a up) x -> p up a x", up=2))
+                out=G[0:66, nt, up * 1024:(up + 1) * 1024].rearrange("p (a x) -> p a x", a=16, x=64),
+                in0=E[0:66, b, up:up + 31:2, 2 * vp:2 * vp + 64],
+                in1=E[0:66, b, up + 1:up + 32:2, 2 * vp:2 * vp + 64])
 
         def feat_x1(nt):
             b, vp = divmod(nt, 2)
@@ -141,8 +136,6 @@ def tile_revolutionnaive_kernel(tc, x, conv_w, bn_gamma, bn_beta, bn_mean, bn_va
                                   scales=FS[:, nt * 512:(nt + 1) * 512], in_=G[:, nt, :])
 
         def chan_max():
-            ta = keep.tile([P, 1984], BF16, name="ta")
-            tb = keep.tile([P, 1024], BF16, name="tb")
             nc.vector.tensor_max(out=ta[:], in0=XS[:, 0:1984], in1=XS[:, 1984:3968])
             nc.vector.tensor_max(out=tb[:], in0=ta[:, 0:1024], in1=ta[:, 960:1984])
             nc.vector.tensor_max(out=ta[:, 0:512], in0=tb[:, 0:512], in1=tb[:, 512:1024])
@@ -151,100 +144,105 @@ def tile_revolutionnaive_kernel(tc, x, conv_w, bn_gamma, bn_beta, bn_mean, bn_va
             nc.vector.tensor_max(out=MR[0:64, 0, 1:65], in0=ta[0:64, 0:64], in1=ta[0:64, 64:128])
             nc.vector.tensor_max(out=MR[64:128, 1, 1:65], in0=ta[64:128, 0:64], in1=ta[64:128, 64:128])
 
-        def select_rows(b):
-            for u0 in range(0, 32, 7):
-                un = min(7, 32 - u0)
-                ps = mp.tile([P, 512], F32, name="ps", tag="misc")
-                for ul in range(un):
-                    u = u0 + ul
-                    nc.tensor.matmul(out=ps[:, ul * 66:(ul + 1) * 66], lhsT=band[:, 2 * u:2 * u + 128],
-                                     rhs=MR[:, b, :], start=True, stop=True)
-                nc.scalar.copy(out=M4[0:4, b, u0:u0 + un, :],
-                               in_=ps[0:4, 0:un * 66].rearrange("p (u s) -> p u s", s=66))
+        pss = {}
 
-        def wprep(r):
-            wg = wgp.tile([P, 2048], BF16, name="wg", align_bytes=64)
-            for kl in range(2):
-                k = 2 * r + kl
-                wt = mp.tile([P, 512], F32, name="wt", tag="misc")
-                for m in range(2):
-                    words = Wsb[:, k, m * 512:(m + 1) * 512].bitcast(F32)
-                    for e in range(2):
-                        q = 2 * m + e
-                        nc.tensor.transpose(out=wt[:, q * 128:(q + 1) * 128], in_=words[:, e:256:2],
-                                            identity=identF[:])
-                nc.scalar.copy(
-                    out=wg[:, kl * 1024:(kl + 1) * 1024].bitcast(F32).rearrange("p (m o e) -> p m o e", m=2, o=128, e=2),
-                    in_=wt[:].rearrange("p (m e o) -> p m o e", m=2, e=2, o=128))
-            nc.vector.quantize_mx(out=WC[:, r * 512:(r + 1) * 512].bitcast(FP8X4),
-                                  scales=WS[:, r * 512:(r + 1) * 512], in_=wg[:])
+        def sel_pe(b, q):
+            u0 = 7 * q
+            un = min(7, 32 - u0)
+            ps = mp.tile([P, 512], F32, name="ps", tag="pp")
+            pss[(b, q)] = ps
+            for ul in range(un):
+                u = u0 + ul
+                nc.tensor.matmul(out=ps[:, ul * 66:(ul + 1) * 66], lhsT=band[:, 2 * u:2 * u + 128],
+                                 rhs=MR[:, b, :], start=True, stop=True)
+
+        def sel_s(b, q):
+            u0 = 7 * q
+            un = min(7, 32 - u0)
+            nc.scalar.copy(out=M4[0:4, b, u0:u0 + un, :],
+                           in_=pss[(b, q)][0:4, 0:un * 66].rearrange("p (u s) -> p u s", s=66))
+
+        wts = {}
+        wgs = {}
+
+        def w_pe(k):
+            wt = mp.tile([P, 512], F32, name="wt", tag="pp")
+            wts[k] = wt
+            for m in range(2):
+                words = Wsb[:, k, m * 512:(m + 1) * 512].bitcast(F32)
+                for e in range(2):
+                    q = 2 * m + e
+                    nc.tensor.transpose(out=wt[:, q * 128:(q + 1) * 128], in_=words[:, e:256:2],
+                                        identity=identF[:])
+
+        def w_s(k):
+            wg = wgp.tile([P, 1024], BF16, name="wg", align_bytes=64)
+            wgs[k] = wg
+            nc.scalar.copy(out=wg[:].bitcast(F32).rearrange("p (m o e) -> p m o e", m=2, o=128, e=2),
+                           in_=wts[k][:].rearrange("p (m e o) -> p m o e", m=2, e=2, o=128))
+
+        def w_v(k):
+            nc.vector.quantize_mx(out=WC[:, k * 256:(k + 1) * 256].bitcast(FP8X4),
+                                  scales=WS[:, k * 256:(k + 1) * 256], in_=wgs[k][:])
 
         ys = {}
         zs = {}
         accs = {}
         ats = {}
+        fbs = {}
+        outs = {}
 
-        def mx(g):
-            nt, kp = divmod(g, 8)
-            for kl in range(2):
-                for m in range(2):
-                    tl = (2 * kp + kl) * 2 + m
-                    y = yp.tile([P, 512], F32, name="y")
-                    nc.tensor.matmul_mx(out=y[:],
-                                        lhsT=WC[:, tl * 128:(tl + 1) * 128].bitcast(FP8X4),
-                                        lhsT_scale=WS[:, tl * 128:(tl + 1) * 128],
-                                        rhs=FC[:, nt * 512:(nt + 1) * 512].bitcast(FP8X4),
-                                        rhs_scale=FS[:, nt * 512:(nt + 1) * 512],
-                                        start=True, stop=True)
-                    ys[(g, kl, m)] = y
+        def mx(h):
+            nt, k = divmod(h, 16)
+            for m in range(2):
+                tl = 2 * k + m
+                y = yp.tile([P, 512], F32, name="y")
+                nc.tensor.matmul_mx(out=y[:],
+                                    lhsT=WC[:, tl * 128:(tl + 1) * 128].bitcast(FP8X4),
+                                    lhsT_scale=WS[:, tl * 128:(tl + 1) * 128],
+                                    rhs=FC[:, nt * 512:(nt + 1) * 512].bitcast(FP8X4),
+                                    rhs_scale=FS[:, nt * 512:(nt + 1) * 512],
+                                    start=True, stop=True)
+                ys[(h, m)] = y
 
-        def act(g):
-            nt, kp = divmod(g, 8)
-            for kl in range(2):
-                k = 2 * kp + kl
-                z = zp.tile([P, 2, 512], F32, name="z")
-                zs[(g, kl)] = z
-                for m in range(2):
-                    nc.scalar.activation(out=z[:, m, :], in_=ys[(g, kl, m)][:], func=ACT.Relu,
-                                         bias=Btab[:, k, m:m + 1], scale=Stab[:, k, m:m + 1])
+        def act(h):
+            nt, k = divmod(h, 16)
+            z = zp.tile([P, 2, 512], F32, name="z")
+            zs[h] = z
+            for m in range(2):
+                nc.scalar.activation(out=z[:, m, :], in_=ys[(h, m)][:], func=ACT.Relu,
+                                     bias=Btab[:, k, m:m + 1], scale=Stab[:, k, m:m + 1])
 
-        def mul(g):
-            nt, kp = divmod(g, 8)
+        def mul(h):
+            nt, k = divmod(h, 16)
             b, vp = divmod(nt, 2)
-            for kl in range(2):
-                k = 2 * kp + kl
-                i, j = divmod(k, 4)
-                w0 = 1 if (j == 0 and vp == 0) else 0
-                w1 = 15 if (j == 3 and vp == 1) else 16
-                s0 = 2 * vp + j - 1 + 4 * w0
-                s1 = 2 * vp + j - 1 + 4 * (w1 - 1) + 1
-                xv = X[:, b, i:i + 64, :].rearrange("p (a up r2) s -> p up a r2 s", a=16, up=2, r2=2)[:, :, :, 0, s0:s1:4]
-                z = zs[(g, kl)]
-                for m in range(2):
-                    nc.vector.tensor_mul(
-                        out=tbuf[j][:, m, :].rearrange("p (up a w) -> p up a w", up=2, a=16, w=16)[:, :, :, w0:w1],
-                        in0=z[:, m, :].rearrange("p (up a w) -> p up a w", up=2, a=16, w=16)[:, :, :, w0:w1],
-                        in1=xv)
+            i, j = divmod(k, 4)
+            if (vp == 0 and k == 0) or (vp == 1 and k == 3):
+                w = 0 if vp == 0 else 15
+                nc.vector.memset(tbuf[j][:].rearrange("p m (q w) -> p m q w", w=16)[:, :, :, w:w + 1], 0.0)
+            w0 = 1 if (j == 0 and vp == 0) else 0
+            w1 = 15 if (j == 3 and vp == 1) else 16
+            s0 = 2 * vp + j - 1 + 4 * w0
+            s1 = 2 * vp + j - 1 + 4 * (w1 - 1) + 1
+            xv = X[:, b, i:i + 64, :].rearrange("p (a up r2) s -> p up a r2 s", a=16, up=2, r2=2)[:, :, :, 0, s0:s1:4]
+            for m in range(2):
+                nc.vector.tensor_mul(
+                    out=tbuf[j][:, m, :].rearrange("p (up a w) -> p up a w", up=2, a=16, w=16)[:, :, :, w0:w1],
+                    in0=zs[h][:, m, :].rearrange("p (up a w) -> p up a w", up=2, a=16, w=16)[:, :, :, w0:w1],
+                    in1=xv)
 
-        def tr(g):
-            nt, kp = divmod(g, 8)
-            if kp == 0:
+        def tr(h):
+            nt, k = divmod(h, 16)
+            if k == 0:
                 for m in range(2):
-                    accs[(nt, m)] = accp.tile([P, 512], F32, name="acc%d" % m)
-            for kl in range(2):
-                k = 2 * kp + kl
-                j = k % 4
-                for m in range(2):
-                    for blk in range(4):
-                        nc.tensor.matmul(out=accs[(nt, m)][:, blk * 128:(blk + 1) * 128],
-                                         lhsT=tbuf[j][:, m, blk * 128:(blk + 1) * 128],
-                                         rhs=identF[:], is_transpose=True,
-                                         start=(k == 0 and blk == 0), stop=(k == 15 and blk == 3))
-
-        def border(nt):
-            vp = nt % 2
-            j, w = (0, 0) if vp == 0 else (3, 15)
-            nc.vector.memset(tbuf[j][:].rearrange("p m (q w) -> p m q w", w=16)[:, :, :, w:w + 1], 0.0)
+                    accs[(nt, m)] = mp.tile([P, 512], F32, name="acc", tag="pp")
+            j = k % 4
+            for m in range(2):
+                for blk in range(4):
+                    nc.tensor.matmul(out=accs[(nt, m)][:, blk * 128:(blk + 1) * 128],
+                                     lhsT=tbuf[j][:, m, blk * 128:(blk + 1) * 128],
+                                     rhs=identF[:], is_transpose=True,
+                                     start=(k == 0 and blk == 0), stop=(k == 15 and blk == 3))
 
         def evac(nt):
             for m in range(2):
@@ -252,67 +250,130 @@ def tile_revolutionnaive_kernel(tc, x, conv_w, bn_gamma, bn_beta, bn_mean, bn_va
                 nc.scalar.mul(out=at[:], in_=accs[(nt, m)][:], mul=1.0 / 16.0)
                 ats[(nt, m)] = at
 
-        def fin(b):
-            o = op.tile([P, 2048], F32, name="o")
-            ov = o[:].rearrange("p (ah al up x) -> p ah up al x", ah=2, al=8, up=2, x=64)
-            for blk in range(4):
-                up, ah = divmod(blk, 2)
-                fb = mp.tile([P, 512], F32, name="fb", tag="misc")
-                for vp in range(2):
-                    for m in range(2):
-                        q = 2 * vp + m
-                        nc.tensor.transpose(out=fb[:, q * 128:(q + 1) * 128],
-                                            in_=ats[(2 * b + vp, m)][:, blk * 128:(blk + 1) * 128],
-                                            identity=identF[:])
-                dst = ov[:, ah, up].rearrange("p al (w q) -> p al w q", q=4)
-                src = fb[:].rearrange("p (q al w) -> p al w q", q=4, al=8, w=16)
-                if blk % 2 == 0:
-                    nc.vector.tensor_copy(out=dst, in_=src)
-                else:
-                    nc.scalar.copy(out=dst, in_=src)
+        def fin_pe(b, blk):
+            fb = mp.tile([P, 512], F32, name="fb", tag="pp")
+            fbs[(b, blk)] = fb
+            for vp in range(2):
+                for m in range(2):
+                    q = 2 * vp + m
+                    nc.tensor.transpose(out=fb[:, q * 128:(q + 1) * 128],
+                                        in_=ats[(2 * b + vp, m)][:, blk * 128:(blk + 1) * 128],
+                                        identity=identF[:])
+
+        def fin_ev(b, blk, on_vector):
+            if blk == 0:
+                outs[b] = op.tile([P, 2048], F32, name="o")
+            up, ah = divmod(blk, 2)
+            ov = outs[b][:].rearrange("p (ah al up x) -> p ah up al x", ah=2, al=8, up=2, x=64)
+            dst = ov[:, ah, up].rearrange("p al (w q) -> p al w q", q=4)
+            src = fbs[(b, blk)][:].rearrange("p (q al w) -> p al w q", q=4, al=8, w=16)
+            if on_vector:
+                nc.vector.tensor_copy(out=dst, in_=src)
+            else:
+                nc.scalar.copy(out=dst, in_=src)
+
+        def store(b):
             for (p0, c0, cn, n) in REGIONS:
                 nc.sync.dma_start(
                     out=out[b, c0:c0 + cn].rearrange("c (u n) x -> c u n x", n=2)[:, :, n, :],
-                    in_=o[p0:p0 + cn, :].rearrange("p (u x) -> p u x", x=64))
+                    in_=outs[b][p0:p0 + cn, :].rearrange("p (u x) -> p u x", x=64))
 
-        feat_e(0)
-        feat_ft(0)
+        feat_e(0, 0, 33)
+        feat_ft(0, 1, 32)
+        feat_ftb(0)
+        nc.vector.tensor_scalar_add(out=vv[:], in0=raw[0][:], scalar1=BN_EPS)
+        nc.scalar.sqrt(out=vv[:], in_=vv[:])
         feat_g3(0, 0)
         feat_g3(0, 1)
-        feat_g2(0)
+        feat_g2(0, 0)
+        feat_g2(0, 1)
+        nc.vector.reciprocal(out=vv[:], in_=vv[:])
+        nc.vector.tensor_mul(out=sfull[:], in0=raw[1][:], in1=vv[:])
+        nc.vector.tensor_mul(out=bfull[:], in0=raw[2][:], in1=sfull[:])
+        nc.vector.tensor_sub(out=bfull[:], in0=raw[3][:], in1=bfull[:])
+        for tab, full in ((Stab, sfull), (Btab, bfull)):
+            fv = full[:].rearrange("p (k n m) -> p k n m", k=16, n=2, m=2)
+            nc.vector.tensor_copy(out=tab[64:128], in_=fv[64:128, :, 1, :])
+            nc.vector.tensor_copy(out=tab[0:66], in_=fv[0:66, :, 0, :])
+        nc.vector.tensor_tensor(out=band[:, 1:65], in0=identB[:, 0:64], in1=identB[:, 64:128], op=ALU.add)
         chan_max()
-        select_rows(0)
+        for k in range(4):
+            w_pe(k)
+            w_s(k)
+            w_v(k)
+        for q in range(5):
+            sel_pe(0, q)
+            sel_s(0, q)
         feat_x1(0)
         feat_q(0)
-        wprep(0)
-        wprep(1)
-        select_rows(1)
+        w_pe(4)
+        w_s(4)
+        w_v(4)
 
-        extra = {
-            1: [lambda: feat_g3(1, 0)], 2: [lambda: feat_g3(1, 1)],
-            3: [lambda: feat_g2(1), lambda: feat_x1(1)], 4: [lambda: feat_q(1)],
-            5: [lambda: feat_e(1)], 6: [lambda: feat_ft(1)],
-            8: [lambda: feat_g3(2, 0)], 9: [lambda: feat_g3(2, 1)],
-            10: [lambda: feat_g2(2), lambda: feat_x1(2)], 11: [lambda: feat_q(2)],
-            16: [lambda: feat_g3(3, 0)], 17: [lambda: feat_g3(3, 1)],
-            18: [lambda: feat_g2(3), lambda: feat_x1(3)], 19: [lambda: feat_q(3)],
-        }
-        for g in range(32):
-            mx(g)
-            act(g)
-            if g >= 1:
-                tr(g - 1)
-                if g % 8 == 0:
-                    evac(g // 8 - 1)
-                    if g == 16:
-                        fin(0)
-            if g + 2 < 8:
-                wprep(g + 2)
-            if g % 8 == 0:
-                border(g // 8)
-            mul(g)
-            for fn in extra.get(g, []):
+        pe_x = {}
+        s_x = {}
+        v_x = {}
+
+        def at_step(plan, step, fn):
+            plan[step] = plan.get(step, []) + [fn]
+
+        for k in range(5, 16):
+            at_step(pe_x, k - 5, lambda k=k: w_pe(k))
+            at_step(s_x, k - 4, lambda k=k: w_s(k))
+            at_step(v_x, k - 3, lambda k=k: w_v(k))
+        for q in range(5):
+            at_step(pe_x, 12 + q, lambda q=q: sel_pe(1, q))
+            at_step(s_x, 13 + q, lambda q=q: sel_s(1, q))
+
+        def pieces_nt(nt):
+            return [lambda: feat_g3(nt, 0), lambda: feat_g3(nt, 1), lambda: feat_g2(nt, 0),
+                    lambda: feat_g2(nt, 1), lambda: feat_x1(nt), lambda: feat_q(nt)]
+
+        pieces_b1 = [lambda: feat_e(1, 0, 9), lambda: feat_e(1, 9, 17), lambda: feat_e(1, 17, 25),
+                     lambda: feat_e(1, 25, 33), lambda: feat_ft(1, 1, 9), lambda: feat_ft(1, 9, 17),
+                     lambda: feat_ft(1, 17, 25), lambda: feat_ft(1, 25, 32), lambda: feat_ftb(1)]
+        for q, fn in enumerate(pieces_nt(1)):
+            at_step(v_x, 1 + q, fn)
+        for q, fn in enumerate(pieces_b1 + pieces_nt(2)):
+            at_step(v_x, 13 + q, fn)
+        for q, fn in enumerate(pieces_nt(3)):
+            at_step(v_x, 33 + q, fn)
+        for nt in range(4):
+            e = 16 * nt + (17 if PG == 1 else 18)
+            at_step(s_x, e + 1, lambda nt=nt: evac(nt))
+            if nt % 2 == 1:
+                b = nt // 2
+                for blk in range(4):
+                    at_step(pe_x, e + 2 + blk, lambda b=b, blk=blk: fin_pe(b, blk))
+                    if b == 1 and blk % 2 == 0:
+                        at_step(v_x, e + 3 + blk, lambda b=b, blk=blk: fin_ev(b, blk, True))
+                    else:
+                        at_step(s_x, e + 3 + blk, lambda b=b, blk=blk: fin_ev(b, blk, False))
+                at_step(s_x, e + 7, lambda b=b: store(b))
+
+        for h in range(NS + 26):
+            if PG == 1:
+                mxs = [h]
+                trs = [h - 2]
+            elif h % 2 == 0:
+                mxs = [h, h + 1]
+                trs = [h - 3, h - 2]
+            else:
+                mxs = []
+                trs = []
+            for q in mxs:
+                if q < NS:
+                    mx(q)
+            if h < NS:
+                act(h)
+            for q in trs:
+                if 0 <= q < NS:
+                    tr(q)
+            for fn in pe_x.get(h, []):
                 fn()
-        tr(31)
-        evac(3)
-        fin(1)
+            for fn in s_x.get(h, []):
+                fn()
+            if h < NS:
+                mul(h)
+            for fn in v_x.get(h, []):
+                fn()

@@ -17,7 +17,7 @@ P = 128
 C = 62
 FLOPS = 2 * 3968 * 512 * 2048
 BN_EPS = 1e-5
-PG = 1
+PG = 2
 NS = 64
 
 REGIONS = [(4, 0, 32, 0), (36, 32, 30, 0), (66, 0, 32, 1), (98, 32, 30, 1)]

@@ -1,8 +1,6 @@
 from contextlib import ExitStack
 
-import concourse.bass as bass
 import concourse.mybir as mybir
-import concourse.tile as tile
 from concourse.masks import make_identity
 
 F32 = mybir.dt.float32
@@ -15,12 +13,15 @@ ALU = mybir.AluOpType
 
 P = 128
 C = 62
+TAPS = 16
 FLOPS = 2 * 3968 * 512 * 2048
 BN_EPS = 1e-5
-PG = 2
-NS = 64
+STEPS = 4 * TAPS
+LAG = 2
+W_AHEAD = 6
 
-REGIONS = [(4, 0, 32, 0), (36, 32, 30, 0), (66, 0, 32, 1), (98, 32, 30, 1)]
+LOWER = [(4, 0, 32, 0), (36, 32, 30, 0)]
+UPPER = [(66, 0, 32, 1), (98, 32, 30, 1)]
 
 
 def tile_revolutionnaive_kernel(tc, x, conv_w, bn_gamma, bn_beta, bn_mean, bn_var, out):
@@ -32,15 +33,16 @@ def tile_revolutionnaive_kernel(tc, x, conv_w, bn_gamma, bn_beta, bn_mean, bn_va
         atp = ctx.enter_context(tc.tile_pool(name="atp", bufs=4))
         op = ctx.enter_context(tc.tile_pool(name="op", bufs=2))
         yp = ctx.enter_context(tc.psum_pool(name="yp", bufs=4))
-        mp = ctx.enter_context(tc.psum_pool(name="mp", bufs=4))
+        accp = ctx.enter_context(tc.psum_pool(name="accp", bufs=3))
+        mp = ctx.enter_context(tc.psum_pool(name="mp", bufs=1))
         ctx.enter_context(tc.manual_schedule())
 
-        X = keep.tile([P, 2, 68, 64], BF16, name="X")
+        X = keep.tile([P, 2, 66, 64], BF16, name="X")
         XS = keep.tile([P, C * 64], BF16, name="XS")
-        Wsb = keep.tile([P, 16, 1024], BF16, name="Wsb")
+        Wsb = keep.tile([P, TAPS, 1024], BF16, name="Wsb")
         E = keep.tile([P, 2, 33, 66], BF16, name="E")
         FT = keep.tile([P, 2, 33, 66], BF16, name="FT")
-        M4 = keep.tile([P, 2, 32, 66], BF16, name="M4")
+        M4 = keep.tile([P, 2, 2, 16, 66], BF16, name="M4")
         G = keep.tile([P, 4, 2048], BF16, name="G", align_bytes=64)
         FC = keep.tile([P, 2048], U32, name="FC", align_bytes=64)
         FS = keep.tile([P, 2048], U8, name="FS", align_bytes=64)
@@ -50,16 +52,171 @@ def tile_revolutionnaive_kernel(tc, x, conv_w, bn_gamma, bn_beta, bn_mean, bn_va
         identF = keep.tile([P, P], F32, name="identF")
         identB = keep.tile([P, P], BF16, name="identB")
         band = keep.tile([P, 192], BF16, name="band")
-        MR = keep.tile([P, 2, 66], BF16, name="MR")
+        MR = keep.tile([P, 2, 64], BF16, name="MR")
         raw = [keep.tile([P, 64], BF16, name="raw%d" % q) for q in range(4)]
-        Stab = keep.tile([P, 16, 2], F32, name="Stab")
-        Btab = keep.tile([P, 16, 2], F32, name="Btab")
-
+        Stab = keep.tile([P, TAPS, 2], F32, name="Stab")
+        Btab = keep.tile([P, TAPS, 2], F32, name="Btab")
         ta = keep.tile([P, 1984], BF16, name="ta")
         tb = keep.tile([P, 1024], BF16, name="tb")
         vv = keep.tile([P, 64], F32, name="vv")
         sfull = keep.tile([P, 64], F32, name="sfull")
         bfull = keep.tile([P, 64], F32, name="bfull")
+
+        w5 = conv_w.rearrange("(c k n m) f -> c k n (m f)", c=C, k=TAPS, n=2, m=2)
+
+        def load_x(queue, b, ranges):
+            for (p0, c0, cn, n) in ranges:
+                queue.dma_start(out=X[p0:p0 + cn, b, 1:65, :], in_=x[b, c0:c0 + cn])
+
+        def load_w(queue, k0, ranges):
+            for (p0, c0, cn, n) in ranges:
+                queue.dma_start(out=Wsb[p0:p0 + cn, k0:k0 + 4, :], in_=w5[c0:c0 + cn, k0:k0 + 4, n, :])
+
+        def feat_e(b, u0, u1):
+            xr = X[0:66, b, 2 * u0:2 * u1, :].rearrange("p (u r2) s -> p u r2 s", r2=2)
+            nc.vector.tensor_max(out=E[0:66, b, u0:u1, 1:65], in0=xr[:, :, 0, :], in1=xr[:, :, 1, :])
+
+        def feat_ft(b, v0, v1):
+            nc.vector.tensor_max(out=FT[64:128, b, v0:v1, :],
+                                 in0=X[64:128, b, :, 2 * v0 - 1:2 * v1 - 2:2].rearrange("p r v -> p v r"),
+                                 in1=X[64:128, b, :, 2 * v0:2 * v1 - 1:2].rearrange("p r v -> p v r"))
+
+        def feat_ftb(b):
+            nc.vector.tensor_scalar_max(out=FT[64:128, b, 0:33:32, :],
+                                        in0=X[64:128, b, :, 0:64:63].rearrange("p r v -> p v r"), scalar1=0.0)
+
+        def feat_g3(nt, vp):
+            b, up = divmod(nt, 2)
+            nc.vector.tensor_max(
+                out=G[64:128, nt, vp * 1024:(vp + 1) * 1024].rearrange("p (a w i) -> p a w i", a=16, w=16, i=4),
+                in0=FT[64:128, b, vp:vp + 31:2, 2 * up:2 * up + 64].rearrange("p w (a i) -> p a w i", i=4),
+                in1=FT[64:128, b, vp + 1:vp + 32:2, 2 * up:2 * up + 64].rearrange("p w (a i) -> p a w i", i=4))
+
+        def feat_g2(nt, vp):
+            b, up = divmod(nt, 2)
+            nc.vector.tensor_max(
+                out=G[0:66, nt, vp * 1024:(vp + 1) * 1024].rearrange("p (a s) -> p a s", a=16, s=64),
+                in0=E[0:66, b, up:up + 31:2, 2 * vp:2 * vp + 64],
+                in1=E[0:66, b, up + 1:up + 32:2, 2 * vp:2 * vp + 64])
+
+        def feat_x1(nt, vp):
+            b, up = divmod(nt, 2)
+            nc.vector.tensor_copy(
+                out=G[0:4, nt, vp * 1024:(vp + 1) * 1024].rearrange("p (a s) -> p a s", a=16, s=64),
+                in_=M4[0:4, b, up, :, 2 * vp:2 * vp + 64])
+
+        def feat_q(nt):
+            nc.vector.quantize_mx(out=FC[:, nt * 512:(nt + 1) * 512].bitcast(FP8X4),
+                                  scales=FS[:, nt * 512:(nt + 1) * 512], in_=G[:, nt, :])
+
+        def chan_max():
+            nc.vector.tensor_max(out=ta[:], in0=XS[:, 0:1984], in1=XS[:, 1984:3968])
+            nc.vector.tensor_max(out=tb[:], in0=ta[:, 0:1024], in1=ta[:, 960:1984])
+            nc.vector.tensor_max(out=ta[:, 0:512], in0=tb[:, 0:512], in1=tb[:, 512:1024])
+            nc.vector.tensor_max(out=tb[:, 0:256], in0=ta[:, 0:256], in1=ta[:, 256:512])
+            nc.vector.tensor_max(out=ta[:, 0:128], in0=tb[:, 0:128], in1=tb[:, 128:256])
+            nc.vector.tensor_max(out=MR[0:64, 0, :], in0=ta[0:64, 0:64], in1=ta[0:64, 64:128])
+            nc.vector.tensor_max(out=MR[64:128, 1, :], in0=ta[64:128, 0:64], in1=ta[64:128, 64:128])
+
+        def select_rows(nt, half, pool):
+            b, up = divmod(nt, 2)
+            ps = pool.tile([P, 512], F32, name="ps", tag="y" if pool is yp else "misc")
+            for al in range(8):
+                u = 2 * (8 * half + al) + up
+                nc.tensor.matmul(out=ps[:, al * 64:(al + 1) * 64], lhsT=band[:, 2 * u:2 * u + 128],
+                                 rhs=MR[:, b, :], start=True, stop=True)
+            nc.scalar.copy(out=M4[0:4, b, up, 8 * half:8 * half + 8, 1:65],
+                           in_=ps[0:4, :].rearrange("p (a s) -> p a s", s=64))
+
+        def weights(k, pool):
+            wt = pool.tile([P, 512], F32, name="wt", tag="y" if pool is yp else "misc")
+            for m in range(2):
+                words = Wsb[:, k, m * 512:(m + 1) * 512].bitcast(F32)
+                for e in range(2):
+                    q = 2 * m + e
+                    nc.tensor.transpose(out=wt[:, q * 128:(q + 1) * 128], in_=words[:, e:256:2],
+                                        identity=identF[:])
+            wg = wgp.tile([P, 1024], BF16, name="wg", align_bytes=64)
+            nc.scalar.copy(out=wg[:].bitcast(F32).rearrange("p (m o e) -> p m o e", m=2, o=128, e=2),
+                           in_=wt[:].rearrange("p (m e o) -> p m o e", m=2, e=2, o=128))
+            return wg
+
+        def weights_q(k, wg):
+            nc.vector.quantize_mx(out=WC[:, k * 256:(k + 1) * 256].bitcast(FP8X4),
+                                  scales=WS[:, k * 256:(k + 1) * 256], in_=wg[:])
+
+        def mx_act(h):
+            nt, k = divmod(h, TAPS)
+            z = zp.tile([P, 2, 512], F32, name="z")
+            ys = []
+            for m in range(2):
+                tl = 2 * k + m
+                y = yp.tile([P, 512], F32, name="y")
+                nc.tensor.matmul_mx(out=y[:],
+                                    lhsT=WC[:, tl * 128:(tl + 1) * 128].bitcast(FP8X4),
+                                    lhsT_scale=WS[:, tl * 128:(tl + 1) * 128],
+                                    rhs=FC[:, nt * 512:(nt + 1) * 512].bitcast(FP8X4),
+                                    rhs_scale=FS[:, nt * 512:(nt + 1) * 512],
+                                    start=True, stop=True)
+                ys.append(y)
+            for m in range(2):
+                nc.scalar.activation(out=z[:, m, :], in_=ys[m][:], func=ACT.Relu,
+                                     bias=Btab[:, k, m:m + 1], scale=Stab[:, k, m:m + 1])
+            return z
+
+        def mul(h, z):
+            nt, k = divmod(h, TAPS)
+            b, up = divmod(nt, 2)
+            i, j = divmod(k, 4)
+            for vp in range(2):
+                w0 = 1 if (j == 0 and vp == 0) else 0
+                w1 = 15 if (j == 3 and vp == 1) else 16
+                r0 = 2 * up + i
+                c0 = 2 * vp + j - 1
+                patch = X[:, b, r0:r0 + 61:4, c0 + 4 * w0:c0 + 4 * (w1 - 1) + 1:4]
+                nc.vector.tensor_mul(
+                    out=tbuf[j][:, :, vp * 256:(vp + 1) * 256].rearrange("p m (a w) -> p m a w", w=16)[:, :, :, w0:w1],
+                    in0=z[:, :, vp * 256:(vp + 1) * 256].rearrange("p m (a w) -> p m a w", w=16)[:, :, :, w0:w1],
+                    in1=patch.unsqueeze(1).to_broadcast([P, 2, 16, w1 - w0]))
+
+        def add_up(h, acc):
+            k = h % TAPS
+            for m in range(2):
+                for blk in range(4):
+                    nc.tensor.matmul(out=acc[m][:, blk * 128:(blk + 1) * 128],
+                                     lhsT=tbuf[k % 4][:, m, blk * 128:(blk + 1) * 128],
+                                     rhs=identF[:], is_transpose=True,
+                                     start=(k == 0 and blk == 0), stop=(k == TAPS - 1 and blk == 3))
+
+        def leave_psum(acc):
+            ats = []
+            for m in range(2):
+                at = atp.tile([P, 512], F32, name="at")
+                nc.scalar.mul(out=at[:], in_=acc[m][:], mul=1.0 / TAPS)
+                ats.append(at)
+            return ats
+
+        def turn_back(ats, o, ah, on_vector):
+            fb = mp.tile([P, 512], F32, name="fb", tag="misc")
+            for vp in range(2):
+                for m in range(2):
+                    q = 2 * vp + m
+                    blk = 2 * vp + ah
+                    nc.tensor.transpose(out=fb[:, q * 128:(q + 1) * 128],
+                                        in_=ats[m][:, blk * 128:(blk + 1) * 128], identity=identF[:])
+            dst = o[:, ah * 512:(ah + 1) * 512].rearrange("p (al w q) -> p al w q", al=8, w=16, q=4)
+            src = fb[:].rearrange("p (q al w) -> p al w q", q=4, al=8, w=16)
+            if on_vector:
+                nc.vector.tensor_copy(out=dst, in_=src)
+            else:
+                nc.scalar.copy(out=dst, in_=src)
+
+        def store(nt, o):
+            b, up = divmod(nt, 2)
+            for (p0, c0, cn, n) in LOWER + UPPER:
+                nc.sync.dma_start(
+                    out=out[b, c0:c0 + cn].rearrange("c (a r) s -> c a r s", r=4)[:, :, 2 * up + n, :],
+                    in_=o[p0:p0 + cn, :].rearrange("p (a s) -> p a s", s=64))
 
         for b in range(2):
             nc.gpsimd.dma_start(out=XS[64 * b:64 * b + 64, :].rearrange("r (c s) -> r c s", s=64),
@@ -74,306 +231,100 @@ def tile_revolutionnaive_kernel(tc, x, conv_w, bn_gamma, bn_beta, bn_mean, bn_va
             nc.gpsimd.dma_start(out=raw[q][66:128, :], in_=v2)
         nc.vector.memset(X[:, :, 0:66:65, :], 0.0)
 
-        def load_x(b):
-            for (p0, c0, cn, n) in REGIONS + [(0, 0, 4, 0)]:
-                nc.sync.dma_start(out=X[p0:p0 + cn, b, 1:65, :], in_=x[b, c0:c0 + cn])
-
-        w5 = conv_w.rearrange("(c k n m) f -> c k n (m f)", c=C, k=16, n=2, m=2)
-
-        def load_w(k0, k1):
-            for (p0, c0, cn, n) in REGIONS:
-                nc.sync.dma_start(out=Wsb[p0:p0 + cn, k0:k1, :], in_=w5[c0:c0 + cn, k0:k1, n, :])
-
-        load_x(0)
+        load_x(nc.sync, 0, LOWER + [(0, 0, 4, 0)])
+        load_x(nc.scalar, 0, UPPER)
         nc.sync.dma_start(out=Wsb[0:4, :, :].rearrange("p k f -> p (k f)"),
                           in_=conv_w[0:128, :].rearrange("(p a) f -> p (a f)", p=4))
-        load_w(0, 4)
-        load_w(4, 8)
-        load_w(8, 12)
-        load_w(12, 16)
-        load_x(1)
+        load_w(nc.sync, 0, LOWER)
+        load_w(nc.scalar, 0, UPPER)
+        load_w(nc.sync, 4, LOWER)
+        load_w(nc.scalar, 4, UPPER)
+        load_w(nc.sync, 8, LOWER)
+        load_w(nc.sync, 12, LOWER)
+        load_x(nc.sync, 1, LOWER + [(0, 0, 4, 0)])
 
         nc.vector.memset(band[:], 0.0)
         nc.vector.memset(MR[:], 0.0)
         nc.vector.memset(E[:, :, :, 0:66:65], 0.0)
-
-        def feat_e(b, u0, u1):
-            xr = X[0:66, b, 2 * u0:2 * u1, :].rearrange("p (u r2) s -> p u r2 s", r2=2)
-            nc.vector.tensor_max(out=E[0:66, b, u0:u1, 1:65], in0=xr[:, :, 0, :], in1=xr[:, :, 1, :])
-
-        def feat_ft(b, v0, v1):
-            nc.vector.tensor_max(out=FT[64:128, b, v0:v1, :],
-                                 in0=X[64:128, b, 0:66, 2 * v0 - 1:2 * v1 - 2:2].rearrange("p r v -> p v r"),
-                                 in1=X[64:128, b, 0:66, 2 * v0:2 * v1 - 1:2].rearrange("p r v -> p v r"))
-
-        def feat_ftb(b):
-            nc.vector.tensor_scalar_max(out=FT[64:128, b, 0:33:32, :],
-                                        in0=X[64:128, b, 0:66, 0:64:63].rearrange("p r v -> p v r"),
-                                        scalar1=0.0)
-
-        def feat_g3(nt, up):
-            b, vp = divmod(nt, 2)
-            nc.vector.tensor_max(
-                out=G[64:128, nt, up * 1024:(up + 1) * 1024].rearrange("p (a w i) -> p a w i", a=16, w=16, i=4),
-                in0=FT[64:128, b, vp:vp + 31:2, 2 * up:2 * up + 64].rearrange("p w (a i) -> p a w i", i=4),
-                in1=FT[64:128, b, vp + 1:vp + 32:2, 2 * up:2 * up + 64].rearrange("p w (a i) -> p a w i", i=4))
-
-        def feat_g2(nt, up):
-            b, vp = divmod(nt, 2)
-            nc.vector.tensor_max(
-                out=G[0:66, nt, up * 1024:(up + 1) * 1024].rearrange("p (a x) -> p a x", a=16, x=64),
-                in0=E[0:66, b, up:up + 31:2, 2 * vp:2 * vp + 64],
-                in1=E[0:66, b, up + 1:up + 32:2, 2 * vp:2 * vp + 64])
-
-        def feat_x1(nt):
-            b, vp = divmod(nt, 2)
-            nc.vector.tensor_copy(
-                out=G[0:4, nt, :].rearrange("p (up a x) -> p up a x", up=2, a=16, x=64),
-                in_=M4[0:4, b, :, 2 * vp:2 * vp + 64].rearrange("p (a up) x -> p up a x", up=2))
-
-        def feat_q(nt):
-            nc.vector.quantize_mx(out=FC[:, nt * 512:(nt + 1) * 512].bitcast(FP8X4),
-                                  scales=FS[:, nt * 512:(nt + 1) * 512], in_=G[:, nt, :])
-
-        def chan_max():
-            nc.vector.tensor_max(out=ta[:], in0=XS[:, 0:1984], in1=XS[:, 1984:3968])
-            nc.vector.tensor_max(out=tb[:], in0=ta[:, 0:1024], in1=ta[:, 960:1984])
-            nc.vector.tensor_max(out=ta[:, 0:512], in0=tb[:, 0:512], in1=tb[:, 512:1024])
-            nc.vector.tensor_max(out=tb[:, 0:256], in0=ta[:, 0:256], in1=ta[:, 256:512])
-            nc.vector.tensor_max(out=ta[:, 0:128], in0=tb[:, 0:128], in1=tb[:, 128:256])
-            nc.vector.tensor_max(out=MR[0:64, 0, 1:65], in0=ta[0:64, 0:64], in1=ta[0:64, 64:128])
-            nc.vector.tensor_max(out=MR[64:128, 1, 1:65], in0=ta[64:128, 0:64], in1=ta[64:128, 64:128])
-
-        pss = {}
-
-        def sel_pe(b, q):
-            u0 = 7 * q
-            un = min(7, 32 - u0)
-            ps = mp.tile([P, 512], F32, name="ps", tag="pp")
-            pss[(b, q)] = ps
-            for ul in range(un):
-                u = u0 + ul
-                nc.tensor.matmul(out=ps[:, ul * 66:(ul + 1) * 66], lhsT=band[:, 2 * u:2 * u + 128],
-                                 rhs=MR[:, b, :], start=True, stop=True)
-
-        def sel_s(b, q):
-            u0 = 7 * q
-            un = min(7, 32 - u0)
-            nc.scalar.copy(out=M4[0:4, b, u0:u0 + un, :],
-                           in_=pss[(b, q)][0:4, 0:un * 66].rearrange("p (u s) -> p u s", s=66))
-
-        wts = {}
-        wgs = {}
-
-        def w_pe(k):
-            wt = mp.tile([P, 512], F32, name="wt", tag="pp")
-            wts[k] = wt
-            for m in range(2):
-                words = Wsb[:, k, m * 512:(m + 1) * 512].bitcast(F32)
-                for e in range(2):
-                    q = 2 * m + e
-                    nc.tensor.transpose(out=wt[:, q * 128:(q + 1) * 128], in_=words[:, e:256:2],
-                                        identity=identF[:])
-
-        def w_s(k):
-            wg = wgp.tile([P, 1024], BF16, name="wg", align_bytes=64)
-            wgs[k] = wg
-            nc.scalar.copy(out=wg[:].bitcast(F32).rearrange("p (m o e) -> p m o e", m=2, o=128, e=2),
-                           in_=wts[k][:].rearrange("p (m e o) -> p m o e", m=2, e=2, o=128))
-
-        def w_v(k):
-            nc.vector.quantize_mx(out=WC[:, k * 256:(k + 1) * 256].bitcast(FP8X4),
-                                  scales=WS[:, k * 256:(k + 1) * 256], in_=wgs[k][:])
-
-        ys = {}
-        zs = {}
-        accs = {}
-        ats = {}
-        fbs = {}
-        outs = {}
-
-        def mx(h):
-            nt, k = divmod(h, 16)
-            for m in range(2):
-                tl = 2 * k + m
-                y = yp.tile([P, 512], F32, name="y")
-                nc.tensor.matmul_mx(out=y[:],
-                                    lhsT=WC[:, tl * 128:(tl + 1) * 128].bitcast(FP8X4),
-                                    lhsT_scale=WS[:, tl * 128:(tl + 1) * 128],
-                                    rhs=FC[:, nt * 512:(nt + 1) * 512].bitcast(FP8X4),
-                                    rhs_scale=FS[:, nt * 512:(nt + 1) * 512],
-                                    start=True, stop=True)
-                ys[(h, m)] = y
-
-        def act(h):
-            nt, k = divmod(h, 16)
-            z = zp.tile([P, 2, 512], F32, name="z")
-            zs[h] = z
-            for m in range(2):
-                nc.scalar.activation(out=z[:, m, :], in_=ys[(h, m)][:], func=ACT.Relu,
-                                     bias=Btab[:, k, m:m + 1], scale=Stab[:, k, m:m + 1])
-
-        def mul(h):
-            nt, k = divmod(h, 16)
-            b, vp = divmod(nt, 2)
-            i, j = divmod(k, 4)
-            if (vp == 0 and k == 0) or (vp == 1 and k == 3):
-                w = 0 if vp == 0 else 15
-                nc.vector.memset(tbuf[j][:].rearrange("p m (q w) -> p m q w", w=16)[:, :, :, w:w + 1], 0.0)
-            w0 = 1 if (j == 0 and vp == 0) else 0
-            w1 = 15 if (j == 3 and vp == 1) else 16
-            s0 = 2 * vp + j - 1 + 4 * w0
-            s1 = 2 * vp + j - 1 + 4 * (w1 - 1) + 1
-            xv = X[:, b, i:i + 64, :].rearrange("p (a up r2) s -> p up a r2 s", a=16, up=2, r2=2)[:, :, :, 0, s0:s1:4]
-            for m in range(2):
-                nc.vector.tensor_mul(
-                    out=tbuf[j][:, m, :].rearrange("p (up a w) -> p up a w", up=2, a=16, w=16)[:, :, :, w0:w1],
-                    in0=zs[h][:, m, :].rearrange("p (up a w) -> p up a w", up=2, a=16, w=16)[:, :, :, w0:w1],
-                    in1=xv)
-
-        def tr(h):
-            nt, k = divmod(h, 16)
-            if k == 0:
-                for m in range(2):
-                    accs[(nt, m)] = mp.tile([P, 512], F32, name="acc", tag="pp")
-            j = k % 4
-            for m in range(2):
-                for blk in range(4):
-                    nc.tensor.matmul(out=accs[(nt, m)][:, blk * 128:(blk + 1) * 128],
-                                     lhsT=tbuf[j][:, m, blk * 128:(blk + 1) * 128],
-                                     rhs=identF[:], is_transpose=True,
-                                     start=(k == 0 and blk == 0), stop=(k == 15 and blk == 3))
-
-        def evac(nt):
-            for m in range(2):
-                at = atp.tile([P, 512], F32, name="at")
-                nc.scalar.mul(out=at[:], in_=accs[(nt, m)][:], mul=1.0 / 16.0)
-                ats[(nt, m)] = at
-
-        def fin_pe(b, blk):
-            fb = mp.tile([P, 512], F32, name="fb", tag="pp")
-            fbs[(b, blk)] = fb
-            for vp in range(2):
-                for m in range(2):
-                    q = 2 * vp + m
-                    nc.tensor.transpose(out=fb[:, q * 128:(q + 1) * 128],
-                                        in_=ats[(2 * b + vp, m)][:, blk * 128:(blk + 1) * 128],
-                                        identity=identF[:])
-
-        def fin_ev(b, blk, on_vector):
-            if blk == 0:
-                outs[b] = op.tile([P, 2048], F32, name="o")
-            up, ah = divmod(blk, 2)
-            ov = outs[b][:].rearrange("p (ah al up x) -> p ah up al x", ah=2, al=8, up=2, x=64)
-            dst = ov[:, ah, up].rearrange("p al (w q) -> p al w q", q=4)
-            src = fbs[(b, blk)][:].rearrange("p (q al w) -> p al w q", q=4, al=8, w=16)
-            if on_vector:
-                nc.vector.tensor_copy(out=dst, in_=src)
-            else:
-                nc.scalar.copy(out=dst, in_=src)
-
-        def store(b):
-            for (p0, c0, cn, n) in REGIONS:
-                nc.sync.dma_start(
-                    out=out[b, c0:c0 + cn].rearrange("c (u n) x -> c u n x", n=2)[:, :, n, :],
-                    in_=outs[b][p0:p0 + cn, :].rearrange("p (u x) -> p u x", x=64))
+        nc.vector.memset(M4[0:4, :, :, :, 0:66:65], 0.0)
+        nc.vector.memset(tbuf[0][:, :, 0:256].rearrange("p m (a w) -> p m a w", w=16)[:, :, :, 0:1], 0.0)
+        nc.vector.memset(tbuf[3][:, :, 256:512].rearrange("p m (a w) -> p m a w", w=16)[:, :, :, 15:16], 0.0)
+        nc.vector.tensor_tensor(out=band[:, 1:65], in0=identB[:, 0:64], in1=identB[:, 64:128], op=ALU.add)
 
         feat_e(0, 0, 33)
         feat_ft(0, 1, 32)
         feat_ftb(0)
         nc.vector.tensor_scalar_add(out=vv[:], in0=raw[0][:], scalar1=BN_EPS)
         nc.scalar.sqrt(out=vv[:], in_=vv[:])
-        feat_g3(0, 0)
-        feat_g3(0, 1)
-        feat_g2(0, 0)
-        feat_g2(0, 1)
+        for vp in range(2):
+            feat_g3(0, vp)
+        for vp in range(2):
+            feat_g2(0, vp)
         nc.vector.reciprocal(out=vv[:], in_=vv[:])
         nc.vector.tensor_mul(out=sfull[:], in0=raw[1][:], in1=vv[:])
         nc.vector.tensor_mul(out=bfull[:], in0=raw[2][:], in1=sfull[:])
         nc.vector.tensor_sub(out=bfull[:], in0=raw[3][:], in1=bfull[:])
         for tab, full in ((Stab, sfull), (Btab, bfull)):
-            fv = full[:].rearrange("p (k n m) -> p k n m", k=16, n=2, m=2)
+            fv = full[:].rearrange("p (k n m) -> p k n m", k=TAPS, n=2, m=2)
             nc.vector.tensor_copy(out=tab[64:128], in_=fv[64:128, :, 1, :])
             nc.vector.tensor_copy(out=tab[0:66], in_=fv[0:66, :, 0, :])
-        nc.vector.tensor_tensor(out=band[:, 1:65], in0=identB[:, 0:64], in1=identB[:, 64:128], op=ALU.add)
         chan_max()
+        wgs = {}
         for k in range(4):
-            w_pe(k)
-            w_s(k)
-            w_v(k)
-        for q in range(5):
-            sel_pe(0, q)
-            sel_s(0, q)
-        feat_x1(0)
+            wgs[k] = weights(k, yp)
+        load_w(nc.scalar, 8, UPPER)
+        for half in range(2):
+            select_rows(0, half, yp)
+        load_w(nc.scalar, 12, UPPER)
+        for vp in range(2):
+            feat_g3(1, vp)
+        for k in range(4):
+            weights_q(k, wgs[k])
+        for vp in range(2):
+            feat_x1(0, vp)
         feat_q(0)
-        w_pe(4)
-        w_s(4)
-        w_v(4)
+        for k in range(4, W_AHEAD):
+            weights_q(k, weights(k, yp))
+        load_x(nc.scalar, 1, UPPER)
 
-        pe_x = {}
-        s_x = {}
-        v_x = {}
+        def later(nt):
+            return ([lambda vp=vp: feat_g3(nt, vp) for vp in range(2)] + [lambda vp=vp: feat_g2(nt, vp) for vp in range(2)]
+                    + [lambda vp=vp: feat_x1(nt, vp) for vp in range(2)] + [lambda: feat_q(nt)])
 
-        def at_step(plan, step, fn):
-            plan[step] = plan.get(step, []) + [fn]
+        batch1 = ([lambda u=u: feat_e(1, u, u + 11) for u in (0, 11, 22)]
+                  + [lambda: feat_ft(1, 1, 11), lambda: feat_ft(1, 11, 21), lambda: (feat_ft(1, 21, 32), feat_ftb(1))])
+        side = {1: later(1)[2:], 2: batch1 + later(2), 3: later(3)}
 
-        for k in range(5, 16):
-            at_step(pe_x, k - 5, lambda k=k: w_pe(k))
-            at_step(s_x, k - 4, lambda k=k: w_s(k))
-            at_step(v_x, k - 3, lambda k=k: w_v(k))
-        for q in range(5):
-            at_step(pe_x, 12 + q, lambda q=q: sel_pe(1, q))
-            at_step(s_x, 13 + q, lambda q=q: sel_s(1, q))
-
-        def pieces_nt(nt):
-            return [lambda: feat_g3(nt, 0), lambda: feat_g3(nt, 1), lambda: feat_g2(nt, 0),
-                    lambda: feat_g2(nt, 1), lambda: feat_x1(nt), lambda: feat_q(nt)]
-
-        pieces_b1 = [lambda: feat_e(1, 0, 9), lambda: feat_e(1, 9, 17), lambda: feat_e(1, 17, 25),
-                     lambda: feat_e(1, 25, 33), lambda: feat_ft(1, 1, 9), lambda: feat_ft(1, 9, 17),
-                     lambda: feat_ft(1, 17, 25), lambda: feat_ft(1, 25, 32), lambda: feat_ftb(1)]
-        for q, fn in enumerate(pieces_nt(1)):
-            at_step(v_x, 1 + q, fn)
-        for q, fn in enumerate(pieces_b1 + pieces_nt(2)):
-            at_step(v_x, 13 + q, fn)
-        for q, fn in enumerate(pieces_nt(3)):
-            at_step(v_x, 33 + q, fn)
-        for nt in range(4):
-            e = 16 * nt + (17 if PG == 1 else 18)
-            at_step(s_x, e + 1, lambda nt=nt: evac(nt))
-            if nt % 2 == 1:
-                b = nt // 2
-                for blk in range(4):
-                    at_step(pe_x, e + 2 + blk, lambda b=b, blk=blk: fin_pe(b, blk))
-                    if b == 1 and blk % 2 == 0:
-                        at_step(v_x, e + 3 + blk, lambda b=b, blk=blk: fin_ev(b, blk, True))
-                    else:
-                        at_step(s_x, e + 3 + blk, lambda b=b, blk=blk: fin_ev(b, blk, False))
-                at_step(s_x, e + 7, lambda b=b: store(b))
-
-        for h in range(NS + 26):
-            if PG == 1:
-                mxs = [h]
-                trs = [h - 2]
-            elif h % 2 == 0:
-                mxs = [h, h + 1]
-                trs = [h - 3, h - 2]
-            else:
-                mxs = []
-                trs = []
-            for q in mxs:
-                if q < NS:
-                    mx(q)
-            if h < NS:
-                act(h)
-            for q in trs:
-                if 0 <= q < NS:
-                    tr(q)
-            for fn in pe_x.get(h, []):
-                fn()
-            for fn in s_x.get(h, []):
-                fn()
-            if h < NS:
-                mul(h)
-            for fn in v_x.get(h, []):
-                fn()
+        zs = {}
+        accs = {}
+        done = {}
+        for h in range(STEPS + LAG + 3):
+            nt, k = divmod(h, TAPS)
+            if h < STEPS:
+                zs[h] = mx_act(h)
+            g = h - LAG
+            if 0 <= g < STEPS:
+                if g % TAPS == 0:
+                    accs[g // TAPS] = [accp.tile([P, 512], F32, name="acc") for m in range(2)]
+                add_up(g, accs[g // TAPS])
+                if g % TAPS == TAPS - 1:
+                    done[g // TAPS] = (leave_psum(accs[g // TAPS]), op.tile([P, 1024], F32, name="o"))
+            f = h - LAG - TAPS
+            if f >= 0 and f % TAPS in (0, 1):
+                ats, o = done[f // TAPS]
+                turn_back(ats, o, f % TAPS, on_vector=(h >= STEPS and f % TAPS == 1))
+                if f % TAPS == 1:
+                    store(f // TAPS, o)
+            if h + W_AHEAD < TAPS:
+                wgs[h + W_AHEAD] = weights(h + W_AHEAD, mp)
+            if nt < 3 and k in (10, 11):
+                select_rows(nt + 1, k - 10, mp)
+            if h < STEPS:
+                mul(h, zs[h])
+            if 1 <= h and h - 1 + W_AHEAD < TAPS:
+                weights_q(h - 1 + W_AHEAD, wgs[h - 1 + W_AHEAD])
+            if nt < 3:
+                todo = side[nt + 1]
+                first = TAPS - 1 - len(todo)
+                if 0 <= k - first < len(todo):
+                    todo[k - first]()

@@ -18,7 +18,7 @@ FLOPS = 2 * 3968 * 512 * 2048
 BN_EPS = 1e-5
 STEPS = 4 * TAPS
 LAG = 2
-W_AHEAD = 6
+W_AHEAD = 5
 
 LOWER = [(4, 0, 32, 0), (36, 32, 30, 0)]
 UPPER = [(66, 0, 32, 1), (98, 32, 30, 1)]
@@ -33,8 +33,7 @@ def tile_revolutionnaive_kernel(tc, x, conv_w, bn_gamma, bn_beta, bn_mean, bn_va
         atp = ctx.enter_context(tc.tile_pool(name="atp", bufs=4))
         op = ctx.enter_context(tc.tile_pool(name="op", bufs=2))
         yp = ctx.enter_context(tc.psum_pool(name="yp", bufs=4))
-        accp = ctx.enter_context(tc.psum_pool(name="accp", bufs=3))
-        mp = ctx.enter_context(tc.psum_pool(name="mp", bufs=1))
+        pp = ctx.enter_context(tc.psum_pool(name="pp", bufs=4))
         ctx.enter_context(tc.manual_schedule())
 
         X = keep.tile([P, 2, 66, 64], BF16, name="X")
@@ -118,9 +117,9 @@ def tile_revolutionnaive_kernel(tc, x, conv_w, bn_gamma, bn_beta, bn_mean, bn_va
             nc.vector.tensor_max(out=MR[0:64, 0, :], in0=ta[0:64, 0:64], in1=ta[0:64, 64:128])
             nc.vector.tensor_max(out=MR[64:128, 1, :], in0=ta[64:128, 0:64], in1=ta[64:128, 64:128])
 
-        def select_rows(nt, half, pool):
+        def select_rows(nt, half):
             b, up = divmod(nt, 2)
-            ps = pool.tile([P, 512], F32, name="ps", tag="y" if pool is yp else "misc")
+            ps = pp.tile([P, 512], F32, name="ps", tag="pp")
             for al in range(8):
                 u = 2 * (8 * half + al) + up
                 nc.tensor.matmul(out=ps[:, al * 64:(al + 1) * 64], lhsT=band[:, 2 * u:2 * u + 128],
@@ -128,8 +127,8 @@ def tile_revolutionnaive_kernel(tc, x, conv_w, bn_gamma, bn_beta, bn_mean, bn_va
             nc.scalar.copy(out=M4[0:4, b, up, 8 * half:8 * half + 8, 1:65],
                            in_=ps[0:4, :].rearrange("p (a s) -> p a s", s=64))
 
-        def weights(k, pool):
-            wt = pool.tile([P, 512], F32, name="wt", tag="y" if pool is yp else "misc")
+        def weights(k):
+            wt = pp.tile([P, 512], F32, name="wt", tag="pp")
             for m in range(2):
                 words = Wsb[:, k, m * 512:(m + 1) * 512].bitcast(F32)
                 for e in range(2):
@@ -181,10 +180,11 @@ def tile_revolutionnaive_kernel(tc, x, conv_w, bn_gamma, bn_beta, bn_mean, bn_va
 
         def add_up(h, acc):
             k = h % TAPS
+            src = tbuf[min(k % 4, 2)]
             for m in range(2):
                 for blk in range(4):
                     nc.tensor.matmul(out=acc[m][:, blk * 128:(blk + 1) * 128],
-                                     lhsT=tbuf[k % 4][:, m, blk * 128:(blk + 1) * 128],
+                                     lhsT=src[:, m, blk * 128:(blk + 1) * 128],
                                      rhs=identF[:], is_transpose=True,
                                      start=(k == 0 and blk == 0), stop=(k == TAPS - 1 and blk == 3))
 
@@ -197,7 +197,7 @@ def tile_revolutionnaive_kernel(tc, x, conv_w, bn_gamma, bn_beta, bn_mean, bn_va
             return ats
 
         def turn_back(ats, o, ah, on_vector):
-            fb = mp.tile([P, 512], F32, name="fb", tag="misc")
+            fb = pp.tile([P, 512], F32, name="fb", tag="pp")
             for vp in range(2):
                 for m in range(2):
                     q = 2 * vp + m
@@ -231,17 +231,12 @@ def tile_revolutionnaive_kernel(tc, x, conv_w, bn_gamma, bn_beta, bn_mean, bn_va
             nc.gpsimd.dma_start(out=raw[q][66:128, :], in_=v2)
         nc.vector.memset(X[:, :, 0:66:65, :], 0.0)
 
-        load_x(nc.sync, 0, LOWER + [(0, 0, 4, 0)])
-        load_x(nc.scalar, 0, UPPER)
+        load_x(nc.sync, 0, LOWER + UPPER + [(0, 0, 4, 0)])
         nc.sync.dma_start(out=Wsb[0:4, :, :].rearrange("p k f -> p (k f)"),
                           in_=conv_w[0:128, :].rearrange("(p a) f -> p (a f)", p=4))
-        load_w(nc.sync, 0, LOWER)
-        load_w(nc.scalar, 0, UPPER)
-        load_w(nc.sync, 4, LOWER)
-        load_w(nc.scalar, 4, UPPER)
-        load_w(nc.sync, 8, LOWER)
-        load_w(nc.sync, 12, LOWER)
-        load_x(nc.sync, 1, LOWER + [(0, 0, 4, 0)])
+        for k0 in range(0, TAPS, 4):
+            load_w(nc.sync, k0, LOWER + UPPER)
+        load_x(nc.sync, 1, LOWER + UPPER + [(0, 0, 4, 0)])
 
         nc.vector.memset(band[:], 0.0)
         nc.vector.memset(MR[:], 0.0)
@@ -271,11 +266,9 @@ def tile_revolutionnaive_kernel(tc, x, conv_w, bn_gamma, bn_beta, bn_mean, bn_va
         chan_max()
         wgs = {}
         for k in range(4):
-            wgs[k] = weights(k, yp)
-        load_w(nc.scalar, 8, UPPER)
+            wgs[k] = weights(k)
         for half in range(2):
-            select_rows(0, half, yp)
-        load_w(nc.scalar, 12, UPPER)
+            select_rows(0, half)
         for vp in range(2):
             feat_g3(1, vp)
         for k in range(4):
@@ -284,8 +277,7 @@ def tile_revolutionnaive_kernel(tc, x, conv_w, bn_gamma, bn_beta, bn_mean, bn_va
             feat_x1(0, vp)
         feat_q(0)
         for k in range(4, W_AHEAD):
-            weights_q(k, weights(k, yp))
-        load_x(nc.scalar, 1, UPPER)
+            weights_q(k, weights(k))
 
         def later(nt):
             return ([lambda vp=vp: feat_g3(nt, vp) for vp in range(2)] + [lambda vp=vp: feat_g2(nt, vp) for vp in range(2)]
@@ -305,8 +297,9 @@ def tile_revolutionnaive_kernel(tc, x, conv_w, bn_gamma, bn_beta, bn_mean, bn_va
             g = h - LAG
             if 0 <= g < STEPS:
                 if g % TAPS == 0:
-                    accs[g // TAPS] = [accp.tile([P, 512], F32, name="acc") for m in range(2)]
-                add_up(g, accs[g // TAPS])
+                    accs[g // TAPS] = [pp.tile([P, 512], F32, name="acc", tag="pp") for m in range(2)]
+                if g % 4 != 2:
+                    add_up(g, accs[g // TAPS])
                 if g % TAPS == TAPS - 1:
                     done[g // TAPS] = (leave_psum(accs[g // TAPS]), op.tile([P, 1024], F32, name="o"))
             f = h - LAG - TAPS
@@ -316,11 +309,13 @@ def tile_revolutionnaive_kernel(tc, x, conv_w, bn_gamma, bn_beta, bn_mean, bn_va
                 if f % TAPS == 1:
                     store(f // TAPS, o)
             if h + W_AHEAD < TAPS:
-                wgs[h + W_AHEAD] = weights(h + W_AHEAD, mp)
+                wgs[h + W_AHEAD] = weights(h + W_AHEAD)
             if nt < 3 and k in (10, 11):
-                select_rows(nt + 1, k - 10, mp)
+                select_rows(nt + 1, k - 10)
             if h < STEPS:
                 mul(h, zs[h])
+                if h % 4 == 3:
+                    nc.vector.tensor_add(out=tbuf[2][:], in0=tbuf[2][:], in1=tbuf[3][:])
             if 1 <= h and h - 1 + W_AHEAD < TAPS:
                 weights_q(h - 1 + W_AHEAD, wgs[h - 1 + W_AHEAD])
             if nt < 3:

@@ -36,7 +36,8 @@ def tile_revolutionnaive_kernel(tc, x, conv_w, bn_gamma, bn_beta, bn_mean, bn_va
         pp = ctx.enter_context(tc.psum_pool(name="pp", bufs=4))
         ctx.enter_context(tc.manual_schedule())
 
-        X = keep.tile([P, 2, 66, 64], BF16, name="X")
+        X = keep.tile([P, 2, 68, 64], BF16, name="X")
+        XQ = keep.tile([P, 2, 4, 4, 17, 17], F32, name="XQ")
         XS = keep.tile([P, C * 64], BF16, name="XS")
         Wsb = keep.tile([P, TAPS, 1024], BF16, name="Wsb")
         E = keep.tile([P, 2, 33, 66], BF16, name="E")
@@ -77,12 +78,12 @@ def tile_revolutionnaive_kernel(tc, x, conv_w, bn_gamma, bn_beta, bn_mean, bn_va
 
         def feat_ft(b, v0, v1):
             nc.vector.tensor_max(out=FT[64:128, b, v0:v1, :],
-                                 in0=X[64:128, b, :, 2 * v0 - 1:2 * v1 - 2:2].rearrange("p r v -> p v r"),
-                                 in1=X[64:128, b, :, 2 * v0:2 * v1 - 1:2].rearrange("p r v -> p v r"))
+                                 in0=X[64:128, b, 0:66, 2 * v0 - 1:2 * v1 - 2:2].rearrange("p r v -> p v r"),
+                                 in1=X[64:128, b, 0:66, 2 * v0:2 * v1 - 1:2].rearrange("p r v -> p v r"))
 
         def feat_ftb(b):
             nc.vector.tensor_scalar_max(out=FT[64:128, b, 0:33:32, :],
-                                        in0=X[64:128, b, :, 0:64:63].rearrange("p r v -> p v r"), scalar1=0.0)
+                                        in0=X[64:128, b, 0:66, 0:64:63].rearrange("p r v -> p v r"), scalar1=0.0)
 
         def feat_g3(nt, vp):
             b, up = divmod(nt, 2)
@@ -127,6 +128,11 @@ def tile_revolutionnaive_kernel(tc, x, conv_w, bn_gamma, bn_beta, bn_mean, bn_va
             nc.scalar.copy(out=M4[0:4, b, up, 8 * half:8 * half + 8, 1:65],
                            in_=ps[0:4, :].rearrange("p (a s) -> p a s", s=64))
 
+        def patches(b, cc):
+            w0 = 1 if cc == 0 else 0
+            nc.scalar.copy(out=XQ[:, b, :, cc, :, w0:w0 + 16],
+                           in_=X[:, b, :, :].rearrange("p (a rr) (w c) -> p c rr a w", rr=4, c=4)[:, (cc + 3) % 4])
+
         def weights(k):
             wt = pp.tile([P, 512], F32, name="wt", tag="pp")
             for m in range(2):
@@ -167,20 +173,18 @@ def tile_revolutionnaive_kernel(tc, x, conv_w, bn_gamma, bn_beta, bn_mean, bn_va
             nt, k = divmod(h, TAPS)
             b, up = divmod(nt, 2)
             i, j = divmod(k, 4)
+            a0, rr = divmod(2 * up + i, 4)
             for vp in range(2):
-                w0 = 1 if (j == 0 and vp == 0) else 0
-                w1 = 15 if (j == 3 and vp == 1) else 16
-                r0 = 2 * up + i
-                c0 = 2 * vp + j - 1
-                patch = X[:, b, r0:r0 + 61:4, c0 + 4 * w0:c0 + 4 * (w1 - 1) + 1:4]
+                w0, cc = divmod(2 * vp + j, 4)
+                patch = XQ[:, b, rr, cc, a0:a0 + 16, w0:w0 + 16]
                 nc.vector.tensor_mul(
-                    out=tbuf[j][:, :, vp * 256:(vp + 1) * 256].rearrange("p m (a w) -> p m a w", w=16)[:, :, :, w0:w1],
-                    in0=z[:, :, vp * 256:(vp + 1) * 256].rearrange("p m (a w) -> p m a w", w=16)[:, :, :, w0:w1],
-                    in1=patch.unsqueeze(1).to_broadcast([P, 2, 16, w1 - w0]))
+                    out=tbuf[j][:, :, vp * 256:(vp + 1) * 256].rearrange("p m (a w) -> p m a w", w=16),
+                    in0=z[:, :, vp * 256:(vp + 1) * 256].rearrange("p m (a w) -> p m a w", w=16),
+                    in1=patch.unsqueeze(1).to_broadcast([P, 2, 16, 16]))
 
         def add_up(h, acc):
             k = h % TAPS
-            src = tbuf[min(k % 4, 2)]
+            src = tbuf[k % 4]
             for m in range(2):
                 for blk in range(4):
                     nc.tensor.matmul(out=acc[m][:, blk * 128:(blk + 1) * 128],
@@ -229,7 +233,9 @@ def tile_revolutionnaive_kernel(tc, x, conv_w, bn_gamma, bn_beta, bn_mean, bn_va
             v2 = vec.rearrange("(c q) -> c q", q=64)
             nc.gpsimd.dma_start(out=raw[q][4:66, :], in_=v2)
             nc.gpsimd.dma_start(out=raw[q][66:128, :], in_=v2)
-        nc.vector.memset(X[:, :, 0:66:65, :], 0.0)
+        nc.vector.memset(X[:, :, 0, :], 0.0)
+        nc.vector.memset(X[:, :, 65:68, :], 0.0)
+        nc.vector.memset(XQ[:, 0], 0.0)
 
         load_x(nc.sync, 0, LOWER + UPPER + [(0, 0, 4, 0)])
         nc.sync.dma_start(out=Wsb[0:4, :, :].rearrange("p k f -> p (k f)"),
@@ -242,8 +248,6 @@ def tile_revolutionnaive_kernel(tc, x, conv_w, bn_gamma, bn_beta, bn_mean, bn_va
         nc.vector.memset(MR[:], 0.0)
         nc.vector.memset(E[:, :, :, 0:66:65], 0.0)
         nc.vector.memset(M4[0:4, :, :, :, 0:66:65], 0.0)
-        nc.vector.memset(tbuf[0][:, :, 0:256].rearrange("p m (a w) -> p m a w", w=16)[:, :, :, 0:1], 0.0)
-        nc.vector.memset(tbuf[3][:, :, 256:512].rearrange("p m (a w) -> p m a w", w=16)[:, :, :, 15:16], 0.0)
         nc.vector.tensor_tensor(out=band[:, 1:65], in0=identB[:, 0:64], in1=identB[:, 64:128], op=ALU.add)
 
         feat_e(0, 0, 33)
@@ -251,6 +255,8 @@ def tile_revolutionnaive_kernel(tc, x, conv_w, bn_gamma, bn_beta, bn_mean, bn_va
         feat_ftb(0)
         nc.vector.tensor_scalar_add(out=vv[:], in0=raw[0][:], scalar1=BN_EPS)
         nc.scalar.sqrt(out=vv[:], in_=vv[:])
+        for cc in range(4):
+            patches(0, cc)
         for vp in range(2):
             feat_g3(0, vp)
         for vp in range(2):
@@ -263,6 +269,7 @@ def tile_revolutionnaive_kernel(tc, x, conv_w, bn_gamma, bn_beta, bn_mean, bn_va
             fv = full[:].rearrange("p (k n m) -> p k n m", k=TAPS, n=2, m=2)
             nc.vector.tensor_copy(out=tab[64:128], in_=fv[64:128, :, 1, :])
             nc.vector.tensor_copy(out=tab[0:66], in_=fv[0:66, :, 0, :])
+        nc.vector.memset(XQ[:, 1], 0.0)
         chan_max()
         wgs = {}
         for k in range(4):
@@ -298,8 +305,7 @@ def tile_revolutionnaive_kernel(tc, x, conv_w, bn_gamma, bn_beta, bn_mean, bn_va
             if 0 <= g < STEPS:
                 if g % TAPS == 0:
                     accs[g // TAPS] = [pp.tile([P, 512], F32, name="acc", tag="pp") for m in range(2)]
-                if g % 4 != 2:
-                    add_up(g, accs[g // TAPS])
+                add_up(g, accs[g // TAPS])
                 if g % TAPS == TAPS - 1:
                     done[g // TAPS] = (leave_psum(accs[g // TAPS]), op.tile([P, 1024], F32, name="o"))
             f = h - LAG - TAPS
@@ -310,12 +316,12 @@ def tile_revolutionnaive_kernel(tc, x, conv_w, bn_gamma, bn_beta, bn_mean, bn_va
                     store(f // TAPS, o)
             if h + W_AHEAD < TAPS:
                 wgs[h + W_AHEAD] = weights(h + W_AHEAD)
+            if nt == 1 and k < 4:
+                patches(1, k)
             if nt < 3 and k in (10, 11):
                 select_rows(nt + 1, k - 10)
             if h < STEPS:
                 mul(h, zs[h])
-                if h % 4 == 3:
-                    nc.vector.tensor_add(out=tbuf[2][:], in0=tbuf[2][:], in1=tbuf[3][:])
             if 1 <= h and h - 1 + W_AHEAD < TAPS:
                 weights_q(h - 1 + W_AHEAD, wgs[h - 1 + W_AHEAD])
             if nt < 3:

@@ -17,7 +17,8 @@ TAPS = 16
 FLOPS = 2 * 3968 * 512 * 2048
 BN_EPS = 1e-5
 STEPS = 4 * TAPS
-LAG = 2
+LAG = 3
+RING = 8
 W_AHEAD = 5
 
 LOWER = [(4, 0, 32, 0), (36, 32, 30, 0)]
@@ -28,7 +29,7 @@ def tile_revolutionnaive_kernel(tc, x, conv_w, bn_gamma, bn_beta, bn_mean, bn_va
     nc = tc.nc
     with ExitStack() as ctx:
         keep = ctx.enter_context(tc.tile_pool(name="keep", bufs=1))
-        wgp = ctx.enter_context(tc.tile_pool(name="wgp", bufs=3))
+        wgp = ctx.enter_context(tc.tile_pool(name="wgp", bufs=W_AHEAD + 1))
         zp = ctx.enter_context(tc.tile_pool(name="zp", bufs=3))
         atp = ctx.enter_context(tc.tile_pool(name="atp", bufs=4))
         op = ctx.enter_context(tc.tile_pool(name="op", bufs=2))
@@ -36,8 +37,7 @@ def tile_revolutionnaive_kernel(tc, x, conv_w, bn_gamma, bn_beta, bn_mean, bn_va
         pp = ctx.enter_context(tc.psum_pool(name="pp", bufs=4))
         ctx.enter_context(tc.manual_schedule())
 
-        X = keep.tile([P, 2, 68, 64], BF16, name="X")
-        XQ = keep.tile([P, 2, 4, 4, 17, 17], F32, name="XQ")
+        X = keep.tile([P, 2, 66, 64], BF16, name="X")
         XS = keep.tile([P, C * 64], BF16, name="XS")
         Wsb = keep.tile([P, TAPS, 1024], BF16, name="Wsb")
         E = keep.tile([P, 2, 33, 66], BF16, name="E")
@@ -48,7 +48,7 @@ def tile_revolutionnaive_kernel(tc, x, conv_w, bn_gamma, bn_beta, bn_mean, bn_va
         FS = keep.tile([P, 2048], U8, name="FS", align_bytes=64)
         WC = keep.tile([P, 4096], U32, name="WC", align_bytes=64)
         WS = keep.tile([P, 4096], U8, name="WS", align_bytes=64)
-        tbuf = [keep.tile([P, 2, 512], F32, name="t%d" % j) for j in range(4)]
+        tbuf = [keep.tile([P, 2, 512], F32, name="t%d" % j) for j in range(RING)]
         identF = keep.tile([P, P], F32, name="identF")
         identB = keep.tile([P, P], BF16, name="identB")
         band = keep.tile([P, 192], BF16, name="band")
@@ -78,12 +78,12 @@ def tile_revolutionnaive_kernel(tc, x, conv_w, bn_gamma, bn_beta, bn_mean, bn_va
 
         def feat_ft(b, v0, v1):
             nc.vector.tensor_max(out=FT[64:128, b, v0:v1, :],
-                                 in0=X[64:128, b, 0:66, 2 * v0 - 1:2 * v1 - 2:2].rearrange("p r v -> p v r"),
-                                 in1=X[64:128, b, 0:66, 2 * v0:2 * v1 - 1:2].rearrange("p r v -> p v r"))
+                                 in0=X[64:128, b, :, 2 * v0 - 1:2 * v1 - 2:2].rearrange("p r v -> p v r"),
+                                 in1=X[64:128, b, :, 2 * v0:2 * v1 - 1:2].rearrange("p r v -> p v r"))
 
         def feat_ftb(b):
             nc.vector.tensor_scalar_max(out=FT[64:128, b, 0:33:32, :],
-                                        in0=X[64:128, b, 0:66, 0:64:63].rearrange("p r v -> p v r"), scalar1=0.0)
+                                        in0=X[64:128, b, :, 0:64:63].rearrange("p r v -> p v r"), scalar1=0.0)
 
         def feat_g3(nt, vp):
             b, up = divmod(nt, 2)
@@ -128,11 +128,6 @@ def tile_revolutionnaive_kernel(tc, x, conv_w, bn_gamma, bn_beta, bn_mean, bn_va
             nc.scalar.copy(out=M4[0:4, b, up, 8 * half:8 * half + 8, 1:65],
                            in_=ps[0:4, :].rearrange("p (a s) -> p a s", s=64))
 
-        def patches(b, cc):
-            w0 = 1 if cc == 0 else 0
-            nc.scalar.copy(out=XQ[:, b, :, cc, :, w0:w0 + 16],
-                           in_=X[:, b, :, :].rearrange("p (a rr) (w c) -> p c rr a w", rr=4, c=4)[:, (cc + 3) % 4])
-
         def weights(k):
             wt = pp.tile([P, 512], F32, name="wt", tag="pp")
             for m in range(2):
@@ -173,18 +168,20 @@ def tile_revolutionnaive_kernel(tc, x, conv_w, bn_gamma, bn_beta, bn_mean, bn_va
             nt, k = divmod(h, TAPS)
             b, up = divmod(nt, 2)
             i, j = divmod(k, 4)
-            a0, rr = divmod(2 * up + i, 4)
             for vp in range(2):
-                w0, cc = divmod(2 * vp + j, 4)
-                patch = XQ[:, b, rr, cc, a0:a0 + 16, w0:w0 + 16]
+                w0 = 1 if (j == 0 and vp == 0) else 0
+                w1 = 15 if (j == 3 and vp == 1) else 16
+                r0 = 2 * up + i
+                c0 = 2 * vp + j - 1
+                patch = X[:, b, r0:r0 + 61:4, c0 + 4 * w0:c0 + 4 * (w1 - 1) + 1:4]
                 nc.vector.tensor_mul(
-                    out=tbuf[j][:, :, vp * 256:(vp + 1) * 256].rearrange("p m (a w) -> p m a w", w=16),
-                    in0=z[:, :, vp * 256:(vp + 1) * 256].rearrange("p m (a w) -> p m a w", w=16),
-                    in1=patch.unsqueeze(1).to_broadcast([P, 2, 16, 16]))
+                    out=tbuf[k % RING][:, :, vp * 256:(vp + 1) * 256].rearrange("p m (a w) -> p m a w", w=16)[:, :, :, w0:w1],
+                    in0=z[:, :, vp * 256:(vp + 1) * 256].rearrange("p m (a w) -> p m a w", w=16)[:, :, :, w0:w1],
+                    in1=patch.unsqueeze(1).to_broadcast([P, 2, 16, w1 - w0]))
 
         def add_up(h, acc):
             k = h % TAPS
-            src = tbuf[k % 4]
+            src = tbuf[k % RING - (1 if k % RING == RING - 1 else 0)]
             for m in range(2):
                 for blk in range(4):
                     nc.tensor.matmul(out=acc[m][:, blk * 128:(blk + 1) * 128],
@@ -223,7 +220,7 @@ def tile_revolutionnaive_kernel(tc, x, conv_w, bn_gamma, bn_beta, bn_mean, bn_va
                     in_=o[p0:p0 + cn, :].rearrange("p (a s) -> p a s", s=64))
 
         for b in range(2):
-            nc.gpsimd.dma_start(out=XS[64 * b:64 * b + 64, :].rearrange("r (c s) -> r c s", s=64),
+            nc.scalar.dma_start(out=XS[64 * b:64 * b + 64, :].rearrange("r (c s) -> r c s", s=64),
                                 in_=x[b].rearrange("c r s -> r c s"))
         make_identity(nc, identF[:])
         make_identity(nc, identB[:])
@@ -231,11 +228,9 @@ def tile_revolutionnaive_kernel(tc, x, conv_w, bn_gamma, bn_beta, bn_mean, bn_va
             nc.vector.memset(raw[q][:], 0.0)
         for q, vec in enumerate((bn_var, bn_gamma, bn_mean, bn_beta)):
             v2 = vec.rearrange("(c q) -> c q", q=64)
-            nc.gpsimd.dma_start(out=raw[q][4:66, :], in_=v2)
-            nc.gpsimd.dma_start(out=raw[q][66:128, :], in_=v2)
-        nc.vector.memset(X[:, :, 0, :], 0.0)
-        nc.vector.memset(X[:, :, 65:68, :], 0.0)
-        nc.vector.memset(XQ[:, 0], 0.0)
+            nc.scalar.dma_start(out=raw[q][4:66, :], in_=v2)
+            nc.scalar.dma_start(out=raw[q][66:128, :], in_=v2)
+        nc.vector.memset(X[:, :, 0:66:65, :], 0.0)
 
         load_x(nc.sync, 0, LOWER + UPPER + [(0, 0, 4, 0)])
         nc.sync.dma_start(out=Wsb[0:4, :, :].rearrange("p k f -> p (k f)"),
@@ -248,19 +243,32 @@ def tile_revolutionnaive_kernel(tc, x, conv_w, bn_gamma, bn_beta, bn_mean, bn_va
         nc.vector.memset(MR[:], 0.0)
         nc.vector.memset(E[:, :, :, 0:66:65], 0.0)
         nc.vector.memset(M4[0:4, :, :, :, 0:66:65], 0.0)
+        for j in range(0, RING, 4):
+            nc.vector.memset(tbuf[j][:, :, 0:256].rearrange("p m (a w) -> p m a w", w=16)[:, :, :, 0:1], 0.0)
+            nc.vector.memset(tbuf[j + 3][:, :, 256:512].rearrange("p m (a w) -> p m a w", w=16)[:, :, :, 15:16], 0.0)
         nc.vector.tensor_tensor(out=band[:, 1:65], in0=identB[:, 0:64], in1=identB[:, 64:128], op=ALU.add)
 
+        nc.vector.tensor_scalar_add(out=vv[:], in0=raw[0][:], scalar1=BN_EPS)
+        nc.scalar.sqrt(out=vv[:], in_=vv[:])
         feat_e(0, 0, 33)
         feat_ft(0, 1, 32)
         feat_ftb(0)
-        nc.vector.tensor_scalar_add(out=vv[:], in0=raw[0][:], scalar1=BN_EPS)
-        nc.scalar.sqrt(out=vv[:], in_=vv[:])
-        for cc in range(4):
-            patches(0, cc)
+        chan_max()
+        wgs = {}
+        for k in range(2):
+            wgs[k] = weights(k)
+        for half in range(2):
+            select_rows(0, half)
+        for k in range(2, W_AHEAD):
+            wgs[k] = weights(k)
         for vp in range(2):
             feat_g3(0, vp)
         for vp in range(2):
             feat_g2(0, vp)
+        for vp in range(2):
+            feat_x1(0, vp)
+        feat_q(0)
+        weights_q(0, wgs[0])
         nc.vector.reciprocal(out=vv[:], in_=vv[:])
         nc.vector.tensor_mul(out=sfull[:], in0=raw[1][:], in1=vv[:])
         nc.vector.tensor_mul(out=bfull[:], in0=raw[2][:], in1=sfull[:])
@@ -269,22 +277,8 @@ def tile_revolutionnaive_kernel(tc, x, conv_w, bn_gamma, bn_beta, bn_mean, bn_va
             fv = full[:].rearrange("p (k n m) -> p k n m", k=TAPS, n=2, m=2)
             nc.vector.tensor_copy(out=tab[64:128], in_=fv[64:128, :, 1, :])
             nc.vector.tensor_copy(out=tab[0:66], in_=fv[0:66, :, 0, :])
-        nc.vector.memset(XQ[:, 1], 0.0)
-        chan_max()
-        wgs = {}
-        for k in range(4):
-            wgs[k] = weights(k)
-        for half in range(2):
-            select_rows(0, half)
-        for vp in range(2):
-            feat_g3(1, vp)
-        for k in range(4):
+        for k in range(1, W_AHEAD):
             weights_q(k, wgs[k])
-        for vp in range(2):
-            feat_x1(0, vp)
-        feat_q(0)
-        for k in range(4, W_AHEAD):
-            weights_q(k, weights(k))
 
         def later(nt):
             return ([lambda vp=vp: feat_g3(nt, vp) for vp in range(2)] + [lambda vp=vp: feat_g2(nt, vp) for vp in range(2)]
@@ -292,7 +286,7 @@ def tile_revolutionnaive_kernel(tc, x, conv_w, bn_gamma, bn_beta, bn_mean, bn_va
 
         batch1 = ([lambda u=u: feat_e(1, u, u + 11) for u in (0, 11, 22)]
                   + [lambda: feat_ft(1, 1, 11), lambda: feat_ft(1, 11, 21), lambda: (feat_ft(1, 21, 32), feat_ftb(1))])
-        side = {1: later(1)[2:], 2: batch1 + later(2), 3: later(3)}
+        side = {1: later(1), 2: batch1 + later(2), 3: later(3)}
 
         zs = {}
         accs = {}
@@ -305,7 +299,8 @@ def tile_revolutionnaive_kernel(tc, x, conv_w, bn_gamma, bn_beta, bn_mean, bn_va
             if 0 <= g < STEPS:
                 if g % TAPS == 0:
                     accs[g // TAPS] = [pp.tile([P, 512], F32, name="acc", tag="pp") for m in range(2)]
-                add_up(g, accs[g // TAPS])
+                if g % RING != RING - 2:
+                    add_up(g, accs[g // TAPS])
                 if g % TAPS == TAPS - 1:
                     done[g // TAPS] = (leave_psum(accs[g // TAPS]), op.tile([P, 1024], F32, name="o"))
             f = h - LAG - TAPS
@@ -316,12 +311,12 @@ def tile_revolutionnaive_kernel(tc, x, conv_w, bn_gamma, bn_beta, bn_mean, bn_va
                     store(f // TAPS, o)
             if h + W_AHEAD < TAPS:
                 wgs[h + W_AHEAD] = weights(h + W_AHEAD)
-            if nt == 1 and k < 4:
-                patches(1, k)
             if nt < 3 and k in (10, 11):
                 select_rows(nt + 1, k - 10)
             if h < STEPS:
                 mul(h, zs[h])
+                if h % RING == RING - 1:
+                    nc.vector.tensor_add(out=tbuf[RING - 2][:], in0=tbuf[RING - 2][:], in1=tbuf[RING - 1][:])
             if 1 <= h and h - 1 + W_AHEAD < TAPS:
                 weights_q(h - 1 + W_AHEAD, wgs[h - 1 + W_AHEAD])
             if nt < 3:

@@ -181,7 +181,7 @@ def tile_revolutionnaive_kernel(tc, x, conv_w, bn_gamma, bn_beta, bn_mean, bn_va
 
         def add_up(h, acc):
             k = h % TAPS
-            src = tbuf[k % RING - (1 if k % RING == RING - 1 else 0)]
+            src = tbuf[k % RING]
             for m in range(2):
                 for blk in range(4):
                     nc.tensor.matmul(out=acc[m][:, blk * 128:(blk + 1) * 128],
@@ -219,11 +219,11 @@ def tile_revolutionnaive_kernel(tc, x, conv_w, bn_gamma, bn_beta, bn_mean, bn_va
                     out=out[b, c0:c0 + cn].rearrange("c (a r) s -> c a r s", r=4)[:, :, 2 * up + n, :],
                     in_=o[p0:p0 + cn, :].rearrange("p (a s) -> p a s", s=64))
 
-        for b in range(2):
-            nc.scalar.dma_start(out=XS[64 * b:64 * b + 64, :].rearrange("r (c s) -> r c s", s=64),
-                                in_=x[b].rearrange("c r s -> r c s"))
         make_identity(nc, identF[:])
         make_identity(nc, identB[:])
+        for b, queue in enumerate((nc.scalar, nc.gpsimd)):
+            queue.dma_start(out=XS[64 * b:64 * b + 64, :].rearrange("r (c s) -> r c s", s=64),
+                            in_=x[b].rearrange("c r s -> r c s"))
         for q in range(4):
             nc.vector.memset(raw[q][:], 0.0)
         for q, vec in enumerate((bn_var, bn_gamma, bn_mean, bn_beta)):
@@ -253,6 +253,10 @@ def tile_revolutionnaive_kernel(tc, x, conv_w, bn_gamma, bn_beta, bn_mean, bn_va
         feat_e(0, 0, 33)
         feat_ft(0, 1, 32)
         feat_ftb(0)
+        for vp in range(2):
+            feat_g3(0, vp)
+        for vp in range(2):
+            feat_g2(0, vp)
         chan_max()
         wgs = {}
         for k in range(2):
@@ -262,9 +266,9 @@ def tile_revolutionnaive_kernel(tc, x, conv_w, bn_gamma, bn_beta, bn_mean, bn_va
         for k in range(2, W_AHEAD):
             wgs[k] = weights(k)
         for vp in range(2):
-            feat_g3(0, vp)
+            feat_g3(1, vp)
         for vp in range(2):
-            feat_g2(0, vp)
+            feat_g2(1, vp)
         for vp in range(2):
             feat_x1(0, vp)
         feat_q(0)
@@ -286,7 +290,7 @@ def tile_revolutionnaive_kernel(tc, x, conv_w, bn_gamma, bn_beta, bn_mean, bn_va
 
         batch1 = ([lambda u=u: feat_e(1, u, u + 11) for u in (0, 11, 22)]
                   + [lambda: feat_ft(1, 1, 11), lambda: feat_ft(1, 11, 21), lambda: (feat_ft(1, 21, 32), feat_ftb(1))])
-        side = {1: later(1), 2: batch1 + later(2), 3: later(3)}
+        side = {1: later(1)[4:], 2: batch1 + later(2), 3: later(3)}
 
         zs = {}
         accs = {}
@@ -299,8 +303,7 @@ def tile_revolutionnaive_kernel(tc, x, conv_w, bn_gamma, bn_beta, bn_mean, bn_va
             if 0 <= g < STEPS:
                 if g % TAPS == 0:
                     accs[g // TAPS] = [pp.tile([P, 512], F32, name="acc", tag="pp") for m in range(2)]
-                if g % RING != RING - 2:
-                    add_up(g, accs[g // TAPS])
+                add_up(g, accs[g // TAPS])
                 if g % TAPS == TAPS - 1:
                     done[g // TAPS] = (leave_psum(accs[g // TAPS]), op.tile([P, 1024], F32, name="o"))
             f = h - LAG - TAPS
@@ -315,8 +318,6 @@ def tile_revolutionnaive_kernel(tc, x, conv_w, bn_gamma, bn_beta, bn_mean, bn_va
                 select_rows(nt + 1, k - 10)
             if h < STEPS:
                 mul(h, zs[h])
-                if h % RING == RING - 1:
-                    nc.vector.tensor_add(out=tbuf[RING - 2][:], in0=tbuf[RING - 2][:], in1=tbuf[RING - 1][:])
             if 1 <= h and h - 1 + W_AHEAD < TAPS:
                 weights_q(h - 1 + W_AHEAD, wgs[h - 1 + W_AHEAD])
             if nt < 3:

@@ -42,7 +42,6 @@ def tile_revolutionnaive_kernel(tc, x, conv_w, bn_gamma, bn_beta, bn_mean, bn_va
         Wsb = keep.tile([P, TAPS, 1024], BF16, name="Wsb")
         E = keep.tile([P, 2, 33, 66], BF16, name="E")
         FT = keep.tile([P, 2, 33, 66], BF16, name="FT")
-        M4 = keep.tile([P, 2, 2, 16, 66], BF16, name="M4")
         G = keep.tile([P, 4, 2048], BF16, name="G", align_bytes=64)
         FC = keep.tile([P, 2048], U32, name="FC", align_bytes=64)
         FS = keep.tile([P, 2048], U8, name="FS", align_bytes=64)
@@ -50,9 +49,8 @@ def tile_revolutionnaive_kernel(tc, x, conv_w, bn_gamma, bn_beta, bn_mean, bn_va
         WS = keep.tile([P, 4096], U8, name="WS", align_bytes=64)
         tbuf = [keep.tile([P, 2, 512], F32, name="t%d" % j) for j in range(RING)]
         identF = keep.tile([P, P], F32, name="identF")
-        identB = keep.tile([P, P], BF16, name="identB")
-        band = keep.tile([P, 192], BF16, name="band")
-        MR = keep.tile([P, 2, 64], BF16, name="MR")
+        MR = keep.tile([P, 66], BF16, name="MR")
+        zrow = keep.tile([P, 128], BF16, name="zrow")
         raw = [keep.tile([P, 64], BF16, name="raw%d" % q) for q in range(4)]
         Stab = keep.tile([P, TAPS, 2], F32, name="Stab")
         Btab = keep.tile([P, TAPS, 2], F32, name="Btab")
@@ -99,11 +97,18 @@ def tile_revolutionnaive_kernel(tc, x, conv_w, bn_gamma, bn_beta, bn_mean, bn_va
                 in0=E[0:66, b, up:up + 31:2, 2 * vp:2 * vp + 64],
                 in1=E[0:66, b, up + 1:up + 32:2, 2 * vp:2 * vp + 64])
 
-        def feat_x1(nt, vp):
+        def feat_x1(nt):
             b, up = divmod(nt, 2)
-            nc.vector.tensor_copy(
-                out=G[0:4, nt, vp * 1024:(vp + 1) * 1024].rearrange("p (a s) -> p a s", a=16, s=64),
-                in_=M4[0:4, b, up, :, 2 * vp:2 * vp + 64])
+            for i in range(4):
+                a0 = 1 if (up == 0 and i == 0) else 0
+                a1 = 15 if (up == 1 and i == 3) else 16
+                r0 = 64 * b + 4 * a0 + 2 * up + i - 1
+                for vp in range(2):
+                    nc.sync.dma_start(out=G[i:i + 1, nt, vp * 1024 + a0 * 64:vp * 1024 + a1 * 64],
+                                      in_=MR[r0:r0 + 4 * (a1 - a0 - 1) + 1:4, 2 * vp:2 * vp + 64])
+            i, a = (0, 0) if up == 0 else (3, 15)
+            nc.sync.dma_start(out=G[i:i + 1, nt, :].rearrange("p (v r) -> p v r", v=2)[:, :, a * 64:(a + 1) * 64],
+                              in_=zrow[i:i + 1, :].rearrange("p (v s) -> p v s", v=2))
 
         def feat_q(nt):
             nc.vector.quantize_mx(out=FC[:, nt * 512:(nt + 1) * 512].bitcast(FP8X4),
@@ -115,18 +120,7 @@ def tile_revolutionnaive_kernel(tc, x, conv_w, bn_gamma, bn_beta, bn_mean, bn_va
             nc.vector.tensor_max(out=ta[:, 0:512], in0=tb[:, 0:512], in1=tb[:, 512:1024])
             nc.vector.tensor_max(out=tb[:, 0:256], in0=ta[:, 0:256], in1=ta[:, 256:512])
             nc.vector.tensor_max(out=ta[:, 0:128], in0=tb[:, 0:128], in1=tb[:, 128:256])
-            nc.vector.tensor_max(out=MR[0:64, 0, :], in0=ta[0:64, 0:64], in1=ta[0:64, 64:128])
-            nc.vector.tensor_max(out=MR[64:128, 1, :], in0=ta[64:128, 0:64], in1=ta[64:128, 64:128])
-
-        def select_rows(nt, half):
-            b, up = divmod(nt, 2)
-            ps = pp.tile([P, 512], F32, name="ps", tag="pp")
-            for al in range(8):
-                u = 2 * (8 * half + al) + up
-                nc.tensor.matmul(out=ps[:, al * 64:(al + 1) * 64], lhsT=band[:, 2 * u:2 * u + 128],
-                                 rhs=MR[:, b, :], start=True, stop=True)
-            nc.scalar.copy(out=M4[0:4, b, up, 8 * half:8 * half + 8, 1:65],
-                           in_=ps[0:4, :].rearrange("p (a s) -> p a s", s=64))
+            nc.vector.tensor_max(out=MR[:, 1:65], in0=ta[:, 0:64], in1=ta[:, 64:128])
 
         def weights(k):
             wt = pp.tile([P, 512], F32, name="wt", tag="pp")
@@ -220,7 +214,6 @@ def tile_revolutionnaive_kernel(tc, x, conv_w, bn_gamma, bn_beta, bn_mean, bn_va
                     in_=o[p0:p0 + cn, :].rearrange("p (a s) -> p a s", s=64))
 
         make_identity(nc, identF[:])
-        make_identity(nc, identB[:])
         for b, queue in enumerate((nc.scalar, nc.gpsimd)):
             queue.dma_start(out=XS[64 * b:64 * b + 64, :].rearrange("r (c s) -> r c s", s=64),
                             in_=x[b].rearrange("c r s -> r c s"))
@@ -235,18 +228,15 @@ def tile_revolutionnaive_kernel(tc, x, conv_w, bn_gamma, bn_beta, bn_mean, bn_va
         load_x(nc.sync, 0, LOWER + UPPER + [(0, 0, 4, 0)])
         nc.sync.dma_start(out=Wsb[0:4, :, :].rearrange("p k f -> p (k f)"),
                           in_=conv_w[0:128, :].rearrange("(p a) f -> p (a f)", p=4))
-        for k0 in range(0, TAPS, 4):
+        for k0 in (0, 4):
             load_w(nc.sync, k0, LOWER + UPPER)
-        load_x(nc.sync, 1, LOWER + UPPER + [(0, 0, 4, 0)])
 
-        nc.vector.memset(band[:], 0.0)
         nc.vector.memset(MR[:], 0.0)
+        nc.vector.memset(zrow[:], 0.0)
         nc.vector.memset(E[:, :, :, 0:66:65], 0.0)
-        nc.vector.memset(M4[0:4, :, :, :, 0:66:65], 0.0)
         for j in range(0, RING, 4):
             nc.vector.memset(tbuf[j][:, :, 0:256].rearrange("p m (a w) -> p m a w", w=16)[:, :, :, 0:1], 0.0)
             nc.vector.memset(tbuf[j + 3][:, :, 256:512].rearrange("p m (a w) -> p m a w", w=16)[:, :, :, 15:16], 0.0)
-        nc.vector.tensor_tensor(out=band[:, 1:65], in0=identB[:, 0:64], in1=identB[:, 64:128], op=ALU.add)
 
         nc.vector.tensor_scalar_add(out=vv[:], in0=raw[0][:], scalar1=BN_EPS)
         nc.scalar.sqrt(out=vv[:], in_=vv[:])
@@ -258,19 +248,18 @@ def tile_revolutionnaive_kernel(tc, x, conv_w, bn_gamma, bn_beta, bn_mean, bn_va
         for vp in range(2):
             feat_g2(0, vp)
         chan_max()
+        feat_x1(0)
+        for k0 in (8, 12):
+            load_w(nc.sync, k0, LOWER + UPPER)
+        load_x(nc.sync, 1, LOWER + UPPER + [(0, 0, 4, 0)])
         wgs = {}
-        for k in range(2):
-            wgs[k] = weights(k)
-        for half in range(2):
-            select_rows(0, half)
-        for k in range(2, W_AHEAD):
+        for k in range(W_AHEAD):
             wgs[k] = weights(k)
         for vp in range(2):
             feat_g3(1, vp)
         for vp in range(2):
             feat_g2(1, vp)
-        for vp in range(2):
-            feat_x1(0, vp)
+        feat_x1(1)
         feat_q(0)
         weights_q(0, wgs[0])
         nc.vector.reciprocal(out=vv[:], in_=vv[:])
@@ -285,12 +274,12 @@ def tile_revolutionnaive_kernel(tc, x, conv_w, bn_gamma, bn_beta, bn_mean, bn_va
             weights_q(k, wgs[k])
 
         def later(nt):
-            return ([lambda vp=vp: feat_g3(nt, vp) for vp in range(2)] + [lambda vp=vp: feat_g2(nt, vp) for vp in range(2)]
-                    + [lambda vp=vp: feat_x1(nt, vp) for vp in range(2)] + [lambda: feat_q(nt)])
+            return ([lambda vp=vp: feat_g3(nt, vp) for vp in range(2)] + [lambda: feat_g2(nt, 0), lambda: (feat_g2(nt, 1), feat_x1(nt))]
+                    + [lambda: None, lambda: None, lambda: feat_q(nt)])
 
         batch1 = ([lambda u=u: feat_e(1, u, u + 11) for u in (0, 11, 22)]
                   + [lambda: feat_ft(1, 1, 11), lambda: feat_ft(1, 11, 21), lambda: (feat_ft(1, 21, 32), feat_ftb(1))])
-        side = {1: later(1)[4:], 2: batch1 + later(2), 3: later(3)}
+        side = {1: later(1)[6:], 2: batch1 + later(2), 3: later(3)}
 
         zs = {}
         accs = {}
@@ -314,8 +303,6 @@ def tile_revolutionnaive_kernel(tc, x, conv_w, bn_gamma, bn_beta, bn_mean, bn_va
                     store(f // TAPS, o)
             if h + W_AHEAD < TAPS:
                 wgs[h + W_AHEAD] = weights(h + W_AHEAD)
-            if nt < 3 and k in (10, 11):
-                select_rows(nt + 1, k - 10)
             if h < STEPS:
                 mul(h, zs[h])
             if 1 <= h and h - 1 + W_AHEAD < TAPS:

@@ -154,7 +154,8 @@ def tile_revolutionnaive_kernel(tc, x, conv_w, bn_gamma, bn_beta, bn_mean, bn_va
                                     start=True, stop=True)
                 ys.append(y)
             for m in range(2):
-                nc.scalar.activation(out=z[:, m, :], in_=ys[m][:], func=ACT.Relu,
+                nc.scalar.activation(out=z[:, m, :].rearrange("p (r vp) -> p r vp", vp=2),
+                                     in_=ys[m][:].rearrange("p (vp r) -> p r vp", vp=2), func=ACT.Relu,
                                      bias=Btab[:, k, m:m + 1], scale=Stab[:, k, m:m + 1])
             return z
 
@@ -162,16 +163,15 @@ def tile_revolutionnaive_kernel(tc, x, conv_w, bn_gamma, bn_beta, bn_mean, bn_va
             nt, k = divmod(h, TAPS)
             b, up = divmod(nt, 2)
             i, j = divmod(k, 4)
-            for vp in range(2):
-                w0 = 1 if (j == 0 and vp == 0) else 0
-                w1 = 15 if (j == 3 and vp == 1) else 16
-                r0 = 2 * up + i
-                c0 = 2 * vp + j - 1
-                patch = X[:, b, r0:r0 + 61:4, c0 + 4 * w0:c0 + 4 * (w1 - 1) + 1:4]
-                nc.vector.tensor_mul(
-                    out=tbuf[k % RING][:, :, vp * 256:(vp + 1) * 256].rearrange("p m (a w) -> p m a w", w=16)[:, :, :, w0:w1],
-                    in0=z[:, :, vp * 256:(vp + 1) * 256].rearrange("p m (a w) -> p m a w", w=16)[:, :, :, w0:w1],
-                    in1=patch.unsqueeze(1).to_broadcast([P, 2, 16, w1 - w0]))
+            v0 = 1 if j == 0 else 0
+            v1 = 31 if j == 3 else 32
+            r0 = 2 * up + i
+            c0 = j - 1
+            patch = X[:, b, r0:r0 + 61:4, c0 + 2 * v0:c0 + 2 * (v1 - 1) + 1:2]
+            nc.vector.tensor_mul(
+                out=tbuf[k % RING][:, :, :].rearrange("p m (a v) -> p m a v", v=32)[:, :, :, v0:v1],
+                in0=z[:, :, :].rearrange("p m (a v) -> p m a v", v=32)[:, :, :, v0:v1],
+                in1=patch.unsqueeze(1).to_broadcast([P, 2, 16, v1 - v0]))
 
         def add_up(h, acc):
             k = h % TAPS
@@ -193,14 +193,14 @@ def tile_revolutionnaive_kernel(tc, x, conv_w, bn_gamma, bn_beta, bn_mean, bn_va
 
         def turn_back(ats, o, ah, on_vector):
             fb = pp.tile([P, 512], F32, name="fb", tag="pp")
-            for vp in range(2):
-                for m in range(2):
-                    q = 2 * vp + m
-                    blk = 2 * vp + ah
+            for m in range(2):
+                for bl in range(2):
+                    q = 2 * m + bl
+                    blk = 2 * ah + bl
                     nc.tensor.transpose(out=fb[:, q * 128:(q + 1) * 128],
                                         in_=ats[m][:, blk * 128:(blk + 1) * 128], identity=identF[:])
-            dst = o[:, ah * 512:(ah + 1) * 512].rearrange("p (al w q) -> p al w q", al=8, w=16, q=4)
-            src = fb[:].rearrange("p (q al w) -> p al w q", q=4, al=8, w=16)
+            dst = o[:, ah * 512:(ah + 1) * 512].rearrange("p (r m) -> p r m", m=2)
+            src = fb[:].rearrange("p (m r) -> p r m", m=2)
             if on_vector:
                 nc.vector.tensor_copy(out=dst, in_=src)
             else:
@@ -235,8 +235,8 @@ def tile_revolutionnaive_kernel(tc, x, conv_w, bn_gamma, bn_beta, bn_mean, bn_va
         nc.vector.memset(zrow[:], 0.0)
         nc.vector.memset(E[:, :, :, 0:66:65], 0.0)
         for j in range(0, RING, 4):
-            nc.vector.memset(tbuf[j][:, :, 0:256].rearrange("p m (a w) -> p m a w", w=16)[:, :, :, 0:1], 0.0)
-            nc.vector.memset(tbuf[j + 3][:, :, 256:512].rearrange("p m (a w) -> p m a w", w=16)[:, :, :, 15:16], 0.0)
+            nc.vector.memset(tbuf[j][:, :, :].rearrange("p m (a v) -> p m a v", v=32)[:, :, :, 0:1], 0.0)
+            nc.vector.memset(tbuf[j + 3][:, :, :].rearrange("p m (a v) -> p m a v", v=32)[:, :, :, 31:32], 0.0)
 
         nc.vector.tensor_scalar_add(out=vv[:], in0=raw[0][:], scalar1=BN_EPS)
         nc.scalar.sqrt(out=vv[:], in_=vv[:])

@@ -19,7 +19,7 @@ BN_EPS = 1e-5
 STEPS = 4 * TAPS
 LAG = 3
 RING = 8
-W_AHEAD = 5
+W_FRONT = 16
 
 LOWER = [(4, 0, 32, 0), (36, 32, 30, 0)]
 UPPER = [(66, 0, 32, 1), (98, 32, 30, 1)]
@@ -29,7 +29,6 @@ def tile_revolutionnaive_kernel(tc, x, conv_w, bn_gamma, bn_beta, bn_mean, bn_va
     nc = tc.nc
     with ExitStack() as ctx:
         keep = ctx.enter_context(tc.tile_pool(name="keep", bufs=1))
-        wgp = ctx.enter_context(tc.tile_pool(name="wgp", bufs=W_AHEAD + 1))
         zp = ctx.enter_context(tc.tile_pool(name="zp", bufs=3))
         atp = ctx.enter_context(tc.tile_pool(name="atp", bufs=4))
         op = ctx.enter_context(tc.tile_pool(name="op", bufs=2))
@@ -38,8 +37,7 @@ def tile_revolutionnaive_kernel(tc, x, conv_w, bn_gamma, bn_beta, bn_mean, bn_va
         ctx.enter_context(tc.manual_schedule())
 
         X = keep.tile([P, 2, 66, 64], BF16, name="X")
-        XS = keep.tile([P, C * 64], BF16, name="XS")
-        Wsb = keep.tile([P, TAPS, 1024], BF16, name="Wsb")
+        Wsb = keep.tile([P, TAPS, 1024], BF16, name="Wsb", align_bytes=64)
         E = keep.tile([P, 2, 33, 66], BF16, name="E")
         FT = keep.tile([P, 2, 33, 66], BF16, name="FT")
         G = keep.tile([P, 4, 2048], BF16, name="G", align_bytes=64)
@@ -49,13 +47,12 @@ def tile_revolutionnaive_kernel(tc, x, conv_w, bn_gamma, bn_beta, bn_mean, bn_va
         WS = keep.tile([P, 4096], U8, name="WS", align_bytes=64)
         tbuf = [keep.tile([P, 2, 512], F32, name="t%d" % j) for j in range(RING)]
         identF = keep.tile([P, P], F32, name="identF")
-        MR = keep.tile([P, 66], BF16, name="MR")
-        zrow = keep.tile([P, 128], BF16, name="zrow")
+        identB = keep.tile([P, P], BF16, name="identB")
+        MT = keep.tile([P, P], BF16, name="MT")
+        MRp = keep.tile([P, 2, 66], BF16, name="MRp")
         raw = [keep.tile([P, 64], BF16, name="raw%d" % q) for q in range(4)]
         Stab = keep.tile([P, TAPS, 2], F32, name="Stab")
         Btab = keep.tile([P, TAPS, 2], F32, name="Btab")
-        ta = keep.tile([P, 1984], BF16, name="ta")
-        tb = keep.tile([P, 1024], BF16, name="tb")
         vv = keep.tile([P, 64], F32, name="vv")
         sfull = keep.tile([P, 64], F32, name="sfull")
         bfull = keep.tile([P, 64], F32, name="bfull")
@@ -100,27 +97,33 @@ def tile_revolutionnaive_kernel(tc, x, conv_w, bn_gamma, bn_beta, bn_mean, bn_va
         def feat_x1(nt):
             b, up = divmod(nt, 2)
             for i in range(4):
-                a0 = 1 if (up == 0 and i == 0) else 0
-                a1 = 15 if (up == 1 and i == 3) else 16
-                r0 = 64 * b + 4 * a0 + 2 * up + i - 1
-                for vp in range(2):
-                    nc.sync.dma_start(out=G[i:i + 1, nt, vp * 1024 + a0 * 64:vp * 1024 + a1 * 64],
-                                      in_=MR[r0:r0 + 4 * (a1 - a0 - 1) + 1:4, 2 * vp:2 * vp + 64])
-            i, a = (0, 0) if up == 0 else (3, 15)
-            nc.sync.dma_start(out=G[i:i + 1, nt, :].rearrange("p (v r) -> p v r", v=2)[:, :, a * 64:(a + 1) * 64],
-                              in_=zrow[i:i + 1, :].rearrange("p (v s) -> p v s", v=2))
+                d = 2 * up + i - 1
+                p0 = 1 + 64 * b + d // 2
+                nc.sync.dma_start(out=E[i:i + 1, b, up:up + 32, :],
+                                  in_=MRp[p0:p0 + 31:2, d % 2, :].unsqueeze(1).to_broadcast([16, 2, 66]))
 
         def feat_q(nt):
             nc.vector.quantize_mx(out=FC[:, nt * 512:(nt + 1) * 512].bitcast(FP8X4),
                                   scales=FS[:, nt * 512:(nt + 1) * 512], in_=G[:, nt, :])
 
-        def chan_max():
-            nc.vector.tensor_max(out=ta[:], in0=XS[:, 0:1984], in1=XS[:, 1984:3968])
-            nc.vector.tensor_max(out=tb[:], in0=ta[:, 0:1024], in1=ta[:, 960:1984])
-            nc.vector.tensor_max(out=ta[:, 0:512], in0=tb[:, 0:512], in1=tb[:, 512:1024])
-            nc.vector.tensor_max(out=tb[:, 0:256], in0=ta[:, 0:256], in1=ta[:, 256:512])
-            nc.vector.tensor_max(out=ta[:, 0:128], in0=tb[:, 0:128], in1=tb[:, 128:256])
-            nc.vector.tensor_max(out=MR[:, 1:65], in0=ta[:, 0:64], in1=ta[:, 64:128])
+        def chan_turn(b, g4, pool, tag):
+            pt = pool.tile([P, 1024], BF16, name="pt", tag=tag)
+            for jj in range(8):
+                j = 8 * g4 + jj
+                nc.tensor.transpose(out=pt[:, jj * 128:(jj + 1) * 128],
+                                    in_=X[:, b, 1 + 2 * j:3 + 2 * j, :].rearrange("p r s -> p (r s)"), identity=identB[:])
+            return pt
+
+        def chan_reduce(b, g4, pt):
+            c0 = 1 + 64 * b + 8 * g4
+            nc.vector.tensor_reduce(out=MT[:, c0:c0 + 8], in_=pt[:].rearrange("p (j c) -> p j c", c=128)[:, :, 4:66],
+                                    axis=mybir.AxisListType.X, op=ALU.max)
+
+        def chan_rows(b):
+            pm = pp.tile([P, P], BF16, name="pm", tag="pp")
+            nc.tensor.transpose(out=pm[:], in_=MT[:], identity=identB[:])
+            nc.scalar.copy(out=MRp[64 * b:64 * b + 64, :, 1:65],
+                           in_=pm[64 * b:64 * b + 64, :].rearrange("p (rp s) -> p rp s", rp=2))
 
         def weights(k):
             wt = pp.tile([P, 512], F32, name="wt", tag="pp")
@@ -130,14 +133,13 @@ def tile_revolutionnaive_kernel(tc, x, conv_w, bn_gamma, bn_beta, bn_mean, bn_va
                     q = 2 * m + e
                     nc.tensor.transpose(out=wt[:, q * 128:(q + 1) * 128], in_=words[:, e:256:2],
                                         identity=identF[:])
-            wg = wgp.tile([P, 1024], BF16, name="wg", align_bytes=64)
-            nc.scalar.copy(out=wg[:].bitcast(F32).rearrange("p (m o e) -> p m o e", m=2, o=128, e=2),
+            nc.scalar.copy(out=Wsb[:, k, :].bitcast(F32).rearrange("p (m o e) -> p m o e", m=2, o=128, e=2),
                            in_=wt[:].rearrange("p (m e o) -> p m o e", m=2, e=2, o=128))
-            return wg
 
-        def weights_q(k, wg):
-            nc.vector.quantize_mx(out=WC[:, k * 256:(k + 1) * 256].bitcast(FP8X4),
-                                  scales=WS[:, k * 256:(k + 1) * 256], in_=wg[:])
+        def weights_q(k):
+            nc.vector.quantize_mx(out=WC[:, k * 256:(k + 2) * 256].bitcast(FP8X4),
+                                  scales=WS[:, k * 256:(k + 2) * 256],
+                                  in_=Wsb[:, k:k + 2, :].rearrange("p k f -> p (k f)"))
 
         def mx_act(h):
             nt, k = divmod(h, TAPS)
@@ -214,25 +216,27 @@ def tile_revolutionnaive_kernel(tc, x, conv_w, bn_gamma, bn_beta, bn_mean, bn_va
                     in_=o[p0:p0 + cn, :].rearrange("p (a s) -> p a s", s=64))
 
         make_identity(nc, identF[:])
-        for b, queue in enumerate((nc.scalar, nc.gpsimd)):
-            queue.dma_start(out=XS[64 * b:64 * b + 64, :].rearrange("r (c s) -> r c s", s=64),
-                            in_=x[b].rearrange("c r s -> r c s"))
         for q in range(4):
             nc.vector.memset(raw[q][:], 0.0)
         for q, vec in enumerate((bn_var, bn_gamma, bn_mean, bn_beta)):
             v2 = vec.rearrange("(c q) -> c q", q=64)
             nc.scalar.dma_start(out=raw[q][4:66, :], in_=v2)
             nc.scalar.dma_start(out=raw[q][66:128, :], in_=v2)
+        nc.scalar.copy(out=identB[:], in_=identF[:])
         nc.vector.memset(X[:, :, 0:66:65, :], 0.0)
+        nc.vector.memset(X[0:4, 0, 1:65, :].rearrange("p r s -> p (r s)").bitcast(F32), 0.0)
+        for k0 in range(0, TAPS, 4):
+            nc.gpsimd.memset(Wsb[0:4, k0:k0 + 4, :].rearrange("p k f -> p (k f)").bitcast(F32), 0.0)
+        nc.gpsimd.memset(X[0:4, 1, 1:65, :].rearrange("p r s -> p (r s)").bitcast(F32), 0.0)
 
-        load_x(nc.sync, 0, LOWER + UPPER + [(0, 0, 4, 0)])
-        nc.sync.dma_start(out=Wsb[0:4, :, :].rearrange("p k f -> p (k f)"),
-                          in_=conv_w[0:128, :].rearrange("(p a) f -> p (a f)", p=4))
-        for k0 in (0, 4):
+        load_x(nc.sync, 0, LOWER)
+        load_x(nc.sync, 0, UPPER)
+        for k0 in range(0, TAPS, 4):
             load_w(nc.sync, k0, LOWER + UPPER)
+        load_x(nc.sync, 1, LOWER + UPPER)
 
-        nc.vector.memset(MR[:], 0.0)
-        nc.vector.memset(zrow[:], 0.0)
+        nc.vector.memset(MT[:], 0.0)
+        nc.vector.memset(MRp[:], 0.0)
         nc.vector.memset(E[:, :, :, 0:66:65], 0.0)
         for j in range(0, RING, 4):
             nc.vector.memset(tbuf[j][:, :, :].rearrange("p m (a v) -> p m a v", v=32)[:, :, :, 0:1], 0.0)
@@ -241,27 +245,24 @@ def tile_revolutionnaive_kernel(tc, x, conv_w, bn_gamma, bn_beta, bn_mean, bn_va
         nc.vector.tensor_scalar_add(out=vv[:], in0=raw[0][:], scalar1=BN_EPS)
         nc.scalar.sqrt(out=vv[:], in_=vv[:])
         feat_e(0, 0, 33)
+        pts = [chan_turn(0, g4, yp, "y") for g4 in range(4)]
+        for g4 in range(4):
+            chan_reduce(0, g4, pts[g4])
+        for k in range(4):
+            weights(k)
+        chan_rows(0)
+        feat_x1(0)
+        for k in range(4, W_FRONT):
+            weights(k)
         feat_ft(0, 1, 32)
         feat_ftb(0)
         for vp in range(2):
             feat_g3(0, vp)
         for vp in range(2):
             feat_g2(0, vp)
-        chan_max()
-        feat_x1(0)
-        for k0 in (8, 12):
-            load_w(nc.sync, k0, LOWER + UPPER)
-        load_x(nc.sync, 1, LOWER + UPPER + [(0, 0, 4, 0)])
-        wgs = {}
-        for k in range(W_AHEAD):
-            wgs[k] = weights(k)
-        for vp in range(2):
-            feat_g3(1, vp)
-        for vp in range(2):
-            feat_g2(1, vp)
         feat_x1(1)
+        weights_q(0)
         feat_q(0)
-        weights_q(0, wgs[0])
         nc.vector.reciprocal(out=vv[:], in_=vv[:])
         nc.vector.tensor_mul(out=sfull[:], in0=raw[1][:], in1=vv[:])
         nc.vector.tensor_mul(out=bfull[:], in0=raw[2][:], in1=sfull[:])
@@ -270,22 +271,41 @@ def tile_revolutionnaive_kernel(tc, x, conv_w, bn_gamma, bn_beta, bn_mean, bn_va
             fv = full[:].rearrange("p (k n m) -> p k n m", k=TAPS, n=2, m=2)
             nc.vector.tensor_copy(out=tab[64:128], in_=fv[64:128, :, 1, :])
             nc.vector.tensor_copy(out=tab[0:66], in_=fv[0:66, :, 0, :])
-        for k in range(1, W_AHEAD):
-            weights_q(k, wgs[k])
+        for k in (2, 4):
+            weights_q(k)
 
-        def later(nt):
-            return ([lambda vp=vp: feat_g3(nt, vp) for vp in range(2)] + [lambda: feat_g2(nt, 0), lambda: (feat_g2(nt, 1), feat_x1(nt))]
-                    + [lambda: None, lambda: None, lambda: feat_q(nt)])
-
-        batch1 = ([lambda u=u: feat_e(1, u, u + 11) for u in (0, 11, 22)]
-                  + [lambda: feat_ft(1, 1, 11), lambda: feat_ft(1, 11, 21), lambda: (feat_ft(1, 21, 32), feat_ftb(1))])
-        side = {1: later(1)[6:], 2: batch1 + later(2), 3: later(3)}
+        pts1 = {}
+        side = {}
+        side[0] = lambda: (chan_reduce(1, 0, pts1[0]), chan_reduce(1, 1, pts1[1]))
+        side[1] = lambda: (chan_reduce(1, 2, pts1[2]), chan_reduce(1, 3, pts1[3]))
+        for h in range(2, 12, 2):
+            side[h] = lambda k=h + 4: weights_q(k)
+        side[3] = lambda: feat_g3(1, 0)
+        side[5] = lambda: feat_g3(1, 1)
+        side[7] = lambda: feat_g2(1, 0)
+        side[9] = lambda: feat_g2(1, 1)
+        side[11] = lambda: feat_q(1)
+        for h, u in ((12, 0), (13, 11)):
+            side[h] = lambda u=u: feat_e(1, u, u + 11)
+        side[14] = lambda: (feat_e(1, 22, 33), feat_x1(2))
+        for h, v in ((15, 1), (16, 6), (17, 11), (18, 16), (19, 21)):
+            side[h] = lambda v=v: feat_ft(1, v, v + 5)
+        side[20] = lambda: (feat_ft(1, 26, 32), feat_ftb(1))
+        side[21] = lambda: feat_g3(2, 0)
+        side[22] = lambda: feat_g3(2, 1)
+        side[23] = lambda: feat_g2(2, 0)
+        side[24] = lambda: (feat_g2(2, 1), feat_x1(3))
+        side[27] = lambda: feat_q(2)
+        side[29] = lambda: feat_g3(3, 0)
+        side[32] = lambda: feat_g3(3, 1)
+        side[35] = lambda: feat_g2(3, 0)
+        side[38] = lambda: feat_g2(3, 1)
+        side[42] = lambda: feat_q(3)
 
         zs = {}
         accs = {}
         done = {}
         for h in range(STEPS + LAG + 3):
-            nt, k = divmod(h, TAPS)
             if h < STEPS:
                 zs[h] = mx_act(h)
             g = h - LAG
@@ -301,14 +321,14 @@ def tile_revolutionnaive_kernel(tc, x, conv_w, bn_gamma, bn_beta, bn_mean, bn_va
                 turn_back(ats, o, f % TAPS, on_vector=(h >= STEPS and f % TAPS == 1))
                 if f % TAPS == 1:
                     store(f // TAPS, o)
-            if h + W_AHEAD < TAPS:
-                wgs[h + W_AHEAD] = weights(h + W_AHEAD)
+            if h + W_FRONT < TAPS:
+                weights(h + W_FRONT)
+            if h < 2:
+                for g4 in (2 * h, 2 * h + 1):
+                    pts1[g4] = chan_turn(1, g4, pp, "pp")
+            if h == 5:
+                chan_rows(1)
             if h < STEPS:
                 mul(h, zs[h])
-            if 1 <= h and h - 1 + W_AHEAD < TAPS:
-                weights_q(h - 1 + W_AHEAD, wgs[h - 1 + W_AHEAD])
-            if nt < 3:
-                todo = side[nt + 1]
-                first = TAPS - 1 - len(todo)
-                if 0 <= k - first < len(todo):
-                    todo[k - first]()
+            if h in side:
+                side[h]()

@@ -17,8 +17,8 @@ TAPS = 16
 FLOPS = 2 * 3968 * 512 * 2048
 BN_EPS = 1e-5
 STEPS = 4 * TAPS
-LAG = 3
-RING = 8
+LAG = 5
+RING = 12
 W_FRONT = 16
 
 LOWER = [(4, 0, 32, 0), (36, 32, 30, 0)]
@@ -29,7 +29,7 @@ def tile_revolutionnaive_kernel(tc, x, conv_w, bn_gamma, bn_beta, bn_mean, bn_va
     nc = tc.nc
     with ExitStack() as ctx:
         keep = ctx.enter_context(tc.tile_pool(name="keep", bufs=1))
-        zp = ctx.enter_context(tc.tile_pool(name="zp", bufs=3))
+        zp = ctx.enter_context(tc.tile_pool(name="zp", bufs=6))
         atp = ctx.enter_context(tc.tile_pool(name="atp", bufs=4))
         op = ctx.enter_context(tc.tile_pool(name="op", bufs=2))
         yp = ctx.enter_context(tc.psum_pool(name="yp", bufs=4))
@@ -171,13 +171,13 @@ def tile_revolutionnaive_kernel(tc, x, conv_w, bn_gamma, bn_beta, bn_mean, bn_va
             c0 = j - 1
             patch = X[:, b, r0:r0 + 61:4, c0 + 2 * v0:c0 + 2 * (v1 - 1) + 1:2]
             nc.vector.tensor_mul(
-                out=tbuf[k % RING][:, :, :].rearrange("p m (a v) -> p m a v", v=32)[:, :, :, v0:v1],
+                out=tbuf[h % RING][:, :, :].rearrange("p m (a v) -> p m a v", v=32)[:, :, :, v0:v1],
                 in0=z[:, :, :].rearrange("p m (a v) -> p m a v", v=32)[:, :, :, v0:v1],
                 in1=patch.unsqueeze(1).to_broadcast([P, 2, 16, v1 - v0]))
 
         def add_up(h, acc):
             k = h % TAPS
-            src = tbuf[k % RING]
+            src = tbuf[h % RING]
             for m in range(2):
                 for blk in range(4):
                     nc.tensor.matmul(out=acc[m][:, blk * 128:(blk + 1) * 128],
@@ -185,11 +185,14 @@ def tile_revolutionnaive_kernel(tc, x, conv_w, bn_gamma, bn_beta, bn_mean, bn_va
                                      rhs=identF[:], is_transpose=True,
                                      start=(k == 0 and blk == 0), stop=(k == TAPS - 1 and blk == 3))
 
-        def leave_psum(acc):
+        def leave_psum(acc, last):
             ats = []
             for m in range(2):
                 at = atp.tile([P, 512], F32, name="at")
-                nc.scalar.mul(out=at[:], in_=acc[m][:], mul=1.0 / TAPS)
+                if last and m == 1:
+                    nc.vector.tensor_scalar_mul(out=at[:], in0=acc[m][:], scalar1=1.0 / TAPS)
+                else:
+                    nc.scalar.mul(out=at[:], in_=acc[m][:], mul=1.0 / TAPS)
                 ats.append(at)
             return ats
 
@@ -211,7 +214,8 @@ def tile_revolutionnaive_kernel(tc, x, conv_w, bn_gamma, bn_beta, bn_mean, bn_va
         def store(nt, o):
             b, up = divmod(nt, 2)
             for (p0, c0, cn, n) in LOWER + UPPER:
-                nc.sync.dma_start(
+                queue = nc.scalar if (nt == 3 and n == 1) else nc.sync
+                queue.dma_start(
                     out=out[b, c0:c0 + cn].rearrange("c (a r) s -> c a r s", r=4)[:, :, 2 * up + n, :],
                     in_=o[p0:p0 + cn, :].rearrange("p (a s) -> p a s", s=64))
 
@@ -222,7 +226,6 @@ def tile_revolutionnaive_kernel(tc, x, conv_w, bn_gamma, bn_beta, bn_mean, bn_va
             v2 = vec.rearrange("(c q) -> c q", q=64)
             nc.scalar.dma_start(out=raw[q][4:66, :], in_=v2)
             nc.scalar.dma_start(out=raw[q][66:128, :], in_=v2)
-        nc.scalar.copy(out=identB[:], in_=identF[:])
         nc.vector.memset(X[:, :, 0:66:65, :], 0.0)
         nc.vector.memset(X[0:4, 0, 1:65, :].rearrange("p r s -> p (r s)").bitcast(F32), 0.0)
         for k0 in range(0, TAPS, 4):
@@ -235,6 +238,7 @@ def tile_revolutionnaive_kernel(tc, x, conv_w, bn_gamma, bn_beta, bn_mean, bn_va
             load_w(nc.sync, k0, LOWER + UPPER)
         load_x(nc.sync, 1, LOWER + UPPER)
 
+        nc.vector.tensor_copy(out=identB[:], in_=identF[:])
         nc.vector.memset(MT[:], 0.0)
         nc.vector.memset(MRp[:], 0.0)
         nc.vector.memset(E[:, :, :, 0:66:65], 0.0)
@@ -258,10 +262,10 @@ def tile_revolutionnaive_kernel(tc, x, conv_w, bn_gamma, bn_beta, bn_mean, bn_va
         feat_ftb(0)
         for vp in range(2):
             feat_g3(0, vp)
+        weights_q(0)
         for vp in range(2):
             feat_g2(0, vp)
         feat_x1(1)
-        weights_q(0)
         feat_q(0)
         nc.vector.reciprocal(out=vv[:], in_=vv[:])
         nc.vector.tensor_mul(out=sfull[:], in0=raw[1][:], in1=vv[:])
@@ -276,14 +280,14 @@ def tile_revolutionnaive_kernel(tc, x, conv_w, bn_gamma, bn_beta, bn_mean, bn_va
 
         pts1 = {}
         side = {}
-        side[0] = lambda: (chan_reduce(1, 0, pts1[0]), chan_reduce(1, 1, pts1[1]))
-        side[1] = lambda: (chan_reduce(1, 2, pts1[2]), chan_reduce(1, 3, pts1[3]))
-        for h in range(2, 12, 2):
-            side[h] = lambda k=h + 4: weights_q(k)
-        side[3] = lambda: feat_g3(1, 0)
-        side[5] = lambda: feat_g3(1, 1)
+        for h in range(0, 10, 2):
+            side[h] = lambda k=h + 6: weights_q(k)
+        side[1] = lambda: feat_g3(1, 0)
+        side[3] = lambda: feat_g3(1, 1)
+        side[5] = lambda: (chan_reduce(1, 0, pts1[0]), chan_reduce(1, 1, pts1[1]))
         side[7] = lambda: feat_g2(1, 0)
         side[9] = lambda: feat_g2(1, 1)
+        side[10] = lambda: (chan_reduce(1, 2, pts1[2]), chan_reduce(1, 3, pts1[3]))
         side[11] = lambda: feat_q(1)
         for h, u in ((12, 0), (13, 11)):
             side[h] = lambda u=u: feat_e(1, u, u + 11)
@@ -314,7 +318,7 @@ def tile_revolutionnaive_kernel(tc, x, conv_w, bn_gamma, bn_beta, bn_mean, bn_va
                     accs[g // TAPS] = [pp.tile([P, 512], F32, name="acc", tag="pp") for m in range(2)]
                 add_up(g, accs[g // TAPS])
                 if g % TAPS == TAPS - 1:
-                    done[g // TAPS] = (leave_psum(accs[g // TAPS]), op.tile([P, 1024], F32, name="o"))
+                    done[g // TAPS] = (leave_psum(accs[g // TAPS], g == STEPS - 1), op.tile([P, 1024], F32, name="o"))
             f = h - LAG - TAPS
             if f >= 0 and f % TAPS in (0, 1):
                 ats, o = done[f // TAPS]
@@ -323,10 +327,10 @@ def tile_revolutionnaive_kernel(tc, x, conv_w, bn_gamma, bn_beta, bn_mean, bn_va
                     store(f // TAPS, o)
             if h + W_FRONT < TAPS:
                 weights(h + W_FRONT)
-            if h < 2:
-                for g4 in (2 * h, 2 * h + 1):
+            if h in (3, 9):
+                for g4 in ((0, 1) if h == 3 else (2, 3)):
                     pts1[g4] = chan_turn(1, g4, pp, "pp")
-            if h == 5:
+            if h == 14:
                 chan_rows(1)
             if h < STEPS:
                 mul(h, zs[h])

@@ -136,10 +136,10 @@ def tile_revolutionnaive_kernel(tc, x, conv_w, bn_gamma, bn_beta, bn_mean, bn_va
             nc.scalar.copy(out=Wsb[:, k, :].bitcast(F32).rearrange("p (m o e) -> p m o e", m=2, o=128, e=2),
                            in_=wt[:].rearrange("p (m e o) -> p m o e", m=2, e=2, o=128))
 
-        def weights_q(k):
-            nc.vector.quantize_mx(out=WC[:, k * 256:(k + 2) * 256].bitcast(FP8X4),
-                                  scales=WS[:, k * 256:(k + 2) * 256],
-                                  in_=Wsb[:, k:k + 2, :].rearrange("p k f -> p (k f)"))
+        def weights_q(k, n):
+            nc.vector.quantize_mx(out=WC[:, k * 256:(k + n) * 256].bitcast(FP8X4),
+                                  scales=WS[:, k * 256:(k + n) * 256],
+                                  in_=Wsb[:, k:k + n, :].rearrange("p k f -> p (k f)"))
 
         def mx_act(h):
             nt, k = divmod(h, TAPS)
@@ -262,7 +262,7 @@ def tile_revolutionnaive_kernel(tc, x, conv_w, bn_gamma, bn_beta, bn_mean, bn_va
         feat_ftb(0)
         for vp in range(2):
             feat_g3(0, vp)
-        weights_q(0)
+        weights_q(0, 2)
         for vp in range(2):
             feat_g2(0, vp)
         feat_x1(1)
@@ -276,18 +276,19 @@ def tile_revolutionnaive_kernel(tc, x, conv_w, bn_gamma, bn_beta, bn_mean, bn_va
             nc.vector.tensor_copy(out=tab[64:128], in_=fv[64:128, :, 1, :])
             nc.vector.tensor_copy(out=tab[0:66], in_=fv[0:66, :, 0, :])
         for k in (2, 4):
-            weights_q(k)
+            weights_q(k, 2)
 
         pts1 = {}
         side = {}
-        for h in range(0, 10, 2):
-            side[h] = lambda k=h + 6: weights_q(k)
-        side[1] = lambda: feat_g3(1, 0)
-        side[3] = lambda: feat_g3(1, 1)
-        side[5] = lambda: (chan_reduce(1, 0, pts1[0]), chan_reduce(1, 1, pts1[1]))
-        side[7] = lambda: feat_g2(1, 0)
-        side[9] = lambda: feat_g2(1, 1)
-        side[10] = lambda: (chan_reduce(1, 2, pts1[2]), chan_reduce(1, 3, pts1[3]))
+        side[0] = lambda: weights_q(6, 2)
+        for g4 in range(4):
+            side[1 + g4] = lambda g4=g4: chan_reduce(1, g4, pts1[g4])
+        side[5] = lambda: weights_q(8, 4)
+        side[6] = lambda: feat_g3(1, 0)
+        side[7] = lambda: feat_g3(1, 1)
+        side[8] = lambda: weights_q(12, 4)
+        side[9] = lambda: feat_g2(1, 0)
+        side[10] = lambda: feat_g2(1, 1)
         side[11] = lambda: feat_q(1)
         for h, u in ((12, 0), (13, 11)):
             side[h] = lambda u=u: feat_e(1, u, u + 11)
@@ -327,10 +328,9 @@ def tile_revolutionnaive_kernel(tc, x, conv_w, bn_gamma, bn_beta, bn_mean, bn_va
                     store(f // TAPS, o)
             if h + W_FRONT < TAPS:
                 weights(h + W_FRONT)
-            if h in (3, 9):
-                for g4 in ((0, 1) if h == 3 else (2, 3)):
-                    pts1[g4] = chan_turn(1, g4, pp, "pp")
-            if h == 14:
+            if 1 <= h <= 4:
+                pts1[h - 1] = chan_turn(1, h - 1, pp, "pp")
+            if h == 8:
                 chan_rows(1)
             if h < STEPS:
                 mul(h, zs[h])

@@ -40,6 +40,7 @@ def tile_revolutionnaive_kernel(tc, x, conv_w, bn_gamma, bn_beta, bn_mean, bn_va
         Wsb = keep.tile([P, TAPS, 1024], BF16, name="Wsb", align_bytes=64)
         E = keep.tile([P, 2, 33, 66], BF16, name="E")
         FT = keep.tile([P, 2, 33, 66], BF16, name="FT")
+        XT = keep.tile([P, 64, 66], BF16, name="XT")
         G = keep.tile([P, 4, 2048], BF16, name="G", align_bytes=64)
         FC = keep.tile([P, 2048], U32, name="FC", align_bytes=64)
         FS = keep.tile([P, 2048], U8, name="FS", align_bytes=64)
@@ -79,6 +80,14 @@ def tile_revolutionnaive_kernel(tc, x, conv_w, bn_gamma, bn_beta, bn_mean, bn_va
         def feat_ftb(b):
             nc.vector.tensor_scalar_max(out=FT[64:128, b, 0:33:32, :],
                                         in0=X[64:128, b, :, 0:64:63].rearrange("p r v -> p v r"), scalar1=0.0)
+
+        def turn_x(c8):
+            nc.scalar.copy(out=XT[64:128, 8 * c8:8 * c8 + 8, :],
+                           in_=X[64:128, 1, :, 8 * c8:8 * c8 + 8].rearrange("p r s -> p s r"))
+
+        def feat_ft_turned():
+            nc.vector.tensor_max(out=FT[64:128, 1, 1:32, :], in0=XT[64:128, 1:62:2, :], in1=XT[64:128, 2:63:2, :])
+            nc.vector.tensor_scalar_max(out=FT[64:128, 1, 0:33:32, :], in0=XT[64:128, 0:64:63, :], scalar1=0.0)
 
         def feat_g3(nt, vp):
             b, up = divmod(nt, 2)
@@ -290,14 +299,10 @@ def tile_revolutionnaive_kernel(tc, x, conv_w, bn_gamma, bn_beta, bn_mean, bn_va
         side[9] = lambda: feat_g2(1, 0)
         side[10] = lambda: feat_g2(1, 1)
         side[11] = lambda: feat_q(1)
-        for h, u in ((12, 0), (13, 11)):
-            side[h] = lambda u=u: feat_e(1, u, u + 11)
-        side[14] = lambda: (feat_e(1, 22, 33), feat_x1(2))
-        for h, v in ((15, 1), (16, 6), (17, 11), (18, 16), (19, 21)):
-            side[h] = lambda v=v: feat_ft(1, v, v + 5)
-        side[20] = lambda: (feat_ft(1, 26, 32), feat_ftb(1))
-        side[21] = lambda: feat_g3(2, 0)
-        side[22] = lambda: feat_g3(2, 1)
+        side[13] = lambda: (feat_e(1, 0, 33), feat_x1(2))
+        side[18] = lambda: feat_ft_turned()
+        side[20] = lambda: feat_g3(2, 0)
+        side[21] = lambda: feat_g3(2, 1)
         side[23] = lambda: feat_g2(2, 0)
         side[24] = lambda: (feat_g2(2, 1), feat_x1(3))
         side[27] = lambda: feat_q(2)
@@ -313,6 +318,8 @@ def tile_revolutionnaive_kernel(tc, x, conv_w, bn_gamma, bn_beta, bn_mean, bn_va
         for h in range(STEPS + LAG + 3):
             if h < STEPS:
                 zs[h] = mx_act(h)
+            if 2 <= h <= 16 and h % 2 == 0:
+                turn_x(h // 2 - 1)
             g = h - LAG
             if 0 <= g < STEPS:
                 if g % TAPS == 0:

@@ -19,7 +19,7 @@ BN_EPS = 1e-5
 STEPS = 4 * TAPS
 LAG = 5
 RING = 12
-W_FRONT = 16
+ORDER = [0, 1, 2, 3, 8, 9, 10, 11, 4, 5, 6, 7, 12, 13, 14, 15]
 
 LOWER = [(4, 0, 32, 0), (36, 32, 30, 0)]
 UPPER = [(66, 0, 32, 1), (98, 32, 30, 1)]
@@ -37,11 +37,12 @@ def tile_revolutionnaive_kernel(tc, x, conv_w, bn_gamma, bn_beta, bn_mean, bn_va
         ctx.enter_context(tc.manual_schedule())
 
         X = keep.tile([P, 2, 66, 64], BF16, name="X")
+        Wraw = keep.tile([P, 32, 512], BF16, name="Wraw", align_bytes=64)
         Wsb = keep.tile([P, TAPS, 1024], BF16, name="Wsb", align_bytes=64)
         E = keep.tile([P, 2, 33, 66], BF16, name="E")
         FT = keep.tile([P, 2, 33, 66], BF16, name="FT")
         XT = keep.tile([P, 64, 66], BF16, name="XT")
-        G = keep.tile([P, 4, 2048], BF16, name="G", align_bytes=64)
+        G = keep.tile([P, 2, 2048], BF16, name="G", align_bytes=64)
         FC = keep.tile([P, 2048], U32, name="FC", align_bytes=64)
         FS = keep.tile([P, 2048], U8, name="FS", align_bytes=64)
         WC = keep.tile([P, 4096], U32, name="WC", align_bytes=64)
@@ -58,15 +59,16 @@ def tile_revolutionnaive_kernel(tc, x, conv_w, bn_gamma, bn_beta, bn_mean, bn_va
         sfull = keep.tile([P, 64], F32, name="sfull")
         bfull = keep.tile([P, 64], F32, name="bfull")
 
-        w5 = conv_w.rearrange("(c k n m) f -> c k n (m f)", c=C, k=TAPS, n=2, m=2)
+        w32 = conv_w.rearrange("(p r) f -> p (r f)", r=32)
 
         def load_x(queue, b, ranges):
             for (p0, c0, cn, n) in ranges:
                 queue.dma_start(out=X[p0:p0 + cn, b, 1:65, :], in_=x[b, c0:c0 + cn])
 
-        def load_w(queue, k0, ranges):
-            for (p0, c0, cn, n) in ranges:
-                queue.dma_start(out=Wsb[p0:p0 + cn, k0:k0 + 4, :], in_=w5[c0:c0 + cn, k0:k0 + 4, n, :])
+        def load_w(queue, q):
+            for (p0, pn) in ((0, 112), (112, 12)):
+                queue.dma_start(out=Wraw[4 + p0:4 + p0 + pn, 8 * q:8 * q + 8, :].rearrange("p r f -> p (r f)"),
+                                in_=w32[p0:p0 + pn, 4096 * q:4096 * q + 4096])
 
         def feat_e(b, u0, u1):
             xr = X[0:66, b, 2 * u0:2 * u1, :].rearrange("p (u r2) s -> p u r2 s", r2=2)
@@ -92,28 +94,28 @@ def tile_revolutionnaive_kernel(tc, x, conv_w, bn_gamma, bn_beta, bn_mean, bn_va
         def feat_g3(nt, vp):
             b, up = divmod(nt, 2)
             nc.vector.tensor_max(
-                out=G[64:128, nt, vp * 1024:(vp + 1) * 1024].rearrange("p (a w i) -> p a w i", a=16, w=16, i=4),
+                out=G[64:128, nt % 2, vp * 1024:(vp + 1) * 1024].rearrange("p (a w i) -> p a w i", a=16, w=16, i=4),
                 in0=FT[64:128, b, vp:vp + 31:2, 2 * up:2 * up + 64].rearrange("p w (a i) -> p a w i", i=4),
                 in1=FT[64:128, b, vp + 1:vp + 32:2, 2 * up:2 * up + 64].rearrange("p w (a i) -> p a w i", i=4))
 
         def feat_g2(nt, vp):
             b, up = divmod(nt, 2)
             nc.vector.tensor_max(
-                out=G[0:66, nt, vp * 1024:(vp + 1) * 1024].rearrange("p (a s) -> p a s", a=16, s=64),
+                out=G[0:66, nt % 2, vp * 1024:(vp + 1) * 1024].rearrange("p (a s) -> p a s", a=16, s=64),
                 in0=E[0:66, b, up:up + 31:2, 2 * vp:2 * vp + 64],
                 in1=E[0:66, b, up + 1:up + 32:2, 2 * vp:2 * vp + 64])
 
-        def feat_x1(nt):
+        def feat_x1(nt, queue):
             b, up = divmod(nt, 2)
             for i in range(4):
                 d = 2 * up + i - 1
                 p0 = 1 + 64 * b + d // 2
-                nc.sync.dma_start(out=E[i:i + 1, b, up:up + 32, :],
+                queue.dma_start(out=E[i:i + 1, b, up:up + 32, :],
                                   in_=MRp[p0:p0 + 31:2, d % 2, :].unsqueeze(1).to_broadcast([16, 2, 66]))
 
         def feat_q(nt):
             nc.vector.quantize_mx(out=FC[:, nt * 512:(nt + 1) * 512].bitcast(FP8X4),
-                                  scales=FS[:, nt * 512:(nt + 1) * 512], in_=G[:, nt, :])
+                                  scales=FS[:, nt * 512:(nt + 1) * 512], in_=G[:, nt % 2, :])
 
         def chan_turn(b, g4, pool, tag):
             pt = pool.tile([P, 1024], BF16, name="pt", tag=tag)
@@ -135,27 +137,32 @@ def tile_revolutionnaive_kernel(tc, x, conv_w, bn_gamma, bn_beta, bn_mean, bn_va
                            in_=pm[64 * b:64 * b + 64, :].rearrange("p (rp s) -> p rp s", rp=2))
 
         def weights(k):
-            wt = pp.tile([P, 512], F32, name="wt", tag="pp")
             for m in range(2):
-                words = Wsb[:, k, m * 512:(m + 1) * 512].bitcast(F32)
-                for e in range(2):
-                    q = 2 * m + e
-                    nc.tensor.transpose(out=wt[:, q * 128:(q + 1) * 128], in_=words[:, e:256:2],
-                                        identity=identF[:])
-            nc.scalar.copy(out=Wsb[:, k, :].bitcast(F32).rearrange("p (m o e) -> p m o e", m=2, o=128, e=2),
-                           in_=wt[:].rearrange("p (m e o) -> p m o e", m=2, e=2, o=128))
+                wt = pp.tile([P, 512], F32, name="wt", tag="pp")
+                for n in range(2):
+                    words = Wraw[:, 4 * k + 2 * n + m, :].bitcast(F32)
+                    for e in range(2):
+                        q = 2 * n + e
+                        nc.tensor.transpose(out=wt[:, q * 128:(q + 1) * 128], in_=words[:, e:256:2],
+                                            identity=identF[:])
+                for t in range(2):
+                    s = ORDER.index(k + 8 * t)
+                    nc.scalar.copy(
+                        out=Wsb[:, s, m * 512 + 16:(m + 1) * 512].bitcast(F32).rearrange("p (n c e) -> p n c e", n=2, e=2),
+                        in_=wt[:].rearrange("p (n e q) -> p n q e", n=2, e=2)[:, :, 4 + t:128:2, :])
 
-        def weights_q(k, n):
-            nc.vector.quantize_mx(out=WC[:, k * 256:(k + n) * 256].bitcast(FP8X4),
-                                  scales=WS[:, k * 256:(k + n) * 256],
-                                  in_=Wsb[:, k:k + n, :].rearrange("p k f -> p (k f)"))
+        def weights_q(s, n):
+            nc.vector.quantize_mx(out=WC[:, s * 256:(s + n) * 256].bitcast(FP8X4),
+                                  scales=WS[:, s * 256:(s + n) * 256],
+                                  in_=Wsb[:, s:s + n, :].rearrange("p k f -> p (k f)"))
 
         def mx_act(h):
-            nt, k = divmod(h, TAPS)
+            nt, s = divmod(h, TAPS)
+            k = ORDER[s]
             z = zp.tile([P, 2, 512], F32, name="z")
             ys = []
             for m in range(2):
-                tl = 2 * k + m
+                tl = 2 * s + m
                 y = yp.tile([P, 512], F32, name="y")
                 nc.tensor.matmul_mx(out=y[:],
                                     lhsT=WC[:, tl * 128:(tl + 1) * 128].bitcast(FP8X4),
@@ -171,9 +178,9 @@ def tile_revolutionnaive_kernel(tc, x, conv_w, bn_gamma, bn_beta, bn_mean, bn_va
             return z
 
         def mul(h, z):
-            nt, k = divmod(h, TAPS)
+            nt, s = divmod(h, TAPS)
             b, up = divmod(nt, 2)
-            i, j = divmod(k, 4)
+            i, j = divmod(ORDER[s], 4)
             v0 = 1 if j == 0 else 0
             v1 = 31 if j == 3 else 32
             r0 = 2 * up + i
@@ -229,23 +236,23 @@ def tile_revolutionnaive_kernel(tc, x, conv_w, bn_gamma, bn_beta, bn_mean, bn_va
                     in_=o[p0:p0 + cn, :].rearrange("p (a s) -> p a s", s=64))
 
         make_identity(nc, identF[:])
+        nc.vector.memset(X[:, :, 0:66:65, :], 0.0)
         for q in range(4):
             nc.vector.memset(raw[q][:], 0.0)
+        nc.vector.memset(X[0:4, 0, 1:65, :].rearrange("p r s -> p (r s)").bitcast(F32), 0.0)
+        nc.vector.memset(Wsb[:].rearrange("p k (m o) -> p (k m) o", m=2)[:, :, 0:16], 0.0)
+        for q in range(4):
+            nc.gpsimd.memset(Wraw[0:4, 8 * q:8 * q + 8, :].rearrange("p r f -> p (r f)").bitcast(F32), 0.0)
+        nc.gpsimd.memset(X[0:4, 1, 1:65, :].rearrange("p r s -> p (r s)").bitcast(F32), 0.0)
+
+        load_x(nc.sync, 0, LOWER)
+        load_x(nc.scalar, 0, UPPER)
         for q, vec in enumerate((bn_var, bn_gamma, bn_mean, bn_beta)):
             v2 = vec.rearrange("(c q) -> c q", q=64)
             nc.scalar.dma_start(out=raw[q][4:66, :], in_=v2)
             nc.scalar.dma_start(out=raw[q][66:128, :], in_=v2)
-        nc.vector.memset(X[:, :, 0:66:65, :], 0.0)
-        nc.vector.memset(X[0:4, 0, 1:65, :].rearrange("p r s -> p (r s)").bitcast(F32), 0.0)
-        for k0 in range(0, TAPS, 4):
-            nc.gpsimd.memset(Wsb[0:4, k0:k0 + 4, :].rearrange("p k f -> p (k f)").bitcast(F32), 0.0)
-        nc.gpsimd.memset(X[0:4, 1, 1:65, :].rearrange("p r s -> p (r s)").bitcast(F32), 0.0)
-
-        load_x(nc.sync, 0, LOWER)
-        load_x(nc.sync, 0, UPPER)
-        for k0 in range(0, TAPS, 4):
-            load_w(nc.sync, k0, LOWER + UPPER)
-        load_x(nc.sync, 1, LOWER + UPPER)
+        for q in range(4):
+            load_w(nc.sync, q)
 
         nc.vector.tensor_copy(out=identB[:], in_=identF[:])
         nc.vector.memset(MT[:], 0.0)
@@ -261,21 +268,15 @@ def tile_revolutionnaive_kernel(tc, x, conv_w, bn_gamma, bn_beta, bn_mean, bn_va
         pts = [chan_turn(0, g4, yp, "y") for g4 in range(4)]
         for g4 in range(4):
             chan_reduce(0, g4, pts[g4])
-        for k in range(4):
-            weights(k)
         chan_rows(0)
-        feat_x1(0)
-        for k in range(4, W_FRONT):
+        feat_x1(0, nc.scalar)
+        load_x(nc.sync, 1, LOWER + UPPER)
+        for k in range(TAPS // 2):
             weights(k)
         feat_ft(0, 1, 32)
         feat_ftb(0)
         for vp in range(2):
             feat_g3(0, vp)
-        weights_q(0, 2)
-        for vp in range(2):
-            feat_g2(0, vp)
-        feat_x1(1)
-        feat_q(0)
         nc.vector.reciprocal(out=vv[:], in_=vv[:])
         nc.vector.tensor_mul(out=sfull[:], in0=raw[1][:], in1=vv[:])
         nc.vector.tensor_mul(out=bfull[:], in0=raw[2][:], in1=sfull[:])
@@ -284,6 +285,11 @@ def tile_revolutionnaive_kernel(tc, x, conv_w, bn_gamma, bn_beta, bn_mean, bn_va
             fv = full[:].rearrange("p (k n m) -> p k n m", k=TAPS, n=2, m=2)
             nc.vector.tensor_copy(out=tab[64:128], in_=fv[64:128, :, 1, :])
             nc.vector.tensor_copy(out=tab[0:66], in_=fv[0:66, :, 0, :])
+        weights_q(0, 2)
+        for vp in range(2):
+            feat_g2(0, vp)
+        feat_x1(1, nc.sync)
+        feat_q(0)
         for k in (2, 4):
             weights_q(k, 2)
 
@@ -299,12 +305,12 @@ def tile_revolutionnaive_kernel(tc, x, conv_w, bn_gamma, bn_beta, bn_mean, bn_va
         side[9] = lambda: feat_g2(1, 0)
         side[10] = lambda: feat_g2(1, 1)
         side[11] = lambda: feat_q(1)
-        side[13] = lambda: (feat_e(1, 0, 33), feat_x1(2))
+        side[13] = lambda: (feat_e(1, 0, 33), feat_x1(2, nc.sync))
         side[18] = lambda: feat_ft_turned()
         side[20] = lambda: feat_g3(2, 0)
         side[21] = lambda: feat_g3(2, 1)
         side[23] = lambda: feat_g2(2, 0)
-        side[24] = lambda: (feat_g2(2, 1), feat_x1(3))
+        side[24] = lambda: (feat_g2(2, 1), feat_x1(3, nc.sync))
         side[27] = lambda: feat_q(2)
         side[29] = lambda: feat_g3(3, 0)
         side[32] = lambda: feat_g3(3, 1)
@@ -333,8 +339,6 @@ def tile_revolutionnaive_kernel(tc, x, conv_w, bn_gamma, bn_beta, bn_mean, bn_va
                 turn_back(ats, o, f % TAPS, on_vector=(h >= STEPS and f % TAPS == 1))
                 if f % TAPS == 1:
                     store(f // TAPS, o)
-            if h + W_FRONT < TAPS:
-                weights(h + W_FRONT)
             if 1 <= h <= 4:
                 pts1[h - 1] = chan_turn(1, h - 1, pp, "pp")
             if h == 8:

@@ -41,7 +41,7 @@ def tile_revolutionnaive_kernel(tc, x, conv_w, bn_gamma, bn_beta, bn_mean, bn_va
         Wsb = keep.tile([P, TAPS, 1024], BF16, name="Wsb", align_bytes=64)
         E = keep.tile([P, 2, 33, 66], BF16, name="E")
         FT = keep.tile([P, 2, 33, 66], BF16, name="FT")
-        XT = keep.tile([P, 64, 66], BF16, name="XT")
+        XT = keep.tile([P, 32, 132], BF16, name="XT")
         G = keep.tile([P, 2, 2048], BF16, name="G", align_bytes=64)
         FC = keep.tile([P, 2048], U32, name="FC", align_bytes=64)
         FS = keep.tile([P, 2048], U8, name="FS", align_bytes=64)
@@ -52,7 +52,7 @@ def tile_revolutionnaive_kernel(tc, x, conv_w, bn_gamma, bn_beta, bn_mean, bn_va
         identB = keep.tile([P, P], BF16, name="identB")
         MT = keep.tile([P, P], BF16, name="MT")
         MRp = keep.tile([P, 2, 66], BF16, name="MRp")
-        raw = [keep.tile([P, 64], BF16, name="raw%d" % q) for q in range(4)]
+        raw = keep.tile([P, 4, 64], BF16, name="raw")
         Stab = keep.tile([P, TAPS, 2], F32, name="Stab")
         Btab = keep.tile([P, TAPS, 2], F32, name="Btab")
         vv = keep.tile([P, 64], F32, name="vv")
@@ -74,22 +74,16 @@ def tile_revolutionnaive_kernel(tc, x, conv_w, bn_gamma, bn_beta, bn_mean, bn_va
             xr = X[0:66, b, 2 * u0:2 * u1, :].rearrange("p (u r2) s -> p u r2 s", r2=2)
             nc.vector.tensor_max(out=E[0:66, b, u0:u1, 1:65], in0=xr[:, :, 0, :], in1=xr[:, :, 1, :])
 
-        def feat_ft(b, v0, v1):
-            nc.vector.tensor_max(out=FT[64:128, b, v0:v1, :],
-                                 in0=X[64:128, b, :, 2 * v0 - 1:2 * v1 - 2:2].rearrange("p r v -> p v r"),
-                                 in1=X[64:128, b, :, 2 * v0:2 * v1 - 1:2].rearrange("p r v -> p v r"))
-
-        def feat_ftb(b):
+        def feat_ft(b):
+            xt = XT[64:128].rearrange("p w (r e) -> p w r e", e=2)
+            nc.vector.tensor_max(out=FT[64:128, b, 1:32, :], in0=xt[:, 0:31, :, 1], in1=xt[:, 1:32, :, 0])
             nc.vector.tensor_scalar_max(out=FT[64:128, b, 0:33:32, :],
                                         in0=X[64:128, b, :, 0:64:63].rearrange("p r v -> p v r"), scalar1=0.0)
 
-        def turn_x(c8):
-            nc.scalar.copy(out=XT[64:128, 8 * c8:8 * c8 + 8, :],
-                           in_=X[64:128, 1, :, 8 * c8:8 * c8 + 8].rearrange("p r s -> p s r"))
-
-        def feat_ft_turned():
-            nc.vector.tensor_max(out=FT[64:128, 1, 1:32, :], in0=XT[64:128, 1:62:2, :], in1=XT[64:128, 2:63:2, :])
-            nc.vector.tensor_scalar_max(out=FT[64:128, 1, 0:33:32, :], in0=XT[64:128, 0:64:63, :], scalar1=0.0)
+        def turn_x(b, w0, wn):
+            nc.scalar.copy(out=XT[64:128, w0:w0 + wn, :].bitcast(F32),
+                           in_=X[64:128, b].rearrange("p r s -> p (r s)").bitcast(F32).rearrange(
+                               "p (r w) -> p w r", w=32)[:, w0:w0 + wn, :])
 
         def feat_g3(nt, vp):
             b, up = divmod(nt, 2)
@@ -236,9 +230,9 @@ def tile_revolutionnaive_kernel(tc, x, conv_w, bn_gamma, bn_beta, bn_mean, bn_va
                     in_=o[p0:p0 + cn, :].rearrange("p (a s) -> p a s", s=64))
 
         make_identity(nc, identF[:])
+        nc.vector.memset(vv[:, 0:1], 1.0)
         nc.vector.memset(X[:, :, 0:66:65, :], 0.0)
-        for q in range(4):
-            nc.vector.memset(raw[q][:], 0.0)
+        nc.vector.memset(raw[:], 0.0)
         nc.vector.memset(X[0:4, 0, 1:65, :].rearrange("p r s -> p (r s)").bitcast(F32), 0.0)
         nc.vector.memset(Wsb[:].rearrange("p k (m o) -> p (k m) o", m=2)[:, :, 0:16], 0.0)
         for q in range(4):
@@ -247,12 +241,12 @@ def tile_revolutionnaive_kernel(tc, x, conv_w, bn_gamma, bn_beta, bn_mean, bn_va
 
         load_x(nc.sync, 0, LOWER)
         load_x(nc.scalar, 0, UPPER)
+        nc.scalar.sqrt(out=vv[:, 0:1], in_=vv[:, 0:1])
+        load_w(nc.sync, 0)
         for q, vec in enumerate((bn_var, bn_gamma, bn_mean, bn_beta)):
-            v2 = vec.rearrange("(c q) -> c q", q=64)
-            nc.scalar.dma_start(out=raw[q][4:66, :], in_=v2)
-            nc.scalar.dma_start(out=raw[q][66:128, :], in_=v2)
-        for q in range(4):
-            load_w(nc.sync, q)
+            queue = nc.scalar if q < 2 else nc.sync
+            queue.dma_start(out=raw[4:66, q, :], in_=vec.rearrange("(c q) -> c q", q=64))
+        load_w(nc.sync, 1)
 
         nc.vector.tensor_copy(out=identB[:], in_=identF[:])
         nc.vector.memset(MT[:], 0.0)
@@ -262,33 +256,38 @@ def tile_revolutionnaive_kernel(tc, x, conv_w, bn_gamma, bn_beta, bn_mean, bn_va
             nc.vector.memset(tbuf[j][:, :, :].rearrange("p m (a v) -> p m a v", v=32)[:, :, :, 0:1], 0.0)
             nc.vector.memset(tbuf[j + 3][:, :, :].rearrange("p m (a v) -> p m a v", v=32)[:, :, :, 31:32], 0.0)
 
-        nc.vector.tensor_scalar_add(out=vv[:], in0=raw[0][:], scalar1=BN_EPS)
-        nc.scalar.sqrt(out=vv[:], in_=vv[:])
+        for w0 in range(0, 32, 16):
+            turn_x(0, w0, 16)
         feat_e(0, 0, 33)
         pts = [chan_turn(0, g4, yp, "y") for g4 in range(4)]
         for g4 in range(4):
             chan_reduce(0, g4, pts[g4])
         chan_rows(0)
         feat_x1(0, nc.scalar)
+        load_w(nc.sync, 2)
+        nc.sync.dma_start(out=raw[66:128], in_=raw[4:66])
+        load_w(nc.sync, 3)
         load_x(nc.sync, 1, LOWER + UPPER)
-        for k in range(TAPS // 2):
-            weights(k)
-        feat_ft(0, 1, 32)
-        feat_ftb(0)
+        feat_ft(0)
         for vp in range(2):
             feat_g3(0, vp)
-        nc.vector.reciprocal(out=vv[:], in_=vv[:])
-        nc.vector.tensor_mul(out=sfull[:], in0=raw[1][:], in1=vv[:])
-        nc.vector.tensor_mul(out=bfull[:], in0=raw[2][:], in1=sfull[:])
-        nc.vector.tensor_sub(out=bfull[:], in0=raw[3][:], in1=bfull[:])
-        for tab, full in ((Stab, sfull), (Btab, bfull)):
-            fv = full[:].rearrange("p (k n m) -> p k n m", k=TAPS, n=2, m=2)
-            nc.vector.tensor_copy(out=tab[64:128], in_=fv[64:128, :, 1, :])
-            nc.vector.tensor_copy(out=tab[0:66], in_=fv[0:66, :, 0, :])
+        nc.vector.tensor_scalar_add(out=vv[:], in0=raw[:, 0, :], scalar1=BN_EPS)
+        for k in range(TAPS // 2):
+            weights(k)
+            if k == 4:
+                nc.scalar.sqrt(out=vv[:], in_=vv[:])
         weights_q(0, 2)
         for vp in range(2):
             feat_g2(0, vp)
         feat_x1(1, nc.sync)
+        nc.vector.reciprocal(out=vv[:], in_=vv[:])
+        nc.vector.tensor_mul(out=sfull[:], in0=raw[:, 1, :], in1=vv[:])
+        nc.vector.tensor_mul(out=bfull[:], in0=raw[:, 2, :], in1=sfull[:])
+        nc.vector.tensor_sub(out=bfull[:], in0=raw[:, 3, :], in1=bfull[:])
+        for tab, full in ((Stab, sfull), (Btab, bfull)):
+            fv = full[:].rearrange("p (k n m) -> p k n m", k=TAPS, n=2, m=2)
+            nc.vector.tensor_copy(out=tab[64:128], in_=fv[64:128, :, 1, :])
+            nc.vector.tensor_copy(out=tab[0:66], in_=fv[0:66, :, 0, :])
         feat_q(0)
         for k in (2, 4):
             weights_q(k, 2)
@@ -306,7 +305,7 @@ def tile_revolutionnaive_kernel(tc, x, conv_w, bn_gamma, bn_beta, bn_mean, bn_va
         side[10] = lambda: feat_g2(1, 1)
         side[11] = lambda: feat_q(1)
         side[13] = lambda: (feat_e(1, 0, 33), feat_x1(2, nc.sync))
-        side[18] = lambda: feat_ft_turned()
+        side[18] = lambda: feat_ft(1)
         side[20] = lambda: feat_g3(2, 0)
         side[21] = lambda: feat_g3(2, 1)
         side[23] = lambda: feat_g2(2, 0)
@@ -325,7 +324,7 @@ def tile_revolutionnaive_kernel(tc, x, conv_w, bn_gamma, bn_beta, bn_mean, bn_va
             if h < STEPS:
                 zs[h] = mx_act(h)
             if 2 <= h <= 16 and h % 2 == 0:
-                turn_x(h // 2 - 1)
+                turn_x(1, 2 * h - 4, 4)
             g = h - LAG
             if 0 <= g < STEPS:
                 if g % TAPS == 0:

@@ -41,7 +41,7 @@ def tile_revolutionnaive_kernel(tc, x, conv_w, bn_gamma, bn_beta, bn_mean, bn_va
         Wsb = keep.tile([P, TAPS, 1024], BF16, name="Wsb", align_bytes=64)
         E = keep.tile([P, 2, 33, 66], BF16, name="E")
         FT = keep.tile([P, 2, 33, 66], BF16, name="FT")
-        XT = keep.tile([P, 32, 132], BF16, name="XT")
+        XT = keep.tile([P, 64, 66], BF16, name="XT")
         G = keep.tile([P, 2, 2048], BF16, name="G", align_bytes=64)
         FC = keep.tile([P, 2048], U32, name="FC", align_bytes=64)
         FS = keep.tile([P, 2048], U8, name="FS", align_bytes=64)
@@ -74,23 +74,31 @@ def tile_revolutionnaive_kernel(tc, x, conv_w, bn_gamma, bn_beta, bn_mean, bn_va
             xr = X[0:66, b, 2 * u0:2 * u1, :].rearrange("p (u r2) s -> p u r2 s", r2=2)
             nc.vector.tensor_max(out=E[0:66, b, u0:u1, 1:65], in0=xr[:, :, 0, :], in1=xr[:, :, 1, :])
 
-        def feat_ft(b):
-            xt = XT[64:128].rearrange("p w (r e) -> p w r e", e=2)
-            nc.vector.tensor_max(out=FT[64:128, b, 1:32, :], in0=xt[:, 0:31, :, 1], in1=xt[:, 1:32, :, 0])
-            nc.vector.tensor_scalar_max(out=FT[64:128, b, 0:33:32, :],
-                                        in0=X[64:128, b, :, 0:64:63].rearrange("p r v -> p v r"), scalar1=0.0)
+        def feat_ft_words():
+            xt = XT[:].rearrange("p s r -> p (s r)").rearrange("p (w r e) -> p w r e", w=32, e=2)
+            nc.vector.tensor_max(out=FT[:, 0, 1:32, :], in0=xt[:, 0:31, :, 1], in1=xt[:, 1:32, :, 0])
 
-        def turn_x(b, w0, wn):
-            nc.scalar.copy(out=XT[64:128, w0:w0 + wn, :].bitcast(F32),
-                           in_=X[64:128, b].rearrange("p r s -> p (r s)").bitcast(F32).rearrange(
-                               "p (r w) -> p w r", w=32)[:, w0:w0 + wn, :])
+        def feat_ft():
+            nc.vector.tensor_max(out=FT[:, 1, 1:32, :], in0=XT[:, 1:62:2, :], in1=XT[:, 2:63:2, :])
+
+        def feat_ftb(b):
+            nc.scalar.activation(out=FT[:, b, 0:33:32, :], in_=X[:, b, :, 0:64:63].rearrange("p r v -> p v r"), func=ACT.Relu)
+
+        def turn_words(w0):
+            nc.scalar.copy(out=XT[:, 2 * w0:2 * w0 + 32, :].rearrange("p s r -> p (s r)").bitcast(F32).rearrange("p (w r) -> p w r", w=16),
+                           in_=X[:, 0].rearrange("p r s -> p (r s)").bitcast(F32).rearrange(
+                               "p (r w) -> p w r", w=32)[:, w0:w0 + 16, :])
+
+        def turn_x(c8):
+            nc.scalar.copy(out=XT[:, 8 * c8:8 * c8 + 8, :],
+                           in_=X[:, 1, :, 8 * c8:8 * c8 + 8].rearrange("p r s -> p s r"))
 
         def feat_g3(nt, vp):
             b, up = divmod(nt, 2)
             nc.vector.tensor_max(
-                out=G[64:128, nt % 2, vp * 1024:(vp + 1) * 1024].rearrange("p (a w i) -> p a w i", a=16, w=16, i=4),
-                in0=FT[64:128, b, vp:vp + 31:2, 2 * up:2 * up + 64].rearrange("p w (a i) -> p a w i", i=4),
-                in1=FT[64:128, b, vp + 1:vp + 32:2, 2 * up:2 * up + 64].rearrange("p w (a i) -> p a w i", i=4))
+                out=G[:, nt % 2, vp * 1024:(vp + 1) * 1024].rearrange("p (a w i) -> p a w i", a=16, w=16, i=4),
+                in0=FT[:, b, vp:vp + 31:2, 2 * up:2 * up + 64].rearrange("p w (a i) -> p a w i", i=4),
+                in1=FT[:, b, vp + 1:vp + 32:2, 2 * up:2 * up + 64].rearrange("p w (a i) -> p a w i", i=4))
 
         def feat_g2(nt, vp):
             b, up = divmod(nt, 2)
@@ -257,7 +265,8 @@ def tile_revolutionnaive_kernel(tc, x, conv_w, bn_gamma, bn_beta, bn_mean, bn_va
             nc.vector.memset(tbuf[j + 3][:, :, :].rearrange("p m (a v) -> p m a v", v=32)[:, :, :, 31:32], 0.0)
 
         for w0 in range(0, 32, 16):
-            turn_x(0, w0, 16)
+            turn_words(w0)
+        feat_ftb(0)
         feat_e(0, 0, 33)
         pts = [chan_turn(0, g4, yp, "y") for g4 in range(4)]
         for g4 in range(4):
@@ -268,7 +277,7 @@ def tile_revolutionnaive_kernel(tc, x, conv_w, bn_gamma, bn_beta, bn_mean, bn_va
         nc.sync.dma_start(out=raw[66:128], in_=raw[4:66])
         load_w(nc.sync, 3)
         load_x(nc.sync, 1, LOWER + UPPER)
-        feat_ft(0)
+        feat_ft_words()
         for vp in range(2):
             feat_g3(0, vp)
         nc.vector.tensor_scalar_add(out=vv[:], in0=raw[:, 0, :], scalar1=BN_EPS)
@@ -305,7 +314,7 @@ def tile_revolutionnaive_kernel(tc, x, conv_w, bn_gamma, bn_beta, bn_mean, bn_va
         side[10] = lambda: feat_g2(1, 1)
         side[11] = lambda: feat_q(1)
         side[13] = lambda: (feat_e(1, 0, 33), feat_x1(2, nc.sync))
-        side[18] = lambda: feat_ft(1)
+        side[18] = lambda: feat_ft()
         side[20] = lambda: feat_g3(2, 0)
         side[21] = lambda: feat_g3(2, 1)
         side[23] = lambda: feat_g2(2, 0)
@@ -324,7 +333,9 @@ def tile_revolutionnaive_kernel(tc, x, conv_w, bn_gamma, bn_beta, bn_mean, bn_va
             if h < STEPS:
                 zs[h] = mx_act(h)
             if 2 <= h <= 16 and h % 2 == 0:
-                turn_x(1, 2 * h - 4, 4)
+                turn_x(h // 2 - 1)
+            if h == 17:
+                feat_ftb(1)
             g = h - LAG
             if 0 <= g < STEPS:
                 if g % TAPS == 0:

@@ -17,7 +17,7 @@ TAPS = 16
 FLOPS = 2 * 3968 * 512 * 2048
 BN_EPS = 1e-5
 STEPS = 4 * TAPS
-LAG = 5
+LAG = 6
 RING = 12
 ORDER = [0, 1, 2, 3, 8, 9, 10, 11, 4, 5, 6, 7, 12, 13, 14, 15]
 
@@ -329,9 +329,11 @@ def tile_revolutionnaive_kernel(tc, x, conv_w, bn_gamma, bn_beta, bn_mean, bn_va
         zs = {}
         accs = {}
         done = {}
-        for h in range(STEPS + LAG + 3):
-            if h < STEPS:
-                zs[h] = mx_act(h)
+        for h in range(STEPS + LAG + 2):
+            if h % 2 == 0:
+                for s in (h, h + 1):
+                    if s < STEPS:
+                        zs[s] = mx_act(s)
             if 2 <= h <= 16 and h % 2 == 0:
                 turn_x(h // 2 - 1)
             if h == 17:

@@ -17,7 +17,7 @@ TAPS = 16
 FLOPS = 2 * 3968 * 512 * 2048
 BN_EPS = 1e-5
 STEPS = 4 * TAPS
-LAG = 6
+LAG = 5
 RING = 12
 ORDER = [0, 1, 2, 3, 8, 9, 10, 11, 4, 5, 6, 7, 12, 13, 14, 15]
 
@@ -53,8 +53,6 @@ def tile_revolutionnaive_kernel(tc, x, conv_w, bn_gamma, bn_beta, bn_mean, bn_va
         MT = keep.tile([P, P], BF16, name="MT")
         MRp = keep.tile([P, 2, 66], BF16, name="MRp")
         raw = keep.tile([P, 4, 64], BF16, name="raw")
-        Stab = keep.tile([P, TAPS, 2], F32, name="Stab")
-        Btab = keep.tile([P, TAPS, 2], F32, name="Btab")
         vv = keep.tile([P, 64], F32, name="vv")
         sfull = keep.tile([P, 64], F32, name="sfull")
         bfull = keep.tile([P, 64], F32, name="bfull")
@@ -78,8 +76,8 @@ def tile_revolutionnaive_kernel(tc, x, conv_w, bn_gamma, bn_beta, bn_mean, bn_va
             xt = XT[:].rearrange("p s r -> p (s r)").rearrange("p (w r e) -> p w r e", w=32, e=2)
             nc.vector.tensor_max(out=FT[:, 0, 1:32, :], in0=xt[:, 0:31, :, 1], in1=xt[:, 1:32, :, 0])
 
-        def feat_ft():
-            nc.vector.tensor_max(out=FT[:, 1, 1:32, :], in0=XT[:, 1:62:2, :], in1=XT[:, 2:63:2, :])
+        def feat_ft(v0, v1):
+            nc.vector.tensor_max(out=FT[:, 1, v0:v1, :], in0=XT[:, 2 * v0 - 1:2 * v1 - 2:2, :], in1=XT[:, 2 * v0:2 * v1 - 1:2, :])
 
         def feat_ftb(b):
             nc.scalar.activation(out=FT[:, b, 0:33:32, :], in_=X[:, b, :, 0:64:63].rearrange("p r v -> p v r"), func=ACT.Relu)
@@ -176,7 +174,7 @@ def tile_revolutionnaive_kernel(tc, x, conv_w, bn_gamma, bn_beta, bn_mean, bn_va
             for m in range(2):
                 nc.scalar.activation(out=z[:, m, :].rearrange("p (r vp) -> p r vp", vp=2),
                                      in_=ys[m][:].rearrange("p (vp r) -> p r vp", vp=2), func=ACT.Relu,
-                                     bias=Btab[:, k, m:m + 1], scale=Stab[:, k, m:m + 1])
+                                     bias=bfull[:, 4 * k + m:4 * k + m + 1], scale=sfull[:, 4 * k + m:4 * k + m + 1])
             return z
 
         def mul(h, z):
@@ -229,13 +227,13 @@ def tile_revolutionnaive_kernel(tc, x, conv_w, bn_gamma, bn_beta, bn_mean, bn_va
             else:
                 nc.scalar.copy(out=dst, in_=src)
 
-        def store(nt, o):
+        def store(nt, o, a0, an):
             b, up = divmod(nt, 2)
             for (p0, c0, cn, n) in LOWER + UPPER:
                 queue = nc.scalar if (nt == 3 and n == 1) else nc.sync
                 queue.dma_start(
-                    out=out[b, c0:c0 + cn].rearrange("c (a r) s -> c a r s", r=4)[:, :, 2 * up + n, :],
-                    in_=o[p0:p0 + cn, :].rearrange("p (a s) -> p a s", s=64))
+                    out=out[b, c0:c0 + cn].rearrange("c (a r) s -> c a r s", r=4)[:, a0:a0 + an, 2 * up + n, :],
+                    in_=o[p0:p0 + cn, a0 * 64:(a0 + an) * 64].rearrange("p (a s) -> p a s", s=64))
 
         make_identity(nc, identF[:])
         nc.vector.memset(vv[:, 0:1], 1.0)
@@ -274,52 +272,49 @@ def tile_revolutionnaive_kernel(tc, x, conv_w, bn_gamma, bn_beta, bn_mean, bn_va
         chan_rows(0)
         feat_x1(0, nc.scalar)
         load_w(nc.sync, 2)
-        nc.sync.dma_start(out=raw[66:128], in_=raw[4:66])
+        nc.sync.dma_start(out=raw[66:128, :, 0:62], in_=raw[4:66, :, 2:64])
         load_w(nc.sync, 3)
         load_x(nc.sync, 1, LOWER + UPPER)
         feat_ft_words()
         for vp in range(2):
             feat_g3(0, vp)
-        nc.vector.tensor_scalar_add(out=vv[:], in0=raw[:, 0, :], scalar1=BN_EPS)
         for k in range(TAPS // 2):
             weights(k)
             if k == 4:
-                nc.scalar.sqrt(out=vv[:], in_=vv[:])
+                nc.scalar.activation(out=vv[:], in_=raw[:, 0, :], func=ACT.Sqrt, bias=BN_EPS)
         weights_q(0, 2)
         for vp in range(2):
             feat_g2(0, vp)
         feat_x1(1, nc.sync)
+        feat_q(0)
         nc.vector.reciprocal(out=vv[:], in_=vv[:])
         nc.vector.tensor_mul(out=sfull[:], in0=raw[:, 1, :], in1=vv[:])
         nc.vector.tensor_mul(out=bfull[:], in0=raw[:, 2, :], in1=sfull[:])
         nc.vector.tensor_sub(out=bfull[:], in0=raw[:, 3, :], in1=bfull[:])
-        for tab, full in ((Stab, sfull), (Btab, bfull)):
-            fv = full[:].rearrange("p (k n m) -> p k n m", k=TAPS, n=2, m=2)
-            nc.vector.tensor_copy(out=tab[64:128], in_=fv[64:128, :, 1, :])
-            nc.vector.tensor_copy(out=tab[0:66], in_=fv[0:66, :, 0, :])
-        feat_q(0)
-        for k in (2, 4):
+        for k in (2, 4, 6):
             weights_q(k, 2)
+        weights_q(8, 4)
 
         pts1 = {}
         side = {}
-        side[0] = lambda: weights_q(6, 2)
         for g4 in range(4):
             side[1 + g4] = lambda g4=g4: chan_reduce(1, g4, pts1[g4])
-        side[5] = lambda: weights_q(8, 4)
+        side[0] = lambda: weights_q(12, 2)
+        side[5] = lambda: weights_q(14, 2)
         side[6] = lambda: feat_g3(1, 0)
         side[7] = lambda: feat_g3(1, 1)
-        side[8] = lambda: weights_q(12, 4)
-        side[9] = lambda: feat_g2(1, 0)
-        side[10] = lambda: feat_g2(1, 1)
-        side[11] = lambda: feat_q(1)
-        side[13] = lambda: (feat_e(1, 0, 33), feat_x1(2, nc.sync))
-        side[18] = lambda: feat_ft()
+        side[8] = lambda: feat_g2(1, 0)
+        side[9] = lambda: feat_g2(1, 1)
+        side[10] = lambda: feat_q(1)
+        side[12] = lambda: feat_e(1, 0, 17)
+        side[13] = lambda: (feat_e(1, 17, 33), feat_x1(2, nc.sync))
+        side[17] = lambda: feat_ft(1, 16)
+        side[18] = lambda: feat_ft(16, 32)
         side[20] = lambda: feat_g3(2, 0)
         side[21] = lambda: feat_g3(2, 1)
         side[23] = lambda: feat_g2(2, 0)
         side[24] = lambda: (feat_g2(2, 1), feat_x1(3, nc.sync))
-        side[27] = lambda: feat_q(2)
+        side[26] = lambda: feat_q(2)
         side[29] = lambda: feat_g3(3, 0)
         side[32] = lambda: feat_g3(3, 1)
         side[35] = lambda: feat_g2(3, 0)
@@ -329,14 +324,12 @@ def tile_revolutionnaive_kernel(tc, x, conv_w, bn_gamma, bn_beta, bn_mean, bn_va
         zs = {}
         accs = {}
         done = {}
-        for h in range(STEPS + LAG + 2):
-            if h % 2 == 0:
-                for s in (h, h + 1):
-                    if s < STEPS:
-                        zs[s] = mx_act(s)
+        for h in range(STEPS + LAG + 3):
+            if h < STEPS:
+                zs[h] = mx_act(h)
             if 2 <= h <= 16 and h % 2 == 0:
                 turn_x(h // 2 - 1)
-            if h == 17:
+            if h == 15:
                 feat_ftb(1)
             g = h - LAG
             if 0 <= g < STEPS:
@@ -348,9 +341,12 @@ def tile_revolutionnaive_kernel(tc, x, conv_w, bn_gamma, bn_beta, bn_mean, bn_va
             f = h - LAG - TAPS
             if f >= 0 and f % TAPS in (0, 1):
                 ats, o = done[f // TAPS]
-                turn_back(ats, o, f % TAPS, on_vector=(h >= STEPS and f % TAPS == 1))
-                if f % TAPS == 1:
-                    store(f // TAPS, o)
+                ah = f % TAPS
+                turn_back(ats, o, ah, on_vector=(h >= STEPS and ah == 1))
+                if f // TAPS == 3:
+                    store(3, o, 8 * ah, 8)
+                elif ah == 1:
+                    store(f // TAPS, o, 0, 16)
             if 1 <= h <= 4:
                 pts1[h - 1] = chan_turn(1, h - 1, pp, "pp")
             if h == 8:

from contextlib import ExitStack

import concourse.mybir as mybir
from concourse.masks import make_identity

F32 = mybir.dt.float32
BF16 = mybir.dt.bfloat16
U32 = mybir.dt.uint32
U8 = mybir.dt.uint8
FP8X4 = mybir.dt.float8_e4m3fn_x4
ACT = mybir.ActivationFunctionType
ALU = mybir.AluOpType

P = 128
C = 62
TAPS = 16
FLOPS = 2 * 3968 * 512 * 2048
BN_EPS = 1e-5
STEPS = 4 * TAPS
LAG = 5
RING = 12
ORDER = [0, 1, 2, 3, 8, 9, 10, 11, 4, 5, 6, 7, 12, 13, 14, 15]

LOWER = [(4, 0, 32, 0), (36, 32, 30, 0)]
UPPER = [(66, 0, 32, 1), (98, 32, 30, 1)]


def tile_revolutionnaive_kernel(tc, x, conv_w, bn_gamma, bn_beta, bn_mean, bn_var, out):
    nc = tc.nc
    with ExitStack() as ctx:
        keep = ctx.enter_context(tc.tile_pool(name="keep", bufs=1))
        zp = ctx.enter_context(tc.tile_pool(name="zp", bufs=6))
        atp = ctx.enter_context(tc.tile_pool(name="atp", bufs=4))
        op = ctx.enter_context(tc.tile_pool(name="op", bufs=2))
        yp = ctx.enter_context(tc.psum_pool(name="yp", bufs=4))
        pp = ctx.enter_context(tc.psum_pool(name="pp", bufs=4))
        ctx.enter_context(tc.manual_schedule())

        X = keep.tile([P, 2, 66, 64], BF16, name="X")
        Wraw = keep.tile([P, 32, 512], BF16, name="Wraw", align_bytes=64)
        Wsb = keep.tile([P, TAPS, 1024], BF16, name="Wsb", align_bytes=64)
        E = keep.tile([P, 2, 33, 66], BF16, name="E")
        FT = keep.tile([P, 2, 33, 66], BF16, name="FT")
        XT = keep.tile([P, 64, 66], BF16, name="XT")
        G = keep.tile([P, 2, 2048], BF16, name="G", align_bytes=64)
        FC = keep.tile([P, 2048], U32, name="FC", align_bytes=64)
        FS = keep.tile([P, 2048], U8, name="FS", align_bytes=64)
        WC = keep.tile([P, 4096], U32, name="WC", align_bytes=64)
        WS = keep.tile([P, 4096], U8, name="WS", align_bytes=64)
        tbuf = [keep.tile([P, 2, 512], F32, name="t%d" % j) for j in range(RING)]
        identF = keep.tile([P, P], F32, name="identF")
        identB = keep.tile([P, P], BF16, name="identB")
        MT = keep.tile([P, P], BF16, name="MT")
        MRp = keep.tile([P, 2, 66], BF16, name="MRp")
        raw = keep.tile([P, 4, 64], BF16, name="raw")
        vv = keep.tile([P, 64], F32, name="vv")
        sfull = keep.tile([P, 64], F32, name="sfull")
        bfull = keep.tile([P, 64], F32, name="bfull")

        w32 = conv_w.rearrange("(p r) f -> p (r f)", r=32)

        def load_x(queue, b, ranges):
            for (p0, c0, cn, n) in ranges:
                queue.dma_start(out=X[p0:p0 + cn, b, 1:65, :], in_=x[b, c0:c0 + cn])

        def load_w(queue, q):
            for (p0, pn) in ((0, 112), (112, 12)):
                queue.dma_start(out=Wraw[4 + p0:4 + p0 + pn, 8 * q:8 * q + 8, :].rearrange("p r f -> p (r f)"),
                                in_=w32[p0:p0 + pn, 4096 * q:4096 * q + 4096])

        def feat_e(b, u0, u1):
            xr = X[0:66, b, 2 * u0:2 * u1, :].rearrange("p (u r2) s -> p u r2 s", r2=2)
            nc.vector.tensor_max(out=E[0:66, b, u0:u1, 1:65], in0=xr[:, :, 0, :], in1=xr[:, :, 1, :])

        def feat_ft_words():
            xt = XT[:].rearrange("p s r -> p (s r)").rearrange("p (w r e) -> p w r e", w=32, e=2)
            nc.vector.tensor_max(out=FT[:, 0, 1:32, :], in0=xt[:, 0:31, :, 1], in1=xt[:, 1:32, :, 0])

        def feat_ft(v0, v1):
            nc.vector.tensor_max(out=FT[:, 1, v0:v1, :], in0=XT[:, 2 * v0 - 1:2 * v1 - 2:2, :], in1=XT[:, 2 * v0:2 * v1 - 1:2, :])

        def feat_ftb(b):
            nc.scalar.activation(out=FT[:, b, 0:33:32, :], in_=X[:, b, :, 0:64:63].rearrange("p r v -> p v r"), func=ACT.Relu)

        def turn_words(w0):
            nc.scalar.copy(out=XT[:, 2 * w0:2 * w0 + 32, :].rearrange("p s r -> p (s r)").bitcast(F32).rearrange("p (w r) -> p w r", w=16),
                           in_=X[:, 0].rearrange("p r s -> p (r s)").bitcast(F32).rearrange(
                               "p (r w) -> p w r", w=32)[:, w0:w0 + 16, :])

        def turn_x(c8):
            nc.scalar.copy(out=XT[:, 8 * c8:8 * c8 + 8, :],
                           in_=X[:, 1, :, 8 * c8:8 * c8 + 8].rearrange("p r s -> p s r"))

        def feat_g3(nt, vp):
            b, up = divmod(nt, 2)
            nc.vector.tensor_max(
                out=G[:, nt % 2, vp * 1024:(vp + 1) * 1024].rearrange("p (a w i) -> p a w i", a=16, w=16, i=4),
                in0=FT[:, b, vp:vp + 31:2, 2 * up:2 * up + 64].rearrange("p w (a i) -> p a w i", i=4),
                in1=FT[:, b, vp + 1:vp + 32:2, 2 * up:2 * up + 64].rearrange("p w (a i) -> p a w i", i=4))

        def feat_g2(nt, vp):
            b, up = divmod(nt, 2)
            nc.vector.tensor_max(
                out=G[0:66, nt % 2, vp * 1024:(vp + 1) * 1024].rearrange("p (a s) -> p a s", a=16, s=64),
                in0=E[0:66, b, up:up + 31:2, 2 * vp:2 * vp + 64],
                in1=E[0:66, b, up + 1:up + 32:2, 2 * vp:2 * vp + 64])

        def feat_x1(nt, queue):
            b, up = divmod(nt, 2)
            for i in range(4):
                d = 2 * up + i - 1
                p0 = 1 + 64 * b + d // 2
                queue.dma_start(out=E[i:i + 1, b, up:up + 32, :],
                                  in_=MRp[p0:p0 + 31:2, d % 2, :].unsqueeze(1).to_broadcast([16, 2, 66]))

        def feat_q(nt):
            nc.vector.quantize_mx(out=FC[:, nt * 512:(nt + 1) * 512].bitcast(FP8X4),
                                  scales=FS[:, nt * 512:(nt + 1) * 512], in_=G[:, nt % 2, :])

        def chan_turn(b, g4, pool, tag):
            pt = pool.tile([P, 1024], BF16, name="pt", tag=tag)
            for jj in range(8):
                j = 8 * g4 + jj
                nc.tensor.transpose(out=pt[:, jj * 128:(jj + 1) * 128],
                                    in_=X[:, b, 1 + 2 * j:3 + 2 * j, :].rearrange("p r s -> p (r s)"), identity=identB[:])
            return pt

        def chan_reduce(b, g4, pt):
            c0 = 1 + 64 * b + 8 * g4
            nc.vector.tensor_reduce(out=MT[:, c0:c0 + 8], in_=pt[:].rearrange("p (j c) -> p j c", c=128)[:, :, 4:66],
                                    axis=mybir.AxisListType.X, op=ALU.max)

        def chan_rows(b):
            pm = pp.tile([P, P], BF16, name="pm", tag="pp")
            nc.tensor.transpose(out=pm[:], in_=MT[:], identity=identB[:])
            nc.scalar.copy(out=MRp[64 * b:64 * b + 64, :, 1:65],
                           in_=pm[64 * b:64 * b + 64, :].rearrange("p (rp s) -> p rp s", rp=2))

        def weights(k):
            for m in range(2):
                wt = pp.tile([P, 512], F32, name="wt", tag="pp")
                for n in range(2):
                    words = Wraw[:, 4 * k + 2 * n + m, :].bitcast(F32)
                    for e in range(2):
                        q = 2 * n + e
                        nc.tensor.transpose(out=wt[:, q * 128:(q + 1) * 128], in_=words[:, e:256:2],
                                            identity=identF[:])
                for t in range(2):
                    s = ORDER.index(k + 8 * t)
                    nc.scalar.copy(
                        out=Wsb[:, s, m * 512 + 16:(m + 1) * 512].bitcast(F32).rearrange("p (n c e) -> p n c e", n=2, e=2),
                        in_=wt[:].rearrange("p (n e q) -> p n q e", n=2, e=2)[:, :, 4 + t:128:2, :])

        def weights_q(s, n):
            nc.vector.quantize_mx(out=WC[:, s * 256:(s + n) * 256].bitcast(FP8X4),
                                  scales=WS[:, s * 256:(s + n) * 256],
                                  in_=Wsb[:, s:s + n, :].rearrange("p k f -> p (k f)"))

        def mx_act(h):
            nt, s = divmod(h, TAPS)
            k = ORDER[s]
            z = zp.tile([P, 2, 512], F32, name="z")
            ys = []
            for m in range(2):
                tl = 2 * s + m
                y = yp.tile([P, 512], F32, name="y")
                nc.tensor.matmul_mx(out=y[:],
                                    lhsT=WC[:, tl * 128:(tl + 1) * 128].bitcast(FP8X4),
                                    lhsT_scale=WS[:, tl * 128:(tl + 1) * 128],
                                    rhs=FC[:, nt * 512:(nt + 1) * 512].bitcast(FP8X4),
                                    rhs_scale=FS[:, nt * 512:(nt + 1) * 512],
                                    start=True, stop=True)
                ys.append(y)
            for m in range(2):
                nc.scalar.activation(out=z[:, m, :].rearrange("p (r vp) -> p r vp", vp=2),
                                     in_=ys[m][:].rearrange("p (vp r) -> p r vp", vp=2), func=ACT.Relu,
                                     bias=bfull[:, 4 * k + m:4 * k + m + 1], scale=sfull[:, 4 * k + m:4 * k + m + 1])
            return z

        def mul(h, z):
            nt, s = divmod(h, TAPS)
            b, up = divmod(nt, 2)
            i, j = divmod(ORDER[s], 4)
            v0 = 1 if j == 0 else 0
            v1 = 31 if j == 3 else 32
            r0 = 2 * up + i
            c0 = j - 1
            patch = X[:, b, r0:r0 + 61:4, c0 + 2 * v0:c0 + 2 * (v1 - 1) + 1:2]
            nc.vector.tensor_mul(
                out=tbuf[h % RING][:, :, :].rearrange("p m (a v) -> p m a v", v=32)[:, :, :, v0:v1],
                in0=z[:, :, :].rearrange("p m (a v) -> p m a v", v=32)[:, :, :, v0:v1],
                in1=patch.unsqueeze(1).to_broadcast([P, 2, 16, v1 - v0]))

        def add_up(h, acc):
            k = h % TAPS
            src = tbuf[h % RING]
            for m in range(2):
                for blk in range(4):
                    nc.tensor.matmul(out=acc[m][:, blk * 128:(blk + 1) * 128],
                                     lhsT=src[:, m, blk * 128:(blk + 1) * 128],
                                     rhs=identF[:], is_transpose=True,
                                     start=(k == 0 and blk == 0), stop=(k == TAPS - 1 and blk == 3))

        def leave_psum(acc, last):
            ats = []
            for m in range(2):
                at = atp.tile([P, 512], F32, name="at")
                if last and m == 1:
                    nc.vector.tensor_scalar_mul(out=at[:], in0=acc[m][:], scalar1=1.0 / TAPS)
                else:
                    nc.scalar.mul(out=at[:], in_=acc[m][:], mul=1.0 / TAPS)
                ats.append(at)
            return ats

        def turn_back(ats, o, ah, on_vector):
            fb = pp.tile([P, 512], F32, name="fb", tag="pp")
            for m in range(2):
                for bl in range(2):
                    q = 2 * m + bl
                    blk = 2 * ah + bl
                    nc.tensor.transpose(out=fb[:, q * 128:(q + 1) * 128],
                                        in_=ats[m][:, blk * 128:(blk + 1) * 128], identity=identF[:])
            dst = o[:, ah * 512:(ah + 1) * 512].rearrange("p (r m) -> p r m", m=2)
            src = fb[:].rearrange("p (m r) -> p r m", m=2)
            if on_vector:
                nc.vector.tensor_copy(out=dst, in_=src)
            else:
                nc.scalar.copy(out=dst, in_=src)

        def store(nt, o, a0, an):
            b, up = divmod(nt, 2)
            for (p0, c0, cn, n) in LOWER + UPPER:
                queue = nc.scalar if (nt == 3 and n == 1) else nc.sync
                queue.dma_start(
                    out=out[b, c0:c0 + cn].rearrange("c (a r) s -> c a r s", r=4)[:, a0:a0 + an, 2 * up + n, :],
                    in_=o[p0:p0 + cn, a0 * 64:(a0 + an) * 64].rearrange("p (a s) -> p a s", s=64))

        make_identity(nc, identF[:])
        nc.vector.memset(vv[:, 0:1], 1.0)
        nc.vector.memset(X[:, :, 0:66:65, :], 0.0)
        nc.vector.memset(raw[:], 0.0)
        nc.vector.memset(X[0:4, 0, 1:65, :].rearrange("p r s -> p (r s)").bitcast(F32), 0.0)
        nc.vector.memset(Wsb[:].rearrange("p k (m o) -> p (k m) o", m=2)[:, :, 0:16], 0.0)
        for q in range(4):
            nc.gpsimd.memset(Wraw[0:4, 8 * q:8 * q + 8, :].rearrange("p r f -> p (r f)").bitcast(F32), 0.0)
        nc.gpsimd.memset(X[0:4, 1, 1:65, :].rearrange("p r s -> p (r s)").bitcast(F32), 0.0)

        load_x(nc.sync, 0, LOWER)
        load_x(nc.scalar, 0, UPPER)
        nc.scalar.sqrt(out=vv[:, 0:1], in_=vv[:, 0:1])
        load_w(nc.sync, 0)
        for q, vec in enumerate((bn_var, bn_gamma, bn_mean, bn_beta)):
            queue = nc.scalar if q < 2 else nc.sync
            queue.dma_start(out=raw[4:66, q, :], in_=vec.rearrange("(c q) -> c q", q=64))
        load_w(nc.sync, 1)

        nc.vector.tensor_copy(out=identB[:], in_=identF[:])
        nc.vector.memset(MT[:], 0.0)
        nc.vector.memset(MRp[:], 0.0)
        nc.vector.memset(E[:, :, :, 0:66:65], 0.0)
        for j in range(0, RING, 4):
            nc.vector.memset(tbuf[j][:, :, :].rearrange("p m (a v) -> p m a v", v=32)[:, :, :, 0:1], 0.0)
            nc.vector.memset(tbuf[j + 3][:, :, :].rearrange("p m (a v) -> p m a v", v=32)[:, :, :, 31:32], 0.0)

        for w0 in range(0, 32, 16):
            turn_words(w0)
        feat_ftb(0)
        feat_e(0, 0, 33)
        pts = [chan_turn(0, g4, yp, "y") for g4 in range(4)]
        for g4 in range(4):
            chan_reduce(0, g4, pts[g4])
        chan_rows(0)
        feat_x1(0, nc.scalar)
        load_w(nc.sync, 2)
        nc.sync.dma_start(out=raw[66:128, :, 0:62], in_=raw[4:66, :, 2:64])
        load_w(nc.sync, 3)
        load_x(nc.sync, 1, LOWER + UPPER)
        feat_ft_words()
        for vp in range(2):
            feat_g3(0, vp)
        for k in range(TAPS // 2):
            weights(k)
            if k == 4:
                nc.scalar.activation(out=vv[:], in_=raw[:, 0, :], func=ACT.Sqrt, bias=BN_EPS)
        weights_q(0, 2)
        for vp in range(2):
            feat_g2(0, vp)
        feat_x1(1, nc.sync)
        feat_q(0)
        nc.vector.reciprocal(out=vv[:], in_=vv[:])
        nc.vector.tensor_mul(out=sfull[:], in0=raw[:, 1, :], in1=vv[:])
        nc.vector.tensor_mul(out=bfull[:], in0=raw[:, 2, :], in1=sfull[:])
        nc.vector.tensor_sub(out=bfull[:], in0=raw[:, 3, :], in1=bfull[:])
        for k in (2, 4, 6):
            weights_q(k, 2)
        weights_q(8, 4)

        pts1 = {}
        side = {}
        for g4 in range(4):
            side[1 + g4] = lambda g4=g4: chan_reduce(1, g4, pts1[g4])
        side[0] = lambda: weights_q(12, 2)
        side[5] = lambda: weights_q(14, 2)
        side[6] = lambda: feat_g3(1, 0)
        side[7] = lambda: feat_g3(1, 1)
        side[8] = lambda: feat_g2(1, 0)
        side[9] = lambda: feat_g2(1, 1)
        side[10] = lambda: feat_q(1)
        side[12] = lambda: feat_e(1, 0, 17)
        side[13] = lambda: (feat_e(1, 17, 33), feat_x1(2, nc.sync))
        side[17] = lambda: feat_ft(1, 16)
        side[18] = lambda: feat_ft(16, 32)
        side[20] = lambda: feat_g3(2, 0)
        side[21] = lambda: feat_g3(2, 1)
        side[23] = lambda: feat_g2(2, 0)
        side[24] = lambda: (feat_g2(2, 1), feat_x1(3, nc.sync))
        side[26] = lambda: feat_q(2)
        side[29] = lambda: feat_g3(3, 0)
        side[32] = lambda: feat_g3(3, 1)
        side[35] = lambda: feat_g2(3, 0)
        side[38] = lambda: feat_g2(3, 1)
        side[42] = lambda: feat_q(3)

        zs = {}
        accs = {}
        done = {}
        for h in range(STEPS + LAG + 3):
            if h < STEPS:
                zs[h] = mx_act(h)
            if 2 <= h <= 16 and h % 2 == 0:
                turn_x(h // 2 - 1)
            if h == 15:
                feat_ftb(1)
            g = h - LAG
            if 0 <= g < STEPS:
                if g % TAPS == 0:
                    accs[g // TAPS] = [pp.tile([P, 512], F32, name="acc", tag="pp") for m in range(2)]
                add_up(g, accs[g // TAPS])
                if g % TAPS == TAPS - 1:
                    done[g // TAPS] = (leave_psum(accs[g // TAPS], g == STEPS - 1), op.tile([P, 1024], F32, name="o"))
            f = h - LAG - TAPS
            if f >= 0 and f % TAPS in (0, 1):
                ats, o = done[f // TAPS]
                ah = f % TAPS
                turn_back(ats, o, ah, on_vector=(h >= STEPS and ah == 1))
                if f // TAPS == 3:
                    store(3, o, 8 * ah, 8)
                elif ah == 1:
                    store(f // TAPS, o, 0, 16)
            if 1 <= h <= 4:
                pts1[h - 1] = chan_turn(1, h - 1, pp, "pp")
            if h == 8:
                chan_rows(1)
            if h < STEPS:
                mul(h, zs[h])
            if h in side:
                side[h]()
